import numpy as np
import ml_dtypes


def mxq(x, axis, fmt="e4m3"):
    dtype, down = {"e4m3": (ml_dtypes.float8_e4m3fn, 7), "e5m2": (ml_dtypes.float8_e5m2, 14)}[fmt]
    v = np.moveaxis(np.asarray(x, np.float32).astype(ml_dtypes.bfloat16).astype(np.float64), axis, -1)
    blocks = v.reshape(v.shape[:-1] + (-1, 32))
    amax = np.abs(blocks).max(-1, keepdims=True)
    byte = np.maximum(np.where(amax > 0, np.frexp(amax)[1] - 1 + 127, 0) - down, 1)
    scale = np.exp2(byte - 127.0)
    codes = (blocks / scale).astype(np.float32).astype(dtype).astype(np.float64)
    return np.moveaxis((codes * scale).reshape(v.shape), -1, axis)


WIDE = False


def mx_kscale(k):
    if not WIDE:
        return np.ones(k)
    levels = np.array([10, -10, 5, -5, 0])
    if k % 512:
        return np.exp2(np.random.permutation(np.resize(levels, k // 32))).repeat(32)
    a = np.empty((k // 512, 16))
    for p in range(k // 512):
        a[p, :8] = np.random.permutation(np.resize(levels, 8))
        for g in range(8):
            far = levels[np.abs(levels - a[p, g]) >= 10]
            a[p, g + 8] = far[np.random.randint(len(far))]
    return np.exp2(a.ravel()).repeat(32)


BF16 = ml_dtypes.bfloat16


def bf(x):
    return np.asarray(x, np.float32).astype(BF16)


def f64(x):
    return np.asarray(x).astype(np.float64)


N, M, C, C0, C1 = 128, 8, 128, 8192, 256
EPS = 1e-3


def bn_relu(y, gamma, beta):
    mean = y.mean(axis=(0, 1))
    var = y.var(axis=(0, 1))
    return np.maximum((y - mean) * (1.0 / np.sqrt(var + EPS)) * gamma + beta, 0.0)


def setup_inputs():
    t = mx_kscale(C0)
    r0 = 0.05 * 4.0 ** np.random.random(C0)
    return {"voxel_feats": bf(np.random.standard_normal((N, M, C)) + 0.5 * np.random.standard_normal(C)),
            "W0": bf(np.random.standard_normal((C0, C)) / np.sqrt(C) * r0[:, None]),
            "gamma0": bf((1.0 + 0.1 * np.random.standard_normal(C0)) * t),
            "beta0": bf(0.2 * np.random.standard_normal(C0) * t),
            "W1": bf(np.random.standard_normal((C1, 2 * C0)) * 0.2 / np.sqrt(2 * C0) / np.concatenate([t, t])[None, :]),
            "gamma1": bf(1.0 + 0.1 * np.random.standard_normal(C1)),
            "beta1": bf(0.3 * np.random.standard_normal(C1) - 0.5)}


def reference(voxel_feats, W0, gamma0, beta0, W1, gamma1, beta1):
    y0 = f64(voxel_feats) @ f64(W0).T
    p = bn_relu(y0, f64(gamma0), f64(beta0))
    a = p.max(axis=1)
    w1q = mxq(f64(W1).T, 0, "e4m3")
    y1 = (mxq(p, 2, "e4m3") @ w1q[:C0]) + (mxq(a, 1, "e4m3") @ w1q[C0:])[:, None, :]
    return bn_relu(y1, f64(gamma1), f64(beta1)).max(axis=1)

@@ -1,0 +1,315 @@
+from contextlib import ExitStack
+
+import concourse.mybir as mybir
+from concourse.masks import make_identity
+
+BF16 = mybir.dt.bfloat16
+F32 = mybir.dt.float32
+U32 = mybir.dt.uint32
+U8 = mybir.dt.uint8
+FP8X4 = mybir.dt.float8_e4m3fn_x4
+ALU = mybir.AluOpType
+ACT = mybir.ActivationFunctionType
+AX = mybir.AxisListType
+
+P = 128
+VOXELS = 128
+POINTS = 8
+ROWS = VOXELS * POINTS
+C = 128
+C0 = 8192
+C1 = 256
+EPS = 1e-3
+PACK = 4
+K_PASS = P * PACK
+PASSES = C0 // K_PASS
+CHUNKS = C0 // P
+HALF = ROWS // 2
+GROUP = 2
+GROUPS = PASSES // GROUP
+
+FLOPS = 2 * ROWS * C * C0 + 2 * ROWS * C0 * C1 + 2 * VOXELS * C0 * C1
+
+
+def tile_vfe_k_kernel(tc, voxel_feats, W0, gamma0, beta0, W1, gamma1, beta1, out):
+    nc = tc.nc
+    with ExitStack() as ctx:
+        keep = ctx.enter_context(tc.tile_pool(name="keep", bufs=1))
+        flow = ctx.enter_context(tc.tile_pool(name="flow", bufs=3))
+
+        xT = keep.tile([P, ROWS], BF16)
+        ident_bf = keep.tile([P, P], BF16)
+        ident_f32 = keep.tile([P, P], F32)
+        gb = keep.tile([P, 132], F32)
+        w0T = keep.tile([P, CHUNKS, P], BF16)
+        scale0 = keep.tile([P, CHUNKS], F32)
+        shift0 = keep.tile([P, CHUNKS], F32)
+        w1_codes = keep.tile([P, 2, PASSES, C1], U32, align_bytes=64)
+        w1_scales = keep.tile([P, 2, PASSES, C1], U8, align_bytes=64)
+        p_codes_first = keep.tile([P, PASSES, HALF], U32, align_bytes=64)
+        p_scales_first = keep.tile([P, PASSES, HALF], U8, align_bytes=64)
+        peak_first = keep.tile([P, PASSES, PACK * VOXELS], BF16)
+        a_codes = keep.tile([P, PASSES, VOXELS], U32, align_bytes=64)
+        a_scales = keep.tile([P, PASSES, VOXELS], U8, align_bytes=64)
+        gamma0_t = gb[:, 0:CHUNKS]
+        beta0_t = gb[:, CHUNKS : 2 * CHUNKS]
+        gamma1_t = gb[:, 128:130]
+        beta1_t = gb[:, 130:132]
+
+        def layer0(g, half, psum, codes, scales, peak):
+            planes = flow.tile([P, PACK, HALF], BF16)
+            for t in range(PACK):
+                j = PACK * g + t
+                y0_ps = psum.tile([P, HALF], F32, tag="y0")
+                nc.tensor.matmul(out=y0_ps[:], lhsT=w0T[:, j, :], rhs=xT[:, half * HALF : (half + 1) * HALF], start=True, stop=True)
+                nc.scalar.activation(
+                    out=planes[:, t, :], in_=y0_ps[:], func=ACT.Relu, bias=shift0[:, j : j + 1], scale=scale0[:, j : j + 1]
+                )
+            grouped = flow.tile([P, PACK * HALF], BF16, align_bytes=64)
+            nc.vector.tensor_copy(
+                out=grouped[:].rearrange("p (c i t) -> p c t i", i=4, t=PACK),
+                in_=planes[:].rearrange("p t (c i) -> p c t i", i=4),
+            )
+            nc.vector.quantize_mx(out=codes.bitcast(FP8X4), scales=scales, in_=grouped[:])
+            best2 = flow.tile([P, 2 * PACK * VOXELS], BF16)
+            nc.vector.tensor_tensor(out=best2[:], in0=grouped[:, 0:1024], in1=grouped[:, 1024:2048], op=ALU.max)
+            nc.vector.tensor_tensor(out=peak, in0=best2[:, 0:512], in1=best2[:, 512:1024], op=ALU.max)
+
+        with ExitStack() as first:
+            once = first.enter_context(tc.tile_pool(name="once", bufs=1))
+            stage = first.enter_context(tc.tile_pool(name="stage", bufs=2))
+            loads = first.enter_context(tc.tile_pool(name="loads", bufs=4))
+            psum_y0 = first.enter_context(tc.psum_pool(name="psum_y0", bufs=2))
+            psum_two = first.enter_context(tc.psum_pool(name="psum_two", bufs=2))
+            psum_one = first.enter_context(tc.psum_pool(name="psum_one", bufs=1))
+
+            x_sb = once.tile([P, POINTS, C], BF16)
+            nc.sync.dma_start(out=x_sb[:], in_=voxel_feats)
+            gb_rows = once.tile([P, K_PASS], BF16)
+            nc.vector.memset(gb_rows[:], 0.0)
+            nc.scalar.dma_start(out=gb_rows[0:16, :], in_=gamma0.rearrange("(r w) -> r w", w=K_PASS))
+            nc.scalar.dma_start(out=gb_rows[16:32, :], in_=beta0.rearrange("(r w) -> r w", w=K_PASS))
+            nc.scalar.dma_start(out=gb_rows[32:33, 0:C1], in_=gamma1.rearrange("(r w) -> r w", w=C1))
+            nc.scalar.dma_start(out=gb_rows[33:34, 0:C1], in_=beta1.rearrange("(r w) -> r w", w=C1))
+
+            make_identity(nc, ident_bf[:])
+            make_identity(nc, ident_f32[:])
+            ones_bf = once.tile([P, P], BF16)
+            nc.vector.memset(ones_bf[:], 1.0)
+
+            xt_ps = psum_one.tile([P, POINTS, VOXELS], BF16, tag="w0t")
+            for m in range(POINTS):
+                nc.tensor.transpose(xt_ps[:, m, :], x_sb[:, m, :], ident_bf[:])
+            nc.scalar.copy(out=xT[:], in_=xt_ps[:].rearrange("p m n -> p (m n)"))
+
+            sum_ps = psum_two.tile([P, C], F32, tag="wcov")
+            for m in range(POINTS):
+                nc.tensor.matmul(out=sum_ps[:], lhsT=ones_bf[:], rhs=x_sb[:, m, :], start=(m == 0), stop=(m == POINTS - 1))
+            mu_rows = once.tile([P, C], F32)
+            nc.vector.tensor_scalar(out=mu_rows[:], in0=sum_ps[:], scalar1=1.0 / ROWS, scalar2=None, op0=ALU.mult)
+            xc = once.tile([P, POINTS, C], F32)
+            nc.vector.tensor_tensor(
+                out=xc[:], in0=x_sb[:], in1=mu_rows[:].unsqueeze(1).to_broadcast([P, POINTS, C]), op=ALU.subtract
+            )
+            cov_ps = psum_two.tile([P, C], F32, tag="wcov")
+            for m in range(POINTS):
+                nc.tensor.matmul(out=cov_ps[:], lhsT=xc[:, m, :], rhs=xc[:, m, :], start=(m == 0), stop=(m == POINTS - 1))
+            cov = once.tile([P, C], F32)
+            nc.vector.tensor_scalar(out=cov[:], in0=cov_ps[:], scalar1=1.0 / ROWS, scalar2=None, op0=ALU.mult)
+
+            col_ps = psum_one.tile([P, 2], F32, tag="mean")
+            for m in range(POINTS):
+                nc.tensor.matmul(out=col_ps[:], lhsT=x_sb[:, m, :], rhs=ones_bf[:, 0:2], start=(m == 0), stop=(m == POINTS - 1))
+            mu_pieces = once.tile([P, 4], BF16)
+            nc.vector.memset(mu_pieces[:], 0.0)
+            rest0 = once.tile([P, 1], F32)
+            rest1 = once.tile([P, 1], F32)
+            rest2 = once.tile([P, 1], F32)
+            nc.vector.tensor_scalar(out=rest0[:], in0=col_ps[:, 0:1], scalar1=1.0 / ROWS, scalar2=None, op0=ALU.mult)
+            nc.vector.tensor_copy(out=mu_pieces[:, 0:1], in_=rest0[:])
+            nc.vector.tensor_tensor(out=rest1[:], in0=rest0[:], in1=mu_pieces[:, 0:1], op=ALU.subtract)
+            nc.vector.tensor_copy(out=mu_pieces[:, 1:2], in_=rest1[:])
+            nc.vector.tensor_tensor(out=rest2[:], in0=rest1[:], in1=mu_pieces[:, 1:2], op=ALU.subtract)
+            nc.vector.tensor_copy(out=mu_pieces[:, 2:3], in_=rest2[:])
+
+            gb_words = gb_rows[:].bitcast(F32)
+            gb_ps = psum_two.tile([P, 3, P], F32, tag="w1t")
+            for u in range(2):
+                nc.tensor.transpose(gb_ps[:, u, :], gb_words[:, u : 2 * P : 2], ident_f32[:])
+            nc.tensor.transpose(gb_ps[:, 2, :], gb_words[:, 0:P], ident_f32[:])
+            gb_halves = gb_ps[:].rearrange("p u r -> p (u r)").bitcast(BF16).rearrange("p (u r e) -> p u r e", u=3, e=2)
+            for u in range(2):
+                nc.vector.tensor_copy(
+                    out=gb[:, 0 : 2 * CHUNKS].rearrange("p (r u e) -> p u r e", u=2, e=2)[:, u], in_=gb_halves[:, u, 0:32, :]
+                )
+            nc.vector.tensor_copy(out=gb[:, 128:132].rearrange("p (r e) -> p r e", e=2), in_=gb_halves[:, 2, 32:34, :])
+
+            w0_view = W0.rearrange("(g p t) c -> p g (t c)", p=P, t=PACK)
+            w1_view = W1.rearrange("(n h) k -> n h k", h=2)
+
+            def prepare(group):
+                n_chunks = PACK * GROUP
+                cols = slice(n_chunks * group, n_chunks * (group + 1))
+                w0_raw = loads.tile([P, n_chunks, C], BF16)
+                nc.sync.dma_start(
+                    out=w0_raw[:].rearrange("p (g t) c -> p g (t c)", t=PACK),
+                    in_=w0_view[:, GROUP * group : GROUP * (group + 1), :],
+                )
+                w1_raw = []
+                for part in range(2):
+                    k0 = part * C0 + group * GROUP * K_PASS
+                    raw = loads.tile([P, 2, GROUP * K_PASS], BF16, name="w1_raw%d" % part, tag="w1_raw")
+                    nc.sync.dma_start(out=raw[:], in_=w1_view[:, :, k0 : k0 + GROUP * K_PASS])
+                    w1_raw.append(raw)
+
+                var_g = stage.tile([P, n_chunks], F32)
+                mean_ps = psum_one.tile([P, n_chunks, 4], F32, tag="mean")
+                for i in range(GROUP):
+                    local = slice(PACK * i, PACK * (i + 1))
+                    chunks = slice(n_chunks * group + PACK * i, n_chunks * group + PACK * (i + 1))
+                    w0t_ps = psum_one.tile([P, PACK, P], BF16, tag="w0t")
+                    for t in range(PACK):
+                        nc.tensor.transpose(w0t_ps[:, t, :], w0_raw[:, PACK * i + t, :], ident_bf[:])
+                    nc.scalar.copy(out=w0T[:, chunks, :], in_=w0t_ps[:])
+                    w0T_f32 = stage.tile([P, PACK, P], F32)
+                    nc.gpsimd.tensor_scalar(
+                        out=w0T_f32[:], in0=w0T[:, chunks, :], scalar1=1.0, scalar2=0.0, op0=ALU.mult, op1=ALU.add
+                    )
+                    wcov_ps = psum_two.tile([P, PACK, C], F32, tag="wcov")
+                    for t in range(PACK):
+                        nc.tensor.matmul(out=wcov_ps[:, t, :], lhsT=w0T_f32[:, t, :], rhs=cov[:], start=True, stop=True)
+                        nc.tensor.matmul(
+                            out=mean_ps[:, PACK * i + t, :], lhsT=w0T[:, n_chunks * group + PACK * i + t, :], rhs=mu_pieces[:],
+                            start=True, stop=True,
+                        )
+                    prod = stage.tile([P, PACK, C], F32)
+                    nc.vector.tensor_tensor(out=prod[:], in0=wcov_ps[:], in1=w0_raw[:, local, :], op=ALU.mult)
+                    nc.vector.tensor_reduce(out=var_g[:, local], in_=prod[:], axis=AX.X, op=ALU.add)
+                mean_g = stage.tile([P, n_chunks], F32)
+                nc.vector.tensor_reduce(out=mean_g[:], in_=mean_ps[:], axis=AX.X, op=ALU.add)
+                var_eps = stage.tile([P, n_chunks], F32)
+                nc.vector.tensor_scalar(out=var_eps[:], in0=var_g[:], scalar1=EPS, scalar2=None, op0=ALU.add)
+                std_g = stage.tile([P, n_chunks], F32)
+                nc.scalar.sqrt(out=std_g[:], in_=var_eps[:])
+                rstd_g = stage.tile([P, n_chunks], F32)
+                nc.vector.reciprocal(out=rstd_g[:], in_=std_g[:])
+                nc.vector.tensor_tensor(out=scale0[:, cols], in0=gamma0_t[:, cols], in1=rstd_g[:], op=ALU.mult)
+                mscale_g = stage.tile([P, n_chunks], F32)
+                nc.vector.tensor_tensor(out=mscale_g[:], in0=mean_g[:], in1=scale0[:, cols], op=ALU.mult)
+                nc.vector.tensor_tensor(out=shift0[:, cols], in0=beta0_t[:, cols], in1=mscale_g[:], op=ALU.subtract)
+
+                passes = slice(GROUP * group, GROUP * (group + 1))
+                for part in range(2):
+                    w1_words = w1_raw[part][:].bitcast(F32)
+                    w1_grouped = stage.tile([P, GROUP, PACK * C1], BF16, align_bytes=64)
+                    for i in range(GROUP):
+                        w1t_ps = psum_two.tile([P, 2, 2, P], F32, tag="w1t")
+                        for h in range(2):
+                            for u in range(2):
+                                nc.tensor.transpose(
+                                    w1t_ps[:, h, u, :], w1_words[:, h, 256 * i + u : 256 * (i + 1) : 2], ident_f32[:]
+                                )
+                        nc.scalar.copy(
+                            out=w1_grouped[:, i, :].bitcast(F32).rearrange("p (h n u) -> p h n u", h=2, u=2),
+                            in_=w1t_ps[:].rearrange("p h u n -> p h n u"),
+                        )
+                    nc.vector.quantize_mx(
+                        out=w1_codes[:, part, passes, :].rearrange("p g n -> p (g n)").bitcast(FP8X4),
+                        scales=w1_scales[:, part, passes, :].rearrange("p g n -> p (g n)"),
+                        in_=w1_grouped[:].rearrange("p i w -> p (i w)"),
+                    )
+
+            for step in range(GROUPS + 1):
+                if step < GROUPS:
+                    prepare(step)
+                if step >= 1:
+                    for g in range(GROUP * (step - 1), GROUP * step):
+                        layer0(g, 0, psum_y0, p_codes_first[:, g, :], p_scales_first[:, g, :], peak_first[:, g, :])
+
+        last = ctx.enter_context(tc.tile_pool(name="last", bufs=1))
+        late = ctx.enter_context(tc.tile_pool(name="late", bufs=3))
+        psum_acc = ctx.enter_context(tc.psum_pool(name="psum_acc", bufs=1))
+        psum_rest = ctx.enter_context(tc.psum_pool(name="psum_rest", bufs=4))
+        acc = [[psum_acc.tile([P, HALF], F32, name="acc%d%d" % (h, half)) for half in range(2)] for h in range(2)]
+
+        def layer1(g, half, codes, scales):
+            for h in range(2):
+                nc.tensor.matmul_mx(
+                    out=acc[h][half][:],
+                    lhsT=w1_codes[:, 0, g, h * P : (h + 1) * P].bitcast(FP8X4),
+                    lhsT_scale=w1_scales[:, 0, g, h * P : (h + 1) * P],
+                    rhs=codes.bitcast(FP8X4),
+                    rhs_scale=scales,
+                    start=(g == 0),
+                    stop=(g == PASSES - 1),
+                )
+
+        for g in range(PASSES):
+            p_codes = late.tile([P, HALF], U32, align_bytes=64)
+            p_scales = late.tile([P, HALF], U8, align_bytes=64)
+            peak = late.tile([P, PACK * VOXELS], BF16)
+            layer0(g, 1, psum_rest, p_codes[:], p_scales[:], peak[:])
+            a_grouped = late.tile([P, PACK * VOXELS], BF16, align_bytes=64)
+            nc.vector.tensor_tensor(out=a_grouped[:], in0=peak[:], in1=peak_first[:, g, :], op=ALU.max)
+            nc.vector.quantize_mx(out=a_codes[:, g, :].bitcast(FP8X4), scales=a_scales[:, g, :], in_=a_grouped[:])
+            layer1(g, 0, p_codes_first[:, g, :], p_scales_first[:, g, :])
+            layer1(g, 1, p_codes[:], p_scales[:])
+
+        ya = last.tile([P, 2, VOXELS], F32)
+        for h in range(2):
+            ya_ps = psum_rest.tile([P, VOXELS], F32, tag="y0")
+            for g in range(PASSES):
+                nc.tensor.matmul_mx(
+                    out=ya_ps[:],
+                    lhsT=w1_codes[:, 1, g, h * P : (h + 1) * P].bitcast(FP8X4),
+                    lhsT_scale=w1_scales[:, 1, g, h * P : (h + 1) * P],
+                    rhs=a_codes[:, g, :].bitcast(FP8X4),
+                    rhs_scale=a_scales[:, g, :],
+                    start=(g == 0),
+                    stop=(g == PASSES - 1),
+                )
+            nc.scalar.copy(out=ya[:, h, :], in_=ya_ps[:])
+
+        y1 = last.tile([P, 2, 2, HALF], F32)
+        stats1 = last.tile([P, 2, 2, 6], F32)
+        mv1 = last.tile([P, 2, 2], F32)
+        for h in range(2):
+            for half in range(2):
+                nc.vector.tensor_tensor(
+                    out=y1[:, h, half, :].rearrange("p (m n) -> p m n", n=VOXELS),
+                    in0=acc[h][half][:].rearrange("p (m n) -> p m n", n=VOXELS),
+                    in1=ya[:, h, :].unsqueeze(1).to_broadcast([P, POINTS // 2, VOXELS]),
+                    op=ALU.add,
+                )
+                nc.vector.bn_stats(out=stats1[:, h, half, :], in_=y1[:, h, half, :])
+            nc.vector.bn_aggr(out=mv1[:, h, :], in_=stats1[:, h, :, :].rearrange("p q s -> p (q s)"))
+        var_eps1 = last.tile([P, 2], F32)
+        std1 = last.tile([P, 2], F32)
+        rstd1 = last.tile([P, 2], F32)
+        scale1 = last.tile([P, 2], F32)
+        mscale1 = last.tile([P, 2], F32)
+        shift1 = last.tile([P, 2], F32)
+        nc.vector.tensor_scalar(out=var_eps1[:], in0=mv1[:, :, 1], scalar1=EPS, scalar2=None, op0=ALU.add)
+        nc.scalar.sqrt(out=std1[:], in_=var_eps1[:])
+        nc.vector.reciprocal(out=rstd1[:], in_=std1[:])
+        nc.vector.tensor_tensor(out=scale1[:], in0=gamma1_t, in1=rstd1[:], op=ALU.mult)
+        nc.vector.tensor_tensor(out=mscale1[:], in0=mv1[:, :, 0], in1=scale1[:], op=ALU.mult)
+        nc.vector.tensor_tensor(out=shift1[:], in0=beta1_t, in1=mscale1[:], op=ALU.subtract)
+
+        z = last.tile([P, 2, ROWS], F32)
+        z4 = last.tile([P, 2, 512], F32)
+        z2 = last.tile([P, 2, 256], F32)
+        z1 = last.tile([P, 2, VOXELS], F32)
+        out_ps = psum_rest.tile([P, 2, P], F32, tag="y0")
+        for h in range(2):
+            nc.scalar.activation(
+                out=z[:, h, :], in_=y1[:, h, :, :].rearrange("p q r -> p (q r)"), func=ACT.Relu,
+                bias=shift1[:, h : h + 1], scale=scale1[:, h : h + 1],
+            )
+            nc.vector.tensor_tensor(out=z4[:, h, :], in0=z[:, h, 0:512], in1=z[:, h, 512:1024], op=ALU.max)
+            nc.vector.tensor_tensor(out=z2[:, h, :], in0=z4[:, h, 0:256], in1=z4[:, h, 256:512], op=ALU.max)
+            nc.vector.tensor_tensor(out=z1[:, h, :], in0=z2[:, h, 0:128], in1=z2[:, h, 128:256], op=ALU.max)
+            nc.tensor.transpose(out_ps[:, h, :], z1[:, h, :], ident_f32[:])
+        out_sb = last.tile([P, P, 2], F32)
+        nc.vector.tensor_copy(out=out_sb[:], in_=out_ps[:].rearrange("p h c -> p c h"))
+        nc.sync.dma_start(out=out, in_=out_sb[:].rearrange("p c h -> p (c h)"))

@@ -26,7 +26,7 @@ PASSES = C0 // K_PASS
 CHUNKS = C0 // P
 HALF = ROWS // 2
 GROUP = 2
-GROUPS = PASSES // GROUP
+W1_TILES = 2 * PASSES
 
 FLOPS = 2 * ROWS * C * C0 + 2 * ROWS * C0 * C1 + 2 * VOXELS * C0 * C1
 
@@ -36,11 +36,18 @@ def tile_vfe_k_kernel(tc, voxel_feats, W0, gamma0, beta0, W1, gamma1, beta1, out
     with ExitStack() as ctx:
         keep = ctx.enter_context(tc.tile_pool(name="keep", bufs=1))
         flow = ctx.enter_context(tc.tile_pool(name="flow", bufs=3))
+        loads = ctx.enter_context(tc.tile_pool(name="loads", bufs=4))
+        psum_y0 = ctx.enter_context(tc.psum_pool(name="psum_y0", bufs=3))
+        psum_w1 = ctx.enter_context(tc.psum_pool(name="psum_w1", bufs=1))
+        ctx.enter_context(tc.manual_schedule())
 
         xT = keep.tile([P, ROWS], BF16)
         ident_bf = keep.tile([P, P], BF16)
         ident_f32 = keep.tile([P, P], F32)
         gb = keep.tile([P, 132], F32)
+        sgn1 = keep.tile([P, 2], F32)
+        gamma1_abs = keep.tile([P, 2], F32)
+        eps = keep.tile([P, 1], F32)
         w0T = keep.tile([P, CHUNKS, P], BF16)
         scale0 = keep.tile([P, CHUNKS], F32)
         shift0 = keep.tile([P, CHUNKS], F32)
@@ -56,35 +63,109 @@ def tile_vfe_k_kernel(tc, voxel_feats, W0, gamma0, beta0, W1, gamma1, beta1, out
         gamma1_t = gb[:, 128:130]
         beta1_t = gb[:, 130:132]
 
-        def layer0(g, half, psum, codes, scales, peak):
-            planes = flow.tile([P, PACK, HALF], BF16)
-            for t in range(PACK):
-                j = PACK * g + t
-                y0_ps = psum.tile([P, HALF], F32, tag="y0")
-                nc.tensor.matmul(out=y0_ps[:], lhsT=w0T[:, j, :], rhs=xT[:, half * HALF : (half + 1) * HALF], start=True, stop=True)
-                nc.scalar.activation(
-                    out=planes[:, t, :], in_=y0_ps[:], func=ACT.Relu, bias=shift0[:, j : j + 1], scale=scale0[:, j : j + 1]
-                )
+        w1_view = W1.rearrange("(n h) k -> n h k", h=2)
+        w1_raw = {}
+        w1_grouped = {}
+
+        def load_w1(q):
+            raw = loads.tile([P, 2, GROUP * K_PASS], BF16)
+            nc.sync.dma_start(out=raw[:], in_=w1_view[:, :, q * GROUP * K_PASS : (q + 1) * GROUP * K_PASS])
+            w1_raw[q] = raw
+
+        w1_ps = {}
+
+        def turn_w1(i):
+            q, r = divmod(i, GROUP)
+            words = w1_raw[q][:].bitcast(F32)
+            w1t_ps = psum_w1.tile([P, 2, 2, P], F32, tag="w1t")
+            for h in range(2):
+                for u in range(2):
+                    nc.tensor.transpose(w1t_ps[:, h, u, :], words[:, h, 256 * r + u : 256 * (r + 1) : 2], ident_f32[:])
+            w1_ps[i] = w1t_ps
+
+        def copy_w1(i):
+            q, r = divmod(i, GROUP)
+            if r == 0:
+                grouped = flow.tile([P, GROUP, PACK * C1], BF16, name="w1_g", align_bytes=64)
+                w1_grouped[q] = grouped
+            nc.scalar.copy(
+                out=w1_grouped[q][:, r, :].bitcast(F32).rearrange("p (h n u) -> p h n u", h=2, u=2),
+                in_=w1_ps[i][:].rearrange("p h u n -> p h n u"),
+            )
+
+        def quantise_w1(q):
+            part, g = divmod(GROUP * q, PASSES)
+            nc.vector.quantize_mx(
+                out=w1_codes[:, part, g : g + GROUP, :].rearrange("p g n -> p (g n)").bitcast(FP8X4),
+                scales=w1_scales[:, part, g : g + GROUP, :].rearrange("p g n -> p (g n)"),
+                in_=w1_grouped[q][:].rearrange("p i w -> p (i w)"),
+            )
+
+        y0_tiles = {}
+        planes_of = {}
+        grouped_of = {}
+        best_of = {}
+
+        def multiply0(s, t):
+            half, g = divmod(s, PASSES)
+            y0_ps = psum_y0.tile([P, HALF], F32, tag="y0")
+            nc.tensor.matmul(
+                out=y0_ps[:], lhsT=w0T[:, PACK * g + t, :], rhs=xT[:, half * HALF : (half + 1) * HALF], start=True, stop=True
+            )
+            y0_tiles[s, t] = y0_ps
+
+        def normalise0(s, t):
+            j = PACK * (s % PASSES) + t
+            if t == 0:
+                planes = flow.tile([P, PACK, HALF], BF16)
+                planes_of[s] = planes
+            nc.scalar.activation(
+                out=planes_of[s][:, t, :], in_=y0_tiles[s, t][:], func=ACT.Relu, bias=shift0[:, j : j + 1], scale=scale0[:, j : j + 1]
+            )
+
+        def interleave0(s):
             grouped = flow.tile([P, PACK * HALF], BF16, align_bytes=64)
+            grouped_of[s] = grouped
             nc.vector.tensor_copy(
                 out=grouped[:].rearrange("p (c i t) -> p c t i", i=4, t=PACK),
-                in_=planes[:].rearrange("p t (c i) -> p c t i", i=4),
+                in_=planes_of[s][:].rearrange("p t (c i) -> p c t i", i=4),
             )
-            nc.vector.quantize_mx(out=codes.bitcast(FP8X4), scales=scales, in_=grouped[:])
+
+        def best_two(s):
             best2 = flow.tile([P, 2 * PACK * VOXELS], BF16)
-            nc.vector.tensor_tensor(out=best2[:], in0=grouped[:, 0:1024], in1=grouped[:, 1024:2048], op=ALU.max)
-            nc.vector.tensor_tensor(out=peak, in0=best2[:, 0:512], in1=best2[:, 512:1024], op=ALU.max)
+            best_of[s] = best2
+            nc.vector.tensor_tensor(out=best2[:], in0=grouped_of[s][:, 0:1024], in1=grouped_of[s][:, 1024:2048], op=ALU.max)
 
         with ExitStack() as first:
             once = first.enter_context(tc.tile_pool(name="once", bufs=1))
             stage = first.enter_context(tc.tile_pool(name="stage", bufs=2))
-            loads = first.enter_context(tc.tile_pool(name="loads", bufs=4))
-            psum_y0 = first.enter_context(tc.psum_pool(name="psum_y0", bufs=2))
             psum_two = first.enter_context(tc.psum_pool(name="psum_two", bufs=2))
             psum_one = first.enter_context(tc.psum_pool(name="psum_one", bufs=1))
 
             x_sb = once.tile([P, POINTS, C], BF16)
             nc.sync.dma_start(out=x_sb[:], in_=voxel_feats)
+            w0_view = W0.rearrange("(g p t) c -> p g (t c)", p=P, t=PACK)
+            w0_raw = []
+
+            def load_w0(q):
+                raw = once.tile([P, GROUP, PACK, C], BF16, name="w0_raw%d" % q)
+                w0_raw.append(raw)
+                nc.sync.dma_start(
+                    out=raw[:].rearrange("p g t c -> p g (t c)"), in_=w0_view[:, GROUP * q : GROUP * (q + 1), :]
+                )
+
+            load_w0(0)
+            load_w1(0)
+            load_w0(1)
+            load_w1(1)
+            load_w0(2)
+            load_w1(2)
+            for q in range(3, 6):
+                load_w0(q)
+            load_w1(3)
+            load_w0(6)
+            load_w0(7)
+
             gb_rows = once.tile([P, K_PASS], BF16)
             nc.vector.memset(gb_rows[:], 0.0)
             nc.scalar.dma_start(out=gb_rows[0:16, :], in_=gamma0.rearrange("(r w) -> r w", w=K_PASS))
@@ -92,36 +173,115 @@ def tile_vfe_k_kernel(tc, voxel_feats, W0, gamma0, beta0, W1, gamma1, beta1, out
             nc.scalar.dma_start(out=gb_rows[32:33, 0:C1], in_=gamma1.rearrange("(r w) -> r w", w=C1))
             nc.scalar.dma_start(out=gb_rows[33:34, 0:C1], in_=beta1.rearrange("(r w) -> r w", w=C1))
 
-            make_identity(nc, ident_bf[:])
-            make_identity(nc, ident_f32[:])
             ones_bf = once.tile([P, P], BF16)
             nc.vector.memset(ones_bf[:], 1.0)
+            ones_f32 = once.tile([P, 1], F32)
+            nc.vector.memset(ones_f32[:], 1.0)
+            mu_pieces = once.tile([P, 4], BF16)
+            nc.vector.memset(mu_pieces[:], 0.0)
+            nc.vector.tensor_scalar(out=eps[:], in0=ones_f32[:], scalar1=EPS, scalar2=None, op0=ALU.mult)
+            warm = once.tile([P, 1], F32)
+            nc.scalar.activation(out=warm[:], in_=ones_f32[:], func=ACT.Sqrt)
+            make_identity(nc, ident_bf[:])
+            make_identity(nc, ident_f32[:])
 
-            xt_ps = psum_one.tile([P, POINTS, VOXELS], BF16, tag="w0t")
-            for m in range(POINTS):
-                nc.tensor.transpose(xt_ps[:, m, :], x_sb[:, m, :], ident_bf[:])
-            nc.scalar.copy(out=xT[:], in_=xt_ps[:].rearrange("p m n -> p (m n)"))
+            mean_ps = psum_one.tile([P, CHUNKS, 4], F32, name="mean")
+            stats = {}
+            w0_ps = {}
+            w0_f32 = {}
+
+            def turn_w0(g):
+                w0t_ps = psum_one.tile([P, PACK, P], BF16, tag="w0t")
+                for t in range(PACK):
+                    nc.tensor.transpose(w0t_ps[:, t, :], w0_raw[g // GROUP][:, g % GROUP, t, :], ident_bf[:])
+                w0_ps[g] = w0t_ps
+
+            def copy_w0(g):
+                nc.scalar.copy(out=w0T[:, PACK * g : PACK * (g + 1), :], in_=w0_ps[g][:])
+                wide = stage.tile([P, PACK, P], F32)
+                nc.scalar.copy(out=wide[:], in_=w0_ps[g][:])
+                w0_f32[g] = wide
+
+            groups = [[0], [1]] + [[g, g + 1] for g in range(2, PASSES, 2)]
+            group_of = {g: k for k, members in enumerate(groups) for g in members}
+
+            def moments(g):
+                k = group_of[g]
+                i = groups[k].index(g)
+                if i == 0:
+                    var_g = stage.tile([P, PACK * GROUP], F32)
+                    stats[k] = [var_g]
+                wcov_ps = psum_two.tile([P, PACK, C], F32, tag="wcov")
+                for t in range(PACK):
+                    nc.tensor.matmul(out=wcov_ps[:, t, :], lhsT=w0_f32[g][:, t, :], rhs=cov[:], start=True, stop=True)
+                for t in range(PACK):
+                    nc.tensor.matmul(
+                        out=mean_ps[:, PACK * g + t, :], lhsT=w0T[:, PACK * g + t, :], rhs=mu_pieces[:], start=True, stop=True
+                    )
+                w0_ps[g] = wcov_ps
+
+            def variance(g, t):
+                k = group_of[g]
+                i = groups[k].index(g)
+                prod = stage.tile([P, C], F32)
+                nc.vector.scalar_tensor_tensor(
+                    out=prod[:], in0=w0_ps[g][:, t, :], scalar=1.0, in1=w0_raw[g // GROUP][:, g % GROUP, t, :],
+                    op0=ALU.mult, op1=ALU.mult, accum_out=stats[k][0][:, PACK * i + t : PACK * i + t + 1],
+                )
+
+            def deviation(k):
+                n = PACK * len(groups[k])
+                std_g = stage.tile([P, PACK * GROUP], F32)
+                nc.scalar.activation(out=std_g[:, 0:n], in_=stats[k][0][:, 0:n], func=ACT.Sqrt, bias=eps[:, 0:1])
+                stats[k].append(std_g)
+
+            def constants(k):
+                n = PACK * len(groups[k])
+                cols = slice(PACK * groups[k][0], PACK * groups[k][0] + n)
+                std_g = stats[k][1]
+                mean_g = stage.tile([P, PACK * GROUP], F32)
+                rstd_g = stage.tile([P, PACK * GROUP], F32)
+                mscale_g = stage.tile([P, PACK * GROUP], F32)
+                return [
+                    lambda: nc.vector.tensor_reduce(out=mean_g[:, 0:n], in_=mean_ps[:, cols, :], axis=AX.X, op=ALU.add),
+                    lambda: nc.vector.reciprocal(out=rstd_g[:, 0:n], in_=std_g[:, 0:n]),
+                    lambda: nc.vector.tensor_tensor(out=scale0[:, cols], in0=gamma0_t[:, cols], in1=rstd_g[:, 0:n], op=ALU.mult),
+                    lambda: nc.vector.tensor_tensor(out=mscale_g[:, 0:n], in0=mean_g[:, 0:n], in1=scale0[:, cols], op=ALU.mult),
+                    lambda: nc.vector.tensor_tensor(out=shift0[:, cols], in0=beta0_t[:, cols], in1=mscale_g[:, 0:n], op=ALU.subtract),
+                ]
 
             sum_ps = psum_two.tile([P, C], F32, tag="wcov")
             for m in range(POINTS):
                 nc.tensor.matmul(out=sum_ps[:], lhsT=ones_bf[:], rhs=x_sb[:, m, :], start=(m == 0), stop=(m == POINTS - 1))
             mu_rows = once.tile([P, C], F32)
             nc.vector.tensor_scalar(out=mu_rows[:], in0=sum_ps[:], scalar1=1.0 / ROWS, scalar2=None, op0=ALU.mult)
-            xc = once.tile([P, POINTS, C], F32)
-            nc.vector.tensor_tensor(
-                out=xc[:], in0=x_sb[:], in1=mu_rows[:].unsqueeze(1).to_broadcast([P, POINTS, C]), op=ALU.subtract
-            )
-            cov_ps = psum_two.tile([P, C], F32, tag="wcov")
-            for m in range(POINTS):
-                nc.tensor.matmul(out=cov_ps[:], lhsT=xc[:, m, :], rhs=xc[:, m, :], start=(m == 0), stop=(m == POINTS - 1))
-            cov = once.tile([P, C], F32)
-            nc.vector.tensor_scalar(out=cov[:], in0=cov_ps[:], scalar1=1.0 / ROWS, scalar2=None, op0=ALU.mult)
-
-            col_ps = psum_one.tile([P, 2], F32, tag="mean")
+            col_ps = psum_y0.tile([P, 2], F32, tag="y0")
             for m in range(POINTS):
                 nc.tensor.matmul(out=col_ps[:], lhsT=x_sb[:, m, :], rhs=ones_bf[:, 0:2], start=(m == 0), stop=(m == POINTS - 1))
-            mu_pieces = once.tile([P, 4], BF16)
-            nc.vector.memset(mu_pieces[:], 0.0)
+            xt_ps = psum_y0.tile([P, POINTS, VOXELS], BF16, tag="y0")
+            for m in range(POINTS):
+                nc.tensor.transpose(xt_ps[:, m, :], x_sb[:, m, :], ident_bf[:])
+            nc.scalar.copy(out=xT[:], in_=xt_ps[:].rearrange("p m n -> p (m n)"))
+            turn_w0(0)
+            copy_w0(0)
+            cov_ps = psum_two.tile([P, C], F32, tag="wcov")
+            for q in range(2):
+                xc = once.tile([P, POINTS // 2, C], F32, name="xc%d" % q)
+                nc.vector.tensor_tensor(
+                    out=xc[:], in0=x_sb[:, 4 * q : 4 * (q + 1), :],
+                    in1=mu_rows[:].unsqueeze(1).to_broadcast([P, POINTS // 2, C]), op=ALU.subtract,
+                )
+                for m in range(POINTS // 2):
+                    nc.tensor.matmul(
+                        out=cov_ps[:], lhsT=xc[:, m, :], rhs=xc[:, m, :], start=(q == 0 and m == 0), stop=(q == 1 and m == 3)
+                    )
+            turn_w1(0)
+            copy_w1(0)
+            gb_words = gb_rows[:].bitcast(F32)
+            gb_ps = psum_y0.tile([P, 3, P], F32, tag="y0")
+            for u in range(2):
+                nc.tensor.transpose(gb_ps[:, u, :], gb_words[:, u : 2 * P : 2], ident_f32[:])
+            nc.tensor.transpose(gb_ps[:, 2, :], gb_words[:, 0:P], ident_f32[:])
             rest0 = once.tile([P, 1], F32)
             rest1 = once.tile([P, 1], F32)
             rest2 = once.tile([P, 1], F32)
@@ -131,105 +291,90 @@ def tile_vfe_k_kernel(tc, voxel_feats, W0, gamma0, beta0, W1, gamma1, beta1, out
             nc.vector.tensor_copy(out=mu_pieces[:, 1:2], in_=rest1[:])
             nc.vector.tensor_tensor(out=rest2[:], in0=rest1[:], in1=mu_pieces[:, 1:2], op=ALU.subtract)
             nc.vector.tensor_copy(out=mu_pieces[:, 2:3], in_=rest2[:])
+            cov = once.tile([P, C], F32)
+            nc.vector.tensor_scalar(out=cov[:], in0=cov_ps[:], scalar1=1.0 / ROWS, scalar2=None, op0=ALU.mult)
 
-            gb_words = gb_rows[:].bitcast(F32)
-            gb_ps = psum_two.tile([P, 3, P], F32, tag="w1t")
-            for u in range(2):
-                nc.tensor.transpose(gb_ps[:, u, :], gb_words[:, u : 2 * P : 2], ident_f32[:])
-            nc.tensor.transpose(gb_ps[:, 2, :], gb_words[:, 0:P], ident_f32[:])
+            moments(0)
+            turn_w0(1)
+            copy_w0(1)
+            turn_w1(1)
+            copy_w1(1)
+            moments(1)
             gb_halves = gb_ps[:].rearrange("p u r -> p (u r)").bitcast(BF16).rearrange("p (u r e) -> p u r e", u=3, e=2)
             for u in range(2):
                 nc.vector.tensor_copy(
                     out=gb[:, 0 : 2 * CHUNKS].rearrange("p (r u e) -> p u r e", u=2, e=2)[:, u], in_=gb_halves[:, u, 0:32, :]
                 )
+            for t in range(PACK):
+                variance(0, t)
+            deviation(0)
             nc.vector.tensor_copy(out=gb[:, 128:132].rearrange("p (r e) -> p r e", e=2), in_=gb_halves[:, 2, 32:34, :])
+            for work in constants(0):
+                work()
+            quantise_w1(0)
+            nc.vector.tensor_scalar(out=sgn1[:], in0=gamma1_t, scalar1=0.0, scalar2=2.0, op0=ALU.is_ge, op1=ALU.mult)
+            nc.vector.tensor_scalar(out=sgn1[:], in0=sgn1[:], scalar1=1.0, scalar2=None, op0=ALU.subtract)
+            nc.vector.tensor_tensor(out=gamma1_abs[:], in0=gamma1_t, in1=sgn1[:], op=ALU.mult)
+            for g in range(2, 4):
+                turn_w0(g)
+                copy_w0(g)
 
-            w0_view = W0.rearrange("(g p t) c -> p g (t c)", p=P, t=PACK)
-            w1_view = W1.rearrange("(n h) k -> n h k", h=2)
-
-            def prepare(group):
-                n_chunks = PACK * GROUP
-                cols = slice(n_chunks * group, n_chunks * (group + 1))
-                w0_raw = loads.tile([P, n_chunks, C], BF16)
-                nc.sync.dma_start(
-                    out=w0_raw[:].rearrange("p (g t) c -> p g (t c)", t=PACK),
-                    in_=w0_view[:, GROUP * group : GROUP * (group + 1), :],
-                )
-                w1_raw = []
-                for part in range(2):
-                    k0 = part * C0 + group * GROUP * K_PASS
-                    raw = loads.tile([P, 2, GROUP * K_PASS], BF16, name="w1_raw%d" % part, tag="w1_raw")
-                    nc.sync.dma_start(out=raw[:], in_=w1_view[:, :, k0 : k0 + GROUP * K_PASS])
-                    w1_raw.append(raw)
-
-                var_g = stage.tile([P, n_chunks], F32)
-                mean_ps = psum_one.tile([P, n_chunks, 4], F32, tag="mean")
-                for i in range(GROUP):
-                    local = slice(PACK * i, PACK * (i + 1))
-                    chunks = slice(n_chunks * group + PACK * i, n_chunks * group + PACK * (i + 1))
-                    w0t_ps = psum_one.tile([P, PACK, P], BF16, tag="w0t")
+            w1_next = 2
+            for s in range(PASSES):
+                ahead = [2, 3] if s == 0 else [s + 3] if s + 3 < PASSES else []
+                ready = 1 if s == 0 else s // 2 + 2 if s % 2 == 1 and s + 1 < PASSES else None
+                if s == 0:
                     for t in range(PACK):
-                        nc.tensor.transpose(w0t_ps[:, t, :], w0_raw[:, PACK * i + t, :], ident_bf[:])
-                    nc.scalar.copy(out=w0T[:, chunks, :], in_=w0t_ps[:])
-                    w0T_f32 = stage.tile([P, PACK, P], F32)
-                    nc.gpsimd.tensor_scalar(
-                        out=w0T_f32[:], in0=w0T[:, chunks, :], scalar1=1.0, scalar2=0.0, op0=ALU.mult, op1=ALU.add
+                        variance(1, t)
+                for t in range(3):
+                    multiply0(s, t)
+                turn_w1(w1_next)
+                multiply0(s, 3)
+                for t in range(3):
+                    normalise0(s, t)
+                    if t == 0 and ready is not None:
+                        deviation(ready)
+                copy_w1(w1_next)
+                normalise0(s, 3)
+                small = constants(ready) if ready is not None else []
+                if s >= 1:
+                    interleave0(s - 1)
+                for work in small[0:1]:
+                    work()
+                if s >= 2:
+                    nc.vector.tensor_tensor(
+                        out=peak_first[:, s - 2, :], in0=best_of[s - 2][:, 0:512], in1=best_of[s - 2][:, 512:1024], op=ALU.max
                     )
-                    wcov_ps = psum_two.tile([P, PACK, C], F32, tag="wcov")
-                    for t in range(PACK):
-                        nc.tensor.matmul(out=wcov_ps[:, t, :], lhsT=w0T_f32[:, t, :], rhs=cov[:], start=True, stop=True)
-                        nc.tensor.matmul(
-                            out=mean_ps[:, PACK * i + t, :], lhsT=w0T[:, n_chunks * group + PACK * i + t, :], rhs=mu_pieces[:],
-                            start=True, stop=True,
-                        )
-                    prod = stage.tile([P, PACK, C], F32)
-                    nc.vector.tensor_tensor(out=prod[:], in0=wcov_ps[:], in1=w0_raw[:, local, :], op=ALU.mult)
-                    nc.vector.tensor_reduce(out=var_g[:, local], in_=prod[:], axis=AX.X, op=ALU.add)
-                mean_g = stage.tile([P, n_chunks], F32)
-                nc.vector.tensor_reduce(out=mean_g[:], in_=mean_ps[:], axis=AX.X, op=ALU.add)
-                var_eps = stage.tile([P, n_chunks], F32)
-                nc.vector.tensor_scalar(out=var_eps[:], in0=var_g[:], scalar1=EPS, scalar2=None, op0=ALU.add)
-                std_g = stage.tile([P, n_chunks], F32)
-                nc.scalar.sqrt(out=std_g[:], in_=var_eps[:])
-                rstd_g = stage.tile([P, n_chunks], F32)
-                nc.vector.reciprocal(out=rstd_g[:], in_=std_g[:])
-                nc.vector.tensor_tensor(out=scale0[:, cols], in0=gamma0_t[:, cols], in1=rstd_g[:], op=ALU.mult)
-                mscale_g = stage.tile([P, n_chunks], F32)
-                nc.vector.tensor_tensor(out=mscale_g[:], in0=mean_g[:], in1=scale0[:, cols], op=ALU.mult)
-                nc.vector.tensor_tensor(out=shift0[:, cols], in0=beta0_t[:, cols], in1=mscale_g[:], op=ALU.subtract)
-
-                passes = slice(GROUP * group, GROUP * (group + 1))
-                for part in range(2):
-                    w1_words = w1_raw[part][:].bitcast(F32)
-                    w1_grouped = stage.tile([P, GROUP, PACK * C1], BF16, align_bytes=64)
-                    for i in range(GROUP):
-                        w1t_ps = psum_two.tile([P, 2, 2, P], F32, tag="w1t")
-                        for h in range(2):
-                            for u in range(2):
-                                nc.tensor.transpose(
-                                    w1t_ps[:, h, u, :], w1_words[:, h, 256 * i + u : 256 * (i + 1) : 2], ident_f32[:]
-                                )
-                        nc.scalar.copy(
-                            out=w1_grouped[:, i, :].bitcast(F32).rearrange("p (h n u) -> p h n u", h=2, u=2),
-                            in_=w1t_ps[:].rearrange("p h u n -> p h n u"),
-                        )
+                for work in small[1:2]:
+                    work()
+                if s >= 1:
                     nc.vector.quantize_mx(
-                        out=w1_codes[:, part, passes, :].rearrange("p g n -> p (g n)").bitcast(FP8X4),
-                        scales=w1_scales[:, part, passes, :].rearrange("p g n -> p (g n)"),
-                        in_=w1_grouped[:].rearrange("p i w -> p (i w)"),
+                        out=p_codes_first[:, s - 1, :].bitcast(FP8X4), scales=p_scales_first[:, s - 1, :], in_=grouped_of[s - 1][:]
                     )
-
-            for step in range(GROUPS + 1):
-                if step < GROUPS:
-                    prepare(step)
-                if step >= 1:
-                    for g in range(GROUP * (step - 1), GROUP * step):
-                        layer0(g, 0, psum_y0, p_codes_first[:, g, :], p_scales_first[:, g, :], peak_first[:, g, :])
+                for work in small[2:3]:
+                    work()
+                if s >= 1:
+                    best_two(s - 1)
+                for work in small[3:4]:
+                    work()
+                if w1_next % GROUP == 0 and s >= 1:
+                    quantise_w1(w1_next // GROUP - 1)
+                for work in small[4:5]:
+                    work()
+                for g in ahead:
+                    moments(g)
+                    for t in range(PACK):
+                        variance(g, t)
+                if s + 4 < PASSES:
+                    turn_w0(s + 4)
+                    copy_w0(s + 4)
+                w1_next += 1
+                if w1_next % GROUP == 0:
+                    load_w1(w1_next // GROUP + 2)
 
         last = ctx.enter_context(tc.tile_pool(name="last", bufs=1))
         late = ctx.enter_context(tc.tile_pool(name="late", bufs=3))
         psum_acc = ctx.enter_context(tc.psum_pool(name="psum_acc", bufs=1))
-        psum_rest = ctx.enter_context(tc.psum_pool(name="psum_rest", bufs=4))
         acc = [[psum_acc.tile([P, HALF], F32, name="acc%d%d" % (h, half)) for half in range(2)] for h in range(2)]
 
         def layer1(g, half, codes, scales):
@@ -244,21 +389,8 @@ def tile_vfe_k_kernel(tc, voxel_feats, W0, gamma0, beta0, W1, gamma1, beta1, out
                     stop=(g == PASSES - 1),
                 )
 
-        for g in range(PASSES):
-            p_codes = late.tile([P, HALF], U32, align_bytes=64)
-            p_scales = late.tile([P, HALF], U8, align_bytes=64)
-            peak = late.tile([P, PACK * VOXELS], BF16)
-            layer0(g, 1, psum_rest, p_codes[:], p_scales[:], peak[:])
-            a_grouped = late.tile([P, PACK * VOXELS], BF16, align_bytes=64)
-            nc.vector.tensor_tensor(out=a_grouped[:], in0=peak[:], in1=peak_first[:, g, :], op=ALU.max)
-            nc.vector.quantize_mx(out=a_codes[:, g, :].bitcast(FP8X4), scales=a_scales[:, g, :], in_=a_grouped[:])
-            layer1(g, 0, p_codes_first[:, g, :], p_scales_first[:, g, :])
-            layer1(g, 1, p_codes[:], p_scales[:])
-
-        ya = last.tile([P, 2, VOXELS], F32)
-        for h in range(2):
-            ya_ps = psum_rest.tile([P, VOXELS], F32, tag="y0")
-            for g in range(PASSES):
+        def layer1_peak(h, ya_ps, passes):
+            for g in passes:
                 nc.tensor.matmul_mx(
                     out=ya_ps[:],
                     lhsT=w1_codes[:, 1, g, h * P : (h + 1) * P].bitcast(FP8X4),
@@ -268,47 +400,172 @@ def tile_vfe_k_kernel(tc, voxel_feats, W0, gamma0, beta0, W1, gamma1, beta1, out
                     start=(g == 0),
                     stop=(g == PASSES - 1),
                 )
-            nc.scalar.copy(out=ya[:, h, :], in_=ya_ps[:])
 
+        p_codes_of = {}
+        p_scales_of = {}
+        peak_of = {}
+        a_grouped = {}
+
+        def quantise_p(g):
+            p_codes = late.tile([P, HALF], U32, align_bytes=64)
+            p_scales = late.tile([P, HALF], U8, align_bytes=64)
+            p_codes_of[g] = p_codes
+            p_scales_of[g] = p_scales
+            nc.vector.quantize_mx(out=p_codes[:].bitcast(FP8X4), scales=p_scales[:], in_=grouped_of[PASSES + g][:])
+
+        def peak_four(g):
+            peak = late.tile([P, PACK * VOXELS], BF16)
+            peak_of[g] = peak
+            best2 = best_of[PASSES + g]
+            nc.vector.tensor_tensor(out=peak[:], in0=best2[:, 0:512], in1=best2[:, 512:1024], op=ALU.max)
+
+        def peak_all(g):
+            q, r = divmod(g, GROUP)
+            if r == 0:
+                a_pair = late.tile([P, GROUP, PACK * VOXELS], BF16, align_bytes=64)
+                a_grouped[q] = a_pair
+            nc.vector.tensor_tensor(out=a_grouped[q][:, r, :], in0=peak_of[g][:], in1=peak_first[:, g, :], op=ALU.max)
+
+        def quantise_a(q):
+            passes = slice(GROUP * q, GROUP * (q + 1))
+            nc.vector.quantize_mx(
+                out=a_codes[:, passes, :].rearrange("p g n -> p (g n)").bitcast(FP8X4),
+                scales=a_scales[:, passes, :].rearrange("p g n -> p (g n)"),
+                in_=a_grouped[q][:].rearrange("p i w -> p (i w)"),
+            )
+
+        ya_tiles = {}
+        for s in range(PASSES, 2 * PASSES):
+            g = s - PASSES
+            for t in range(3):
+                multiply0(s, t)
+            if w1_next < W1_TILES:
+                turn_w1(w1_next)
+            multiply0(s, 3)
+            for t in range(3):
+                normalise0(s, t)
+            if w1_next < W1_TILES:
+                copy_w1(w1_next)
+            normalise0(s, 3)
+            layer1(g, 0, p_codes_first[:, g, :], p_scales_first[:, g, :])
+            if g >= 2:
+                layer1(g - 2, 1, p_codes_of[g - 2][:], p_scales_of[g - 2][:])
+            if g == PASSES - 3:
+                ya_ps = psum_w1.tile([P, VOXELS], F32, tag="w1t")
+                ya_tiles[0] = ya_ps
+                layer1_peak(0, ya_ps, range(PASSES - 6))
+            if g == PASSES - 1:
+                layer1_peak(0, ya_tiles[0], range(PASSES - 6, PASSES - 4))
+
+            interleave0(s - 1)
+            if g == 0:
+                nc.vector.tensor_tensor(
+                    out=peak_first[:, s - 2, :], in0=best_of[s - 2][:, 0:512], in1=best_of[s - 2][:, 512:1024], op=ALU.max
+                )
+                nc.vector.quantize_mx(
+                    out=p_codes_first[:, s - 1, :].bitcast(FP8X4), scales=p_scales_first[:, s - 1, :], in_=grouped_of[s - 1][:]
+                )
+            elif g == 1:
+                nc.vector.tensor_tensor(
+                    out=peak_first[:, s - 2, :], in0=best_of[s - 2][:, 0:512], in1=best_of[s - 2][:, 512:1024], op=ALU.max
+                )
+                quantise_p(0)
+            else:
+                peak_four(g - 2)
+                quantise_p(g - 1)
+                peak_all(g - 2)
+            best_two(s - 1)
+            if w1_next % GROUP == 0 and w1_next <= W1_TILES:
+                quantise_w1(w1_next // GROUP - 1)
+            if g % 2 == 0 and g >= 4:
+                quantise_a(g // 2 - 2)
+            if g == PASSES - 1:
+                quantise_a(PASSES // GROUP - 2)
+            w1_next += 1
+            if w1_next % GROUP == 0 and w1_next // GROUP + 2 < W1_TILES // GROUP:
+                load_w1(w1_next // GROUP + 2)
+
+        signed = last.tile([P, 2, 2, HALF], F32)
+        peak1 = last.tile([P, 2, VOXELS], F32)
+        half4 = last.tile([P, 2, 256], F32)
+        ya = last.tile([P, 2, VOXELS], F32)
         y1 = last.tile([P, 2, 2, HALF], F32)
+        end = PASSES - 1
+        layer1(end - 1, 1, p_codes_of[end - 1][:], p_scales_of[end - 1][:])
+        for h in range(2):
+            nc.scalar.activation(out=signed[:, h, 0, :], in_=acc[h][0][:], func=ACT.Copy, scale=sgn1[:, h : h + 1])
+        interleave0(2 * PASSES - 1)
+        peak_four(end - 1)
+        quantise_p(end)
+        best_two(2 * PASSES - 1)
+        peak_all(end - 1)
+        nc.vector.tensor_tensor(out=half4[:], in0=signed[:, :, 0, 0:256], in1=signed[:, :, 0, 256:512], op=ALU.max)
+        peak_four(end)
+        nc.vector.tensor_tensor(out=peak1[:], in0=half4[:, :, 0:128], in1=half4[:, :, 128:256], op=ALU.max)
+        peak_all(end)
+        quantise_a(PASSES // GROUP - 1)
+        ya_ps1 = psum_y0.tile([P, VOXELS], F32, tag="y0")
+        ya_tiles[1] = ya_ps1
+        layer1_peak(0, ya_tiles[0], range(PASSES - 4, PASSES - 2))
+        layer1_peak(1, ya_ps1, range(PASSES - 2))
+        layer1(end, 1, p_codes_of[end][:], p_scales_of[end][:])
+        for h in range(2):
+            layer1_peak(h, ya_tiles[h], range(PASSES - 2, PASSES))
+
         stats1 = last.tile([P, 2, 2, 6], F32)
         mv1 = last.tile([P, 2, 2], F32)
         for h in range(2):
-            for half in range(2):
-                nc.vector.tensor_tensor(
-                    out=y1[:, h, half, :].rearrange("p (m n) -> p m n", n=VOXELS),
-                    in0=acc[h][half][:].rearrange("p (m n) -> p m n", n=VOXELS),
-                    in1=ya[:, h, :].unsqueeze(1).to_broadcast([P, POINTS // 2, VOXELS]),
-                    op=ALU.add,
+            nc.scalar.activation(out=ya[:, h, :], in_=ya_tiles[h][:], func=ACT.Copy, scale=sgn1[:, h : h + 1])
+        best = last.tile([P, 2, VOXELS], F32)
+
+        def add_peak(h, half):
+            points = "p (m n) -> p m n"
+            y1_half = y1[:, h, half, :].rearrange(points, n=VOXELS)
+            shared = ya[:, h, :].unsqueeze(1).to_broadcast([P, POINTS // 2, VOXELS])
+            if half == 0:
+                nc.gpsimd.tensor_tensor(out=y1_half, in0=signed[:, h, 0, :].rearrange(points, n=VOXELS), in1=shared, op=ALU.add)
+            else:
+                nc.vector.scalar_tensor_tensor(
+                    out=y1_half, in0=acc[h][1][:].rearrange(points, n=VOXELS), scalar=sgn1[:, h : h + 1], in1=shared,
+                    op0=ALU.mult, op1=ALU.add,
                 )
-                nc.vector.bn_stats(out=stats1[:, h, half, :], in_=y1[:, h, half, :])
-            nc.vector.bn_aggr(out=mv1[:, h, :], in_=stats1[:, h, :, :].rearrange("p q s -> p (q s)"))
-        var_eps1 = last.tile([P, 2], F32)
+
+        def statistics1(h, half):
+            nc.vector.bn_stats(out=stats1[:, h, half, :], in_=y1[:, h, half, :])
+
+        add_peak(0, 0)
+        add_peak(1, 0)
+        add_peak(0, 1)
+        add_peak(1, 1)
+        for h in range(2):
+            nc.scalar.activation(out=signed[:, h, 1, :], in_=acc[h][1][:], func=ACT.Copy, scale=sgn1[:, h : h + 1])
+        statistics1(0, 1)
+        statistics1(1, 1)
+        statistics1(0, 0)
+        nc.vector.tensor_tensor(out=half4[:], in0=signed[:, :, 1, 0:256], in1=signed[:, :, 1, 256:512], op=ALU.max)
+        nc.vector.bn_aggr(out=mv1[:, 0, :], in_=stats1[:, 0, :, :].rearrange("p q s -> p (q s)"))
+        statistics1(1, 0)
+        nc.vector.tensor_tensor(out=best[:], in0=half4[:, :, 0:128], in1=half4[:, :, 128:256], op=ALU.max)
+        nc.vector.bn_aggr(out=mv1[:, 1, :], in_=stats1[:, 1, :, :].rearrange("p q s -> p (q s)"))
         std1 = last.tile([P, 2], F32)
         rstd1 = last.tile([P, 2], F32)
         scale1 = last.tile([P, 2], F32)
         mscale1 = last.tile([P, 2], F32)
         shift1 = last.tile([P, 2], F32)
-        nc.vector.tensor_scalar(out=var_eps1[:], in0=mv1[:, :, 1], scalar1=EPS, scalar2=None, op0=ALU.add)
-        nc.scalar.sqrt(out=std1[:], in_=var_eps1[:])
+        nc.scalar.activation(out=std1[:], in_=mv1[:, :, 1], func=ACT.Sqrt, bias=eps[:, 0:1])
+        nc.vector.tensor_tensor(out=best[:], in0=best[:], in1=peak1[:], op=ALU.max)
         nc.vector.reciprocal(out=rstd1[:], in_=std1[:])
-        nc.vector.tensor_tensor(out=scale1[:], in0=gamma1_t, in1=rstd1[:], op=ALU.mult)
+        nc.vector.tensor_tensor(out=best[:], in0=best[:], in1=ya[:], op=ALU.add)
+        nc.vector.tensor_tensor(out=scale1[:], in0=gamma1_abs[:], in1=rstd1[:], op=ALU.mult)
         nc.vector.tensor_tensor(out=mscale1[:], in0=mv1[:, :, 0], in1=scale1[:], op=ALU.mult)
         nc.vector.tensor_tensor(out=shift1[:], in0=beta1_t, in1=mscale1[:], op=ALU.subtract)
 
-        z = last.tile([P, 2, ROWS], F32)
-        z4 = last.tile([P, 2, 512], F32)
-        z2 = last.tile([P, 2, 256], F32)
         z1 = last.tile([P, 2, VOXELS], F32)
-        out_ps = psum_rest.tile([P, 2, P], F32, tag="y0")
+        out_ps = psum_y0.tile([P, 2, P], F32, tag="y0")
         for h in range(2):
             nc.scalar.activation(
-                out=z[:, h, :], in_=y1[:, h, :, :].rearrange("p q r -> p (q r)"), func=ACT.Relu,
-                bias=shift1[:, h : h + 1], scale=scale1[:, h : h + 1],
+                out=z1[:, h, :], in_=best[:, h, :], func=ACT.Relu, bias=shift1[:, h : h + 1], scale=scale1[:, h : h + 1]
             )
-            nc.vector.tensor_tensor(out=z4[:, h, :], in0=z[:, h, 0:512], in1=z[:, h, 512:1024], op=ALU.max)
-            nc.vector.tensor_tensor(out=z2[:, h, :], in0=z4[:, h, 0:256], in1=z4[:, h, 256:512], op=ALU.max)
-            nc.vector.tensor_tensor(out=z1[:, h, :], in0=z2[:, h, 0:128], in1=z2[:, h, 128:256], op=ALU.max)
             nc.tensor.transpose(out_ps[:, h, :], z1[:, h, :], ident_f32[:])
         out_sb = last.tile([P, P, 2], F32)
         nc.vector.tensor_copy(out=out_sb[:], in_=out_ps[:].rearrange("p h c -> p c h"))

@@ -26,6 +26,7 @@ PASSES = C0 // K_PASS
 CHUNKS = C0 // P
 HALF = ROWS // 2
 GROUP = 2
+VECTOR_ROWS = 448
 W1_TILES = 2 * PASSES
 
 FLOPS = 2 * ROWS * C * C0 + 2 * ROWS * C0 * C1 + 2 * VOXELS * C0 * C1
@@ -123,18 +124,31 @@ def tile_vfe_k_kernel(tc, voxel_feats, W0, gamma0, beta0, W1, gamma1, beta1, out
                 out=planes_of[s][:, t, :], in_=y0_tiles[s, t][:], func=ACT.Relu, bias=shift0[:, j : j + 1], scale=scale0[:, j : j + 1]
             )
 
-        def interleave0(s):
-            grouped = flow.tile([P, PACK * HALF], BF16, align_bytes=64)
-            grouped_of[s] = grouped
-            nc.vector.tensor_copy(
-                out=grouped[:].rearrange("p (c i t) -> p c t i", i=4, t=PACK),
-                in_=planes_of[s][:].rearrange("p t (c i) -> p c t i", i=4),
+        def interleave0(s, engine_copy, lo, hi):
+            if s not in grouped_of:
+                grouped = flow.tile([P, PACK * HALF], BF16, align_bytes=64)
+                grouped_of[s] = grouped
+            engine_copy(
+                out=grouped_of[s][:, PACK * lo : PACK * hi].rearrange("p (c i t) -> p c t i", i=4, t=PACK),
+                in_=planes_of[s][:, :, lo:hi].rearrange("p t (c i) -> p c t i", i=4),
             )
 
         def best_two(s):
-            best2 = flow.tile([P, 2 * PACK * VOXELS], BF16)
-            best_of[s] = best2
-            nc.vector.tensor_tensor(out=best2[:], in0=grouped_of[s][:, 0:1024], in1=grouped_of[s][:, 1024:2048], op=ALU.max)
+            k, i = divmod(s, GROUP)
+            if i == 0:
+                best2 = flow.tile([P, GROUP, 2 * PACK * VOXELS], BF16, bufs=2)
+                best_of[k] = best2
+            nc.vector.tensor_tensor(
+                out=best_of[k][:, i, :], in0=grouped_of[s][:, 0:1024], in1=grouped_of[s][:, 1024:2048], op=ALU.max
+            )
+
+        def best_four(k, out):
+            nc.vector.tensor_tensor(out=out, in0=best_of[k][:, :, 0:512], in1=best_of[k][:, :, 512:1024], op=ALU.max)
+
+        def quantise_first(g):
+            nc.vector.quantize_mx(
+                out=p_codes_first[:, g, :].bitcast(FP8X4), scales=p_scales_first[:, g, :], in_=grouped_of[g][:]
+            )
 
         with ExitStack() as first:
             once = first.enter_context(tc.tile_pool(name="once", bufs=1))
@@ -154,8 +168,16 @@ def tile_vfe_k_kernel(tc, voxel_feats, W0, gamma0, beta0, W1, gamma1, beta1, out
                     out=raw[:].rearrange("p g t c -> p g (t c)"), in_=w0_view[:, GROUP * q : GROUP * (q + 1), :]
                 )
 
+            ones_bf = once.tile([P, P], BF16)
+            nc.vector.memset(ones_bf[:], 1.0)
+            gb_rows = once.tile([P, K_PASS], BF16)
+            nc.vector.memset(gb_rows[:], 0.0)
             load_w0(0)
             load_w1(0)
+            nc.sync.dma_start(out=gb_rows[0:16, :], in_=gamma0.rearrange("(r w) -> r w", w=K_PASS))
+            nc.sync.dma_start(out=gb_rows[16:32, :], in_=beta0.rearrange("(r w) -> r w", w=K_PASS))
+            nc.sync.dma_start(out=gb_rows[32:33, 0:C1], in_=gamma1.rearrange("(r w) -> r w", w=C1))
+            nc.sync.dma_start(out=gb_rows[33:34, 0:C1], in_=beta1.rearrange("(r w) -> r w", w=C1))
             load_w0(1)
             load_w1(1)
             load_w0(2)
@@ -166,15 +188,6 @@ def tile_vfe_k_kernel(tc, voxel_feats, W0, gamma0, beta0, W1, gamma1, beta1, out
             load_w0(6)
             load_w0(7)
 
-            gb_rows = once.tile([P, K_PASS], BF16)
-            nc.vector.memset(gb_rows[:], 0.0)
-            nc.scalar.dma_start(out=gb_rows[0:16, :], in_=gamma0.rearrange("(r w) -> r w", w=K_PASS))
-            nc.scalar.dma_start(out=gb_rows[16:32, :], in_=beta0.rearrange("(r w) -> r w", w=K_PASS))
-            nc.scalar.dma_start(out=gb_rows[32:33, 0:C1], in_=gamma1.rearrange("(r w) -> r w", w=C1))
-            nc.scalar.dma_start(out=gb_rows[33:34, 0:C1], in_=beta1.rearrange("(r w) -> r w", w=C1))
-
-            ones_bf = once.tile([P, P], BF16)
-            nc.vector.memset(ones_bf[:], 1.0)
             ones_f32 = once.tile([P, 1], F32)
             nc.vector.memset(ones_f32[:], 1.0)
             mu_pieces = once.tile([P, 4], BF16)
@@ -197,9 +210,9 @@ def tile_vfe_k_kernel(tc, voxel_feats, W0, gamma0, beta0, W1, gamma1, beta1, out
                 w0_ps[g] = w0t_ps
 
             def copy_w0(g):
-                nc.scalar.copy(out=w0T[:, PACK * g : PACK * (g + 1), :], in_=w0_ps[g][:])
                 wide = stage.tile([P, PACK, P], F32)
                 nc.scalar.copy(out=wide[:], in_=w0_ps[g][:])
+                nc.scalar.copy(out=w0T[:, PACK * g : PACK * (g + 1), :], in_=w0_ps[g][:])
                 w0_f32[g] = wide
 
             groups = [[0], [1]] + [[g, g + 1] for g in range(2, PASSES, 2)]
@@ -255,15 +268,13 @@ def tile_vfe_k_kernel(tc, voxel_feats, W0, gamma0, beta0, W1, gamma1, beta1, out
                 nc.tensor.matmul(out=sum_ps[:], lhsT=ones_bf[:], rhs=x_sb[:, m, :], start=(m == 0), stop=(m == POINTS - 1))
             mu_rows = once.tile([P, C], F32)
             nc.vector.tensor_scalar(out=mu_rows[:], in0=sum_ps[:], scalar1=1.0 / ROWS, scalar2=None, op0=ALU.mult)
+            turn_w0(0)
+            copy_w0(0)
             col_ps = psum_y0.tile([P, 2], F32, tag="y0")
             for m in range(POINTS):
                 nc.tensor.matmul(out=col_ps[:], lhsT=x_sb[:, m, :], rhs=ones_bf[:, 0:2], start=(m == 0), stop=(m == POINTS - 1))
-            xt_ps = psum_y0.tile([P, POINTS, VOXELS], BF16, tag="y0")
-            for m in range(POINTS):
-                nc.tensor.transpose(xt_ps[:, m, :], x_sb[:, m, :], ident_bf[:])
-            nc.scalar.copy(out=xT[:], in_=xt_ps[:].rearrange("p m n -> p (m n)"))
-            turn_w0(0)
-            copy_w0(0)
+            turn_w1(0)
+            copy_w1(0)
             cov_ps = psum_two.tile([P, C], F32, tag="wcov")
             for q in range(2):
                 xc = once.tile([P, POINTS // 2, C], F32, name="xc%d" % q)
@@ -275,13 +286,10 @@ def tile_vfe_k_kernel(tc, voxel_feats, W0, gamma0, beta0, W1, gamma1, beta1, out
                     nc.tensor.matmul(
                         out=cov_ps[:], lhsT=xc[:, m, :], rhs=xc[:, m, :], start=(q == 0 and m == 0), stop=(q == 1 and m == 3)
                     )
-            turn_w1(0)
-            copy_w1(0)
-            gb_words = gb_rows[:].bitcast(F32)
-            gb_ps = psum_y0.tile([P, 3, P], F32, tag="y0")
-            for u in range(2):
-                nc.tensor.transpose(gb_ps[:, u, :], gb_words[:, u : 2 * P : 2], ident_f32[:])
-            nc.tensor.transpose(gb_ps[:, 2, :], gb_words[:, 0:P], ident_f32[:])
+            xt_ps = psum_y0.tile([P, POINTS, VOXELS], BF16, tag="y0")
+            for m in range(POINTS):
+                nc.tensor.transpose(xt_ps[:, m, :], x_sb[:, m, :], ident_bf[:])
+            nc.scalar.copy(out=xT[:], in_=xt_ps[:].rearrange("p m n -> p (m n)"))
             rest0 = once.tile([P, 1], F32)
             rest1 = once.tile([P, 1], F32)
             rest2 = once.tile([P, 1], F32)
@@ -295,32 +303,31 @@ def tile_vfe_k_kernel(tc, voxel_feats, W0, gamma0, beta0, W1, gamma1, beta1, out
             nc.vector.tensor_scalar(out=cov[:], in0=cov_ps[:], scalar1=1.0 / ROWS, scalar2=None, op0=ALU.mult)
 
             moments(0)
+            gb_words = gb_rows[:].bitcast(F32)
+            gb_ps = psum_y0.tile([P, 3, P], F32, tag="y0")
+            for u in range(2):
+                nc.tensor.transpose(gb_ps[:, u, :], gb_words[:, u : 2 * P : 2], ident_f32[:])
+            nc.tensor.transpose(gb_ps[:, 2, :], gb_words[:, 0:P], ident_f32[:])
             turn_w0(1)
             copy_w0(1)
             turn_w1(1)
-            copy_w1(1)
-            moments(1)
             gb_halves = gb_ps[:].rearrange("p u r -> p (u r)").bitcast(BF16).rearrange("p (u r e) -> p u r e", u=3, e=2)
+            for t in range(PACK):
+                variance(0, t)
+            deviation(0)
+            copy_w1(1)
             for u in range(2):
                 nc.vector.tensor_copy(
                     out=gb[:, 0 : 2 * CHUNKS].rearrange("p (r u e) -> p u r e", u=2, e=2)[:, u], in_=gb_halves[:, u, 0:32, :]
                 )
-            for t in range(PACK):
-                variance(0, t)
-            deviation(0)
-            nc.vector.tensor_copy(out=gb[:, 128:132].rearrange("p (r e) -> p r e", e=2), in_=gb_halves[:, 2, 32:34, :])
             for work in constants(0):
                 work()
-            quantise_w1(0)
-            nc.vector.tensor_scalar(out=sgn1[:], in0=gamma1_t, scalar1=0.0, scalar2=2.0, op0=ALU.is_ge, op1=ALU.mult)
-            nc.vector.tensor_scalar(out=sgn1[:], in0=sgn1[:], scalar1=1.0, scalar2=None, op0=ALU.subtract)
-            nc.vector.tensor_tensor(out=gamma1_abs[:], in0=gamma1_t, in1=sgn1[:], op=ALU.mult)
-            for g in range(2, 4):
-                turn_w0(g)
-                copy_w0(g)
+            nc.vector.tensor_copy(out=gb[:, 128:132].rearrange("p (r e) -> p r e", e=2), in_=gb_halves[:, 2, 32:34, :])
+            moments(1)
+            load_w1(4)
 
-            w1_next = 2
             for s in range(PASSES):
+                w1_tile = s + 2
                 ahead = [2, 3] if s == 0 else [s + 3] if s + 3 < PASSES else []
                 ready = 1 if s == 0 else s // 2 + 2 if s % 2 == 1 and s + 1 < PASSES else None
                 if s == 0:
@@ -328,49 +335,64 @@ def tile_vfe_k_kernel(tc, voxel_feats, W0, gamma0, beta0, W1, gamma1, beta1, out
                         variance(1, t)
                 for t in range(3):
                     multiply0(s, t)
-                turn_w1(w1_next)
+                if s == 0:
+                    turn_w0(2)
+                turn_w1(w1_tile)
                 multiply0(s, 3)
                 for t in range(3):
                     normalise0(s, t)
                     if t == 0 and ready is not None:
                         deviation(ready)
-                copy_w1(w1_next)
+                    if t == 1 and s == 0:
+                        copy_w0(2)
+                copy_w1(w1_tile)
                 normalise0(s, 3)
+
                 small = constants(ready) if ready is not None else []
                 if s >= 1:
-                    interleave0(s - 1)
+                    interleave0(s - 1, nc.vector.tensor_copy, 0, HALF)
                 for work in small[0:1]:
                     work()
-                if s >= 2:
-                    nc.vector.tensor_tensor(
-                        out=peak_first[:, s - 2, :], in0=best_of[s - 2][:, 0:512], in1=best_of[s - 2][:, 512:1024], op=ALU.max
-                    )
+                if s % 2 == 0:
+                    quantise_w1(w1_tile // GROUP - 1)
+                elif s >= 3:
+                    best_four(s // 2 - 1, peak_first[:, s - 3 : s - 1, :])
                 for work in small[1:2]:
                     work()
-                if s >= 1:
-                    nc.vector.quantize_mx(
-                        out=p_codes_first[:, s - 1, :].bitcast(FP8X4), scales=p_scales_first[:, s - 1, :], in_=grouped_of[s - 1][:]
-                    )
+                if s == 0:
+                    nc.vector.tensor_scalar(out=sgn1[:], in0=gamma1_t, scalar1=0.0, scalar2=2.0, op0=ALU.is_ge, op1=ALU.mult)
+                else:
+                    quantise_first(s - 1)
                 for work in small[2:3]:
                     work()
-                if s >= 1:
+                if s == 0:
+                    nc.vector.tensor_scalar(out=sgn1[:], in0=sgn1[:], scalar1=1.0, scalar2=None, op0=ALU.subtract)
+                else:
                     best_two(s - 1)
                 for work in small[3:4]:
                     work()
-                if w1_next % GROUP == 0 and s >= 1:
-                    quantise_w1(w1_next // GROUP - 1)
-                for work in small[4:5]:
-                    work()
+                if s == 0:
+                    nc.vector.tensor_tensor(out=gamma1_abs[:], in0=gamma1_t, in1=sgn1[:], op=ALU.mult)
+                    for work in small[4:5]:
+                        work()
                 for g in ahead:
+                    if g == 3:
+                        turn_w0(3)
+                        copy_w0(3)
                     moments(g)
                     for t in range(PACK):
                         variance(g, t)
+                        if s > 0 and t == 0:
+                            for work in small[4:5]:
+                                work()
+                if not ahead:
+                    for work in small[4:5]:
+                        work()
                 if s + 4 < PASSES:
                     turn_w0(s + 4)
                     copy_w0(s + 4)
-                w1_next += 1
-                if w1_next % GROUP == 0:
-                    load_w1(w1_next // GROUP + 2)
+                if w1_tile % GROUP == 1:
+                    load_w1(w1_tile // GROUP + 4)
 
         last = ctx.enter_context(tc.tile_pool(name="last", bufs=1))
         late = ctx.enter_context(tc.tile_pool(name="late", bufs=3))
@@ -413,77 +435,72 @@ def tile_vfe_k_kernel(tc, voxel_feats, W0, gamma0, beta0, W1, gamma1, beta1, out
             p_scales_of[g] = p_scales
             nc.vector.quantize_mx(out=p_codes[:].bitcast(FP8X4), scales=p_scales[:], in_=grouped_of[PASSES + g][:])
 
-        def peak_four(g):
-            peak = late.tile([P, PACK * VOXELS], BF16)
-            peak_of[g] = peak
-            best2 = best_of[PASSES + g]
-            nc.vector.tensor_tensor(out=peak[:], in0=best2[:, 0:512], in1=best2[:, 512:1024], op=ALU.max)
+        def peak_four(k):
+            peak = late.tile([P, GROUP, PACK * VOXELS], BF16, bufs=2)
+            peak_of[k] = peak
+            best_four(k, peak[:])
 
-        def peak_all(g):
-            q, r = divmod(g, GROUP)
-            if r == 0:
-                a_pair = late.tile([P, GROUP, PACK * VOXELS], BF16, align_bytes=64)
-                a_grouped[q] = a_pair
-            nc.vector.tensor_tensor(out=a_grouped[q][:, r, :], in0=peak_of[g][:], in1=peak_first[:, g, :], op=ALU.max)
+        def peak_all(k):
+            g = GROUP * k - PASSES
+            a_pair = late.tile([P, GROUP, PACK * VOXELS], BF16, bufs=2, align_bytes=64)
+            a_grouped[k] = a_pair
+            nc.vector.tensor_tensor(out=a_pair[:], in0=peak_of[k][:], in1=peak_first[:, g : g + GROUP, :], op=ALU.max)
 
-        def quantise_a(q):
-            passes = slice(GROUP * q, GROUP * (q + 1))
+        def quantise_a(k):
+            g = GROUP * k - PASSES
             nc.vector.quantize_mx(
-                out=a_codes[:, passes, :].rearrange("p g n -> p (g n)").bitcast(FP8X4),
-                scales=a_scales[:, passes, :].rearrange("p g n -> p (g n)"),
-                in_=a_grouped[q][:].rearrange("p i w -> p (i w)"),
+                out=a_codes[:, g : g + GROUP, :].rearrange("p g n -> p (g n)").bitcast(FP8X4),
+                scales=a_scales[:, g : g + GROUP, :].rearrange("p g n -> p (g n)"),
+                in_=a_grouped[k][:].rearrange("p i w -> p (i w)"),
             )
 
+        half_pairs = PASSES // GROUP
+        last_pair = 2 * half_pairs - 1
         ya_tiles = {}
         for s in range(PASSES, 2 * PASSES):
             g = s - PASSES
+            w1_tile = s + 2
             for t in range(3):
                 multiply0(s, t)
-            if w1_next < W1_TILES:
-                turn_w1(w1_next)
+            if w1_tile < W1_TILES:
+                turn_w1(w1_tile)
             multiply0(s, 3)
-            for t in range(3):
+            normalise0(s, 0)
+            if g >= 1:
+                interleave0(s - 1, nc.scalar.copy, VECTOR_ROWS, HALF)
+            for t in range(1, 3):
                 normalise0(s, t)
-            if w1_next < W1_TILES:
-                copy_w1(w1_next)
+            if w1_tile < W1_TILES:
+                copy_w1(w1_tile)
             normalise0(s, 3)
             layer1(g, 0, p_codes_first[:, g, :], p_scales_first[:, g, :])
             if g >= 2:
                 layer1(g - 2, 1, p_codes_of[g - 2][:], p_scales_of[g - 2][:])
-            if g == PASSES - 3:
+            if w1_tile == W1_TILES:
                 ya_ps = psum_w1.tile([P, VOXELS], F32, tag="w1t")
                 ya_tiles[0] = ya_ps
-                layer1_peak(0, ya_ps, range(PASSES - 6))
-            if g == PASSES - 1:
-                layer1_peak(0, ya_tiles[0], range(PASSES - 6, PASSES - 4))
+                layer1_peak(0, ya_ps, range(PASSES - 8))
 
-            interleave0(s - 1)
-            if g == 0:
-                nc.vector.tensor_tensor(
-                    out=peak_first[:, s - 2, :], in0=best_of[s - 2][:, 0:512], in1=best_of[s - 2][:, 512:1024], op=ALU.max
-                )
-                nc.vector.quantize_mx(
-                    out=p_codes_first[:, s - 1, :].bitcast(FP8X4), scales=p_scales_first[:, s - 1, :], in_=grouped_of[s - 1][:]
-                )
-            elif g == 1:
-                nc.vector.tensor_tensor(
-                    out=peak_first[:, s - 2, :], in0=best_of[s - 2][:, 0:512], in1=best_of[s - 2][:, 512:1024], op=ALU.max
-                )
-                quantise_p(0)
+            interleave0(s - 1, nc.vector.tensor_copy, 0, VECTOR_ROWS if g >= 1 else HALF)
+            k = s // 2 - 1
+            if s % 2 == 0:
+                if k > half_pairs:
+                    peak_all(k - 1)
+                if w1_tile <= W1_TILES:
+                    quantise_w1(w1_tile // GROUP - 1)
+            elif k < half_pairs:
+                best_four(k, peak_first[:, GROUP * k : GROUP * (k + 1), :])
             else:
-                peak_four(g - 2)
+                peak_four(k)
+            if g == 0:
+                quantise_first(s - 1)
+            else:
                 quantise_p(g - 1)
-                peak_all(g - 2)
+            if s % 2 == 1 and k > half_pairs:
+                quantise_a(k - 1)
             best_two(s - 1)
-            if w1_next % GROUP == 0 and w1_next <= W1_TILES:
-                quantise_w1(w1_next // GROUP - 1)
-            if g % 2 == 0 and g >= 4:
-                quantise_a(g // 2 - 2)
-            if g == PASSES - 1:
-                quantise_a(PASSES // GROUP - 2)
-            w1_next += 1
-            if w1_next % GROUP == 0 and w1_next // GROUP + 2 < W1_TILES // GROUP:
-                load_w1(w1_next // GROUP + 2)
+            if w1_tile % GROUP == 1 and w1_tile // GROUP + 4 < W1_TILES // GROUP:
+                load_w1(w1_tile // GROUP + 4)
 
         signed = last.tile([P, 2, 2, HALF], F32)
         peak1 = last.tile([P, 2, VOXELS], F32)
@@ -491,23 +508,26 @@ def tile_vfe_k_kernel(tc, voxel_feats, W0, gamma0, beta0, W1, gamma1, beta1, out
         ya = last.tile([P, 2, VOXELS], F32)
         y1 = last.tile([P, 2, 2, HALF], F32)
         end = PASSES - 1
-        layer1(end - 1, 1, p_codes_of[end - 1][:], p_scales_of[end - 1][:])
+        interleave0(2 * PASSES - 1, nc.scalar.copy, VECTOR_ROWS, HALF)
         for h in range(2):
             nc.scalar.activation(out=signed[:, h, 0, :], in_=acc[h][0][:], func=ACT.Copy, scale=sgn1[:, h : h + 1])
-        interleave0(2 * PASSES - 1)
-        peak_four(end - 1)
+        layer1(end - 1, 1, p_codes_of[end - 1][:], p_scales_of[end - 1][:])
+        interleave0(2 * PASSES - 1, nc.vector.tensor_copy, 0, VECTOR_ROWS)
+        peak_all(last_pair - 1)
         quantise_p(end)
         best_two(2 * PASSES - 1)
-        peak_all(end - 1)
+        quantise_a(last_pair - 1)
+        peak_four(last_pair)
         nc.vector.tensor_tensor(out=half4[:], in0=signed[:, :, 0, 0:256], in1=signed[:, :, 0, 256:512], op=ALU.max)
-        peak_four(end)
+        peak_all(last_pair)
         nc.vector.tensor_tensor(out=peak1[:], in0=half4[:, :, 0:128], in1=half4[:, :, 128:256], op=ALU.max)
-        peak_all(end)
-        quantise_a(PASSES // GROUP - 1)
+        quantise_a(last_pair)
         ya_ps1 = psum_y0.tile([P, VOXELS], F32, tag="y0")
         ya_tiles[1] = ya_ps1
-        layer1_peak(0, ya_tiles[0], range(PASSES - 4, PASSES - 2))
-        layer1_peak(1, ya_ps1, range(PASSES - 2))
+        layer1_peak(0, ya_tiles[0], range(PASSES - 8, PASSES - 4))
+        layer1_peak(1, ya_ps1, range(PASSES - 4))
+        for h in range(2):
+            layer1_peak(h, ya_tiles[h], range(PASSES - 4, PASSES - 2))
         layer1(end, 1, p_codes_of[end][:], p_scales_of[end][:])
         for h in range(2):
             layer1_peak(h, ya_tiles[h], range(PASSES - 2, PASSES))

@@ -203,14 +203,14 @@ def tile_vfe_k_kernel(tc, voxel_feats, W0, gamma0, beta0, W1, gamma1, beta1, out
             w0_ps = {}
             w0_f32 = {}
 
-            def turn_w0(g):
-                w0t_ps = psum_one.tile([P, PACK, P], BF16, tag="w0t")
+            def turn_w0(g, pool=psum_one, tag="w0t"):
+                w0t_ps = pool.tile([P, PACK, P], BF16, tag=tag)
                 for t in range(PACK):
                     nc.tensor.transpose(w0t_ps[:, t, :], w0_raw[g // GROUP][:, g % GROUP, t, :], ident_bf[:])
                 w0_ps[g] = w0t_ps
 
             def copy_w0(g):
-                wide = stage.tile([P, PACK, P], F32)
+                wide = stage.tile([P, PACK, P], F32, bufs=4)
                 nc.scalar.copy(out=wide[:], in_=w0_ps[g][:])
                 nc.scalar.copy(out=w0T[:, PACK * g : PACK * (g + 1), :], in_=w0_ps[g][:])
                 w0_f32[g] = wide
@@ -270,11 +270,15 @@ def tile_vfe_k_kernel(tc, voxel_feats, W0, gamma0, beta0, W1, gamma1, beta1, out
             nc.vector.tensor_scalar(out=mu_rows[:], in0=sum_ps[:], scalar1=1.0 / ROWS, scalar2=None, op0=ALU.mult)
             turn_w0(0)
             copy_w0(0)
+            turn_w0(1, psum_y0, "y0")
             col_ps = psum_y0.tile([P, 2], F32, tag="y0")
             for m in range(POINTS):
                 nc.tensor.matmul(out=col_ps[:], lhsT=x_sb[:, m, :], rhs=ones_bf[:, 0:2], start=(m == 0), stop=(m == POINTS - 1))
-            turn_w1(0)
-            copy_w1(0)
+            xt_ps = psum_y0.tile([P, POINTS, VOXELS], BF16, tag="y0")
+            for m in range(POINTS):
+                nc.tensor.transpose(xt_ps[:, m, :], x_sb[:, m, :], ident_bf[:])
+            nc.scalar.copy(out=xT[:], in_=xt_ps[:].rearrange("p m n -> p (m n)"))
+            copy_w0(1)
             cov_ps = psum_two.tile([P, C], F32, tag="wcov")
             for q in range(2):
                 xc = once.tile([P, POINTS // 2, C], F32, name="xc%d" % q)
@@ -286,10 +290,6 @@ def tile_vfe_k_kernel(tc, voxel_feats, W0, gamma0, beta0, W1, gamma1, beta1, out
                     nc.tensor.matmul(
                         out=cov_ps[:], lhsT=xc[:, m, :], rhs=xc[:, m, :], start=(q == 0 and m == 0), stop=(q == 1 and m == 3)
                     )
-            xt_ps = psum_y0.tile([P, POINTS, VOXELS], BF16, tag="y0")
-            for m in range(POINTS):
-                nc.tensor.transpose(xt_ps[:, m, :], x_sb[:, m, :], ident_bf[:])
-            nc.scalar.copy(out=xT[:], in_=xt_ps[:].rearrange("p m n -> p (m n)"))
             rest0 = once.tile([P, 1], F32)
             rest1 = once.tile([P, 1], F32)
             rest2 = once.tile([P, 1], F32)
@@ -302,20 +302,24 @@ def tile_vfe_k_kernel(tc, voxel_feats, W0, gamma0, beta0, W1, gamma1, beta1, out
             cov = once.tile([P, C], F32)
             nc.vector.tensor_scalar(out=cov[:], in0=cov_ps[:], scalar1=1.0 / ROWS, scalar2=None, op0=ALU.mult)
 
+            turn_w1(0)
+            copy_w1(0)
             moments(0)
             gb_words = gb_rows[:].bitcast(F32)
             gb_ps = psum_y0.tile([P, 3, P], F32, tag="y0")
             for u in range(2):
                 nc.tensor.transpose(gb_ps[:, u, :], gb_words[:, u : 2 * P : 2], ident_f32[:])
             nc.tensor.transpose(gb_ps[:, 2, :], gb_words[:, 0:P], ident_f32[:])
-            turn_w0(1)
-            copy_w0(1)
+            turn_w0(2)
+            copy_w0(2)
             turn_w1(1)
             gb_halves = gb_ps[:].rearrange("p u r -> p (u r)").bitcast(BF16).rearrange("p (u r e) -> p u r e", u=3, e=2)
             for t in range(PACK):
                 variance(0, t)
             deviation(0)
             copy_w1(1)
+            turn_w0(3)
+            copy_w0(3)
             for u in range(2):
                 nc.vector.tensor_copy(
                     out=gb[:, 0 : 2 * CHUNKS].rearrange("p (r u e) -> p u r e", u=2, e=2)[:, u], in_=gb_halves[:, u, 0:32, :]
@@ -328,29 +332,29 @@ def tile_vfe_k_kernel(tc, voxel_feats, W0, gamma0, beta0, W1, gamma1, beta1, out
 
             for s in range(PASSES):
                 w1_tile = s + 2
-                ahead = [2, 3] if s == 0 else [s + 3] if s + 3 < PASSES else []
+                ahead = [2] if s == 0 else [s + 3] if s + 3 < PASSES else []
                 ready = 1 if s == 0 else s // 2 + 2 if s % 2 == 1 and s + 1 < PASSES else None
                 if s == 0:
                     for t in range(PACK):
                         variance(1, t)
                 for t in range(3):
                     multiply0(s, t)
-                if s == 0:
-                    turn_w0(2)
                 turn_w1(w1_tile)
                 multiply0(s, 3)
+                if s >= 1:
+                    interleave0(s - 1, nc.vector.tensor_copy, 0, HALF)
+                if s == 1:
+                    moments(3)
+                    for t in range(PACK):
+                        variance(3, t)
                 for t in range(3):
                     normalise0(s, t)
-                    if t == 0 and ready is not None:
+                    if t == (1 if s == 1 else 0) and ready is not None:
                         deviation(ready)
-                    if t == 1 and s == 0:
-                        copy_w0(2)
                 copy_w1(w1_tile)
                 normalise0(s, 3)
 
                 small = constants(ready) if ready is not None else []
-                if s >= 1:
-                    interleave0(s - 1, nc.vector.tensor_copy, 0, HALF)
                 for work in small[0:1]:
                     work()
                 if s % 2 == 0:
@@ -376,9 +380,6 @@ def tile_vfe_k_kernel(tc, voxel_feats, W0, gamma0, beta0, W1, gamma1, beta1, out
                     for work in small[4:5]:
                         work()
                 for g in ahead:
-                    if g == 3:
-                        turn_w0(3)
-                        copy_w0(3)
                     moments(g)
                     for t in range(PACK):
                         variance(g, t)
@@ -526,17 +527,21 @@ def tile_vfe_k_kernel(tc, voxel_feats, W0, gamma0, beta0, W1, gamma1, beta1, out
         ya_tiles[1] = ya_ps1
         layer1_peak(0, ya_tiles[0], range(PASSES - 8, PASSES - 4))
         layer1_peak(1, ya_ps1, range(PASSES - 4))
-        for h in range(2):
-            layer1_peak(h, ya_tiles[h], range(PASSES - 4, PASSES - 2))
         layer1(end, 1, p_codes_of[end][:], p_scales_of[end][:])
         for h in range(2):
+            nc.scalar.activation(out=signed[:, h, 1, :], in_=acc[h][1][:], func=ACT.Copy, scale=sgn1[:, h : h + 1])
+        for h in range(2):
+            layer1_peak(h, ya_tiles[h], range(PASSES - 4, PASSES - 2))
+        for h in range(2):
             layer1_peak(h, ya_tiles[h], range(PASSES - 2, PASSES))
+        best = last.tile([P, 2, VOXELS], F32)
+        nc.vector.tensor_tensor(out=half4[:], in0=signed[:, :, 1, 0:256], in1=signed[:, :, 1, 256:512], op=ALU.max)
+        nc.vector.tensor_tensor(out=best[:], in0=half4[:, :, 0:128], in1=half4[:, :, 128:256], op=ALU.max)
 
         stats1 = last.tile([P, 2, 2, 6], F32)
         mv1 = last.tile([P, 2, 2], F32)
         for h in range(2):
             nc.scalar.activation(out=ya[:, h, :], in_=ya_tiles[h][:], func=ACT.Copy, scale=sgn1[:, h : h + 1])
-        best = last.tile([P, 2, VOXELS], F32)
 
         def add_peak(h, half):
             points = "p (m n) -> p m n"
@@ -557,34 +562,29 @@ def tile_vfe_k_kernel(tc, voxel_feats, W0, gamma0, beta0, W1, gamma1, beta1, out
         add_peak(1, 0)
         add_peak(0, 1)
         add_peak(1, 1)
-        for h in range(2):
-            nc.scalar.activation(out=signed[:, h, 1, :], in_=acc[h][1][:], func=ACT.Copy, scale=sgn1[:, h : h + 1])
         statistics1(0, 1)
         statistics1(1, 1)
+        nc.vector.tensor_tensor(out=best[:], in0=best[:], in1=peak1[:], op=ALU.max)
         statistics1(0, 0)
-        nc.vector.tensor_tensor(out=half4[:], in0=signed[:, :, 1, 0:256], in1=signed[:, :, 1, 256:512], op=ALU.max)
+        nc.vector.tensor_tensor(out=best[:], in0=best[:], in1=ya[:], op=ALU.add)
         nc.vector.bn_aggr(out=mv1[:, 0, :], in_=stats1[:, 0, :, :].rearrange("p q s -> p (q s)"))
         statistics1(1, 0)
-        nc.vector.tensor_tensor(out=best[:], in0=half4[:, :, 0:128], in1=half4[:, :, 128:256], op=ALU.max)
         nc.vector.bn_aggr(out=mv1[:, 1, :], in_=stats1[:, 1, :, :].rearrange("p q s -> p (q s)"))
         std1 = last.tile([P, 2], F32)
         rstd1 = last.tile([P, 2], F32)
-        scale1 = last.tile([P, 2], F32)
-        mscale1 = last.tile([P, 2], F32)
-        shift1 = last.tile([P, 2], F32)
         nc.scalar.activation(out=std1[:], in_=mv1[:, :, 1], func=ACT.Sqrt, bias=eps[:, 0:1])
-        nc.vector.tensor_tensor(out=best[:], in0=best[:], in1=peak1[:], op=ALU.max)
+        for h in range(2):
+            nc.vector.tensor_scalar(
+                out=best[:, h, :], in0=best[:, h, :], scalar1=mv1[:, h, 0:1], scalar2=gamma1_abs[:, h : h + 1],
+                op0=ALU.subtract, op1=ALU.mult,
+            )
         nc.vector.reciprocal(out=rstd1[:], in_=std1[:])
-        nc.vector.tensor_tensor(out=best[:], in0=best[:], in1=ya[:], op=ALU.add)
-        nc.vector.tensor_tensor(out=scale1[:], in0=gamma1_abs[:], in1=rstd1[:], op=ALU.mult)
-        nc.vector.tensor_tensor(out=mscale1[:], in0=mv1[:, :, 0], in1=scale1[:], op=ALU.mult)
-        nc.vector.tensor_tensor(out=shift1[:], in0=beta1_t, in1=mscale1[:], op=ALU.subtract)
 
         z1 = last.tile([P, 2, VOXELS], F32)
         out_ps = psum_y0.tile([P, 2, P], F32, tag="y0")
         for h in range(2):
             nc.scalar.activation(
-                out=z1[:, h, :], in_=best[:, h, :], func=ACT.Relu, bias=shift1[:, h : h + 1], scale=scale1[:, h : h + 1]
+                out=z1[:, h, :], in_=best[:, h, :], func=ACT.Relu, bias=beta1_t[:, h : h + 1], scale=rstd1[:, h : h + 1]
             )
             nc.tensor.transpose(out_ps[:, h, :], z1[:, h, :], ident_f32[:])
         out_sb = last.tile([P, P, 2], F32)

@@ -49,9 +49,10 @@ def tile_vfe_k_kernel(tc, voxel_feats, W0, gamma0, beta0, W1, gamma1, beta1, out
         sgn1 = keep.tile([P, 2], F32)
         gamma1_abs = keep.tile([P, 2], F32)
         eps = keep.tile([P, 1], F32)
-        w0T = keep.tile([P, CHUNKS, P], BF16)
+        w0T = keep.tile([P, CHUNKS, P], F32)
         scale0 = keep.tile([P, CHUNKS], F32)
         shift0 = keep.tile([P, CHUNKS], F32)
+        w0T_halves = w0T[:].rearrange("p j m -> p (j m)").bitcast(BF16)
         w1_codes = keep.tile([P, 2, PASSES, C1], U32, align_bytes=64)
         w1_scales = keep.tile([P, 2, PASSES, C1], U8, align_bytes=64)
         p_codes_first = keep.tile([P, PASSES, HALF], U32, align_bytes=64)
@@ -107,11 +108,14 @@ def tile_vfe_k_kernel(tc, voxel_feats, W0, gamma0, beta0, W1, gamma1, beta1, out
         grouped_of = {}
         best_of = {}
 
+        def w0T_bf(j):
+            return w0T_halves[:, 2 * P * j + 1 : 2 * P * (j + 1) : 2]
+
         def multiply0(s, t):
             half, g = divmod(s, PASSES)
             y0_ps = psum_y0.tile([P, HALF], F32, tag="y0")
             nc.tensor.matmul(
-                out=y0_ps[:], lhsT=w0T[:, PACK * g + t, :], rhs=xT[:, half * HALF : (half + 1) * HALF], start=True, stop=True
+                out=y0_ps[:], lhsT=w0T_bf(PACK * g + t), rhs=xT[:, half * HALF : (half + 1) * HALF], start=True, stop=True
             )
             y0_tiles[s, t] = y0_ps
 
@@ -201,7 +205,6 @@ def tile_vfe_k_kernel(tc, voxel_feats, W0, gamma0, beta0, W1, gamma1, beta1, out
             mean_ps = psum_one.tile([P, CHUNKS, 4], F32, name="mean")
             stats = {}
             w0_ps = {}
-            w0_f32 = {}
 
             def turn_w0(g, pool=psum_one, tag="w0t"):
                 w0t_ps = pool.tile([P, PACK, P], BF16, tag=tag)
@@ -210,10 +213,7 @@ def tile_vfe_k_kernel(tc, voxel_feats, W0, gamma0, beta0, W1, gamma1, beta1, out
                 w0_ps[g] = w0t_ps
 
             def copy_w0(g):
-                wide = stage.tile([P, PACK, P], F32, bufs=4)
-                nc.scalar.copy(out=wide[:], in_=w0_ps[g][:])
                 nc.scalar.copy(out=w0T[:, PACK * g : PACK * (g + 1), :], in_=w0_ps[g][:])
-                w0_f32[g] = wide
 
             groups = [[0], [1]] + [[g, g + 1] for g in range(2, PASSES, 2)]
             group_of = {g: k for k, members in enumerate(groups) for g in members}
@@ -226,10 +226,10 @@ def tile_vfe_k_kernel(tc, voxel_feats, W0, gamma0, beta0, W1, gamma1, beta1, out
                     stats[k] = [var_g]
                 wcov_ps = psum_two.tile([P, PACK, C], F32, tag="wcov")
                 for t in range(PACK):
-                    nc.tensor.matmul(out=wcov_ps[:, t, :], lhsT=w0_f32[g][:, t, :], rhs=cov[:], start=True, stop=True)
+                    nc.tensor.matmul(out=wcov_ps[:, t, :], lhsT=w0T[:, PACK * g + t, :], rhs=cov[:], start=True, stop=True)
                 for t in range(PACK):
                     nc.tensor.matmul(
-                        out=mean_ps[:, PACK * g + t, :], lhsT=w0T[:, PACK * g + t, :], rhs=mu_pieces[:], start=True, stop=True
+                        out=mean_ps[:, PACK * g + t, :], lhsT=w0T_bf(PACK * g + t), rhs=mu_pieces[:], start=True, stop=True
                     )
                 w0_ps[g] = wcov_ps
 
@@ -332,7 +332,8 @@ def tile_vfe_k_kernel(tc, voxel_feats, W0, gamma0, beta0, W1, gamma1, beta1, out
 
             for s in range(PASSES):
                 w1_tile = s + 2
-                ahead = [2] if s == 0 else [s + 3] if s + 3 < PASSES else []
+                moments_of = [2, 3] if s == 0 else [s + 3] if s + 3 < PASSES else []
+                variances_of = [2] if s == 0 else [s + 3] if s + 3 < PASSES else []
                 ready = 1 if s == 0 else s // 2 + 2 if s % 2 == 1 and s + 1 < PASSES else None
                 if s == 0:
                     for t in range(PACK):
@@ -340,23 +341,29 @@ def tile_vfe_k_kernel(tc, voxel_feats, W0, gamma0, beta0, W1, gamma1, beta1, out
                 for t in range(3):
                     multiply0(s, t)
                 turn_w1(w1_tile)
-                multiply0(s, 3)
                 if s >= 1:
-                    interleave0(s - 1, nc.vector.tensor_copy, 0, HALF)
+                    interleave0(s - 1, nc.vector.tensor_copy, 0, VECTOR_ROWS)
                 if s == 1:
-                    moments(3)
                     for t in range(PACK):
                         variance(3, t)
                 for t in range(3):
                     normalise0(s, t)
+                    if t == 0 and s >= 1:
+                        interleave0(s - 1, nc.scalar.copy, VECTOR_ROWS, HALF)
                     if t == (1 if s == 1 else 0) and ready is not None:
                         deviation(ready)
-                copy_w1(w1_tile)
-                normalise0(s, 3)
-
                 small = constants(ready) if ready is not None else []
                 for work in small[0:1]:
                     work()
+                if s == 0:
+                    multiply0(s, 3)
+                for g in moments_of:
+                    moments(g)
+                if s > 0:
+                    multiply0(s, 3)
+                copy_w1(w1_tile)
+                normalise0(s, 3)
+
                 if s % 2 == 0:
                     quantise_w1(w1_tile // GROUP - 1)
                 elif s >= 3:
@@ -379,14 +386,13 @@ def tile_vfe_k_kernel(tc, voxel_feats, W0, gamma0, beta0, W1, gamma1, beta1, out
                     nc.vector.tensor_tensor(out=gamma1_abs[:], in0=gamma1_t, in1=sgn1[:], op=ALU.mult)
                     for work in small[4:5]:
                         work()
-                for g in ahead:
-                    moments(g)
+                for g in variances_of:
                     for t in range(PACK):
                         variance(g, t)
                         if s > 0 and t == 0:
                             for work in small[4:5]:
                                 work()
-                if not ahead:
+                if not variances_of:
                     for work in small[4:5]:
                         work()
                 if s + 4 < PASSES:
@@ -467,8 +473,7 @@ def tile_vfe_k_kernel(tc, voxel_feats, W0, gamma0, beta0, W1, gamma1, beta1, out
                 turn_w1(w1_tile)
             multiply0(s, 3)
             normalise0(s, 0)
-            if g >= 1:
-                interleave0(s - 1, nc.scalar.copy, VECTOR_ROWS, HALF)
+            interleave0(s - 1, nc.scalar.copy, VECTOR_ROWS, HALF)
             for t in range(1, 3):
                 normalise0(s, t)
             if w1_tile < W1_TILES:
@@ -482,7 +487,7 @@ def tile_vfe_k_kernel(tc, voxel_feats, W0, gamma0, beta0, W1, gamma1, beta1, out
                 ya_tiles[0] = ya_ps
                 layer1_peak(0, ya_ps, range(PASSES - 8))
 
-            interleave0(s - 1, nc.vector.tensor_copy, 0, VECTOR_ROWS if g >= 1 else HALF)
+            interleave0(s - 1, nc.vector.tensor_copy, 0, VECTOR_ROWS)
             k = s // 2 - 1
             if s % 2 == 0:
                 if k > half_pairs:
@@ -507,7 +512,7 @@ def tile_vfe_k_kernel(tc, voxel_feats, W0, gamma0, beta0, W1, gamma1, beta1, out
         peak1 = last.tile([P, 2, VOXELS], F32)
         half4 = last.tile([P, 2, 256], F32)
         ya = last.tile([P, 2, VOXELS], F32)
-        y1 = last.tile([P, 2, 2, HALF], F32)
+        y1_late = last.tile([P, 2, HALF], F32)
         end = PASSES - 1
         interleave0(2 * PASSES - 1, nc.scalar.copy, VECTOR_ROWS, HALF)
         for h in range(2):
@@ -545,18 +550,18 @@ def tile_vfe_k_kernel(tc, voxel_feats, W0, gamma0, beta0, W1, gamma1, beta1, out
 
         def add_peak(h, half):
             points = "p (m n) -> p m n"
-            y1_half = y1[:, h, half, :].rearrange(points, n=VOXELS)
             shared = ya[:, h, :].unsqueeze(1).to_broadcast([P, POINTS // 2, VOXELS])
             if half == 0:
-                nc.gpsimd.tensor_tensor(out=y1_half, in0=signed[:, h, 0, :].rearrange(points, n=VOXELS), in1=shared, op=ALU.add)
+                first4 = signed[:, h, 0, :].rearrange(points, n=VOXELS)
+                nc.gpsimd.tensor_tensor(out=first4, in0=first4, in1=shared, op=ALU.add)
             else:
                 nc.vector.scalar_tensor_tensor(
-                    out=y1_half, in0=acc[h][1][:].rearrange(points, n=VOXELS), scalar=sgn1[:, h : h + 1], in1=shared,
+                    out=y1_late[:, h, :].rearrange(points, n=VOXELS), in0=acc[h][1][:].rearrange(points, n=VOXELS), scalar=sgn1[:, h : h + 1], in1=shared,
                     op0=ALU.mult, op1=ALU.add,
                 )
 
         def statistics1(h, half):
-            nc.vector.bn_stats(out=stats1[:, h, half, :], in_=y1[:, h, half, :])
+            nc.vector.bn_stats(out=stats1[:, h, half, :], in_=signed[:, h, 0, :] if half == 0 else y1_late[:, h, :])
 
         add_peak(0, 0)
         add_peak(1, 0)

@@ -65,7 +65,7 @@ def tile_vfe_k_kernel(tc, voxel_feats, W0, gamma0, beta0, W1, gamma1, beta1, out
         gamma1_t = gb[:, 128:130]
         beta1_t = gb[:, 130:132]
 
-        w1_view = W1.rearrange("(n h) k -> n h k", h=2)
+        w1_view = W1.rearrange("(h n) k -> n h k", h=2)
         w1_raw = {}
         w1_grouped = {}
 
@@ -111,9 +111,9 @@ def tile_vfe_k_kernel(tc, voxel_feats, W0, gamma0, beta0, W1, gamma1, beta1, out
         def w0T_bf(j):
             return w0T_halves[:, 2 * P * j + 1 : 2 * P * (j + 1) : 2]
 
-        def multiply0(s, t):
+        def multiply0(s, t, pool=psum_y0, tag="y0"):
             half, g = divmod(s, PASSES)
-            y0_ps = psum_y0.tile([P, HALF], F32, tag="y0")
+            y0_ps = pool.tile([P, HALF], F32, tag=tag)
             nc.tensor.matmul(
                 out=y0_ps[:], lhsT=w0T_bf(PACK * g + t), rhs=xT[:, half * HALF : (half + 1) * HALF], start=True, stop=True
             )
@@ -180,8 +180,8 @@ def tile_vfe_k_kernel(tc, voxel_feats, W0, gamma0, beta0, W1, gamma1, beta1, out
             load_w1(0)
             nc.sync.dma_start(out=gb_rows[0:16, :], in_=gamma0.rearrange("(r w) -> r w", w=K_PASS))
             nc.sync.dma_start(out=gb_rows[16:32, :], in_=beta0.rearrange("(r w) -> r w", w=K_PASS))
-            nc.sync.dma_start(out=gb_rows[32:33, 0:C1], in_=gamma1.rearrange("(r w) -> r w", w=C1))
-            nc.sync.dma_start(out=gb_rows[33:34, 0:C1], in_=beta1.rearrange("(r w) -> r w", w=C1))
+            nc.sync.dma_start(out=gb_rows[32:34, 0:P], in_=gamma1.rearrange("(r w) -> r w", w=P))
+            nc.sync.dma_start(out=gb_rows[34:36, 0:P], in_=beta1.rearrange("(r w) -> r w", w=P))
             load_w0(1)
             load_w1(1)
             load_w0(2)
@@ -202,18 +202,21 @@ def tile_vfe_k_kernel(tc, voxel_feats, W0, gamma0, beta0, W1, gamma1, beta1, out
             make_identity(nc, ident_bf[:])
             make_identity(nc, ident_f32[:])
 
-            mean_ps = psum_one.tile([P, CHUNKS, 4], F32, name="mean")
+            shared_ps = psum_one.tile([P, HALF], F32, name="shared")
+            w0t_bank = shared_ps[:, 0 : HALF // 2].bitcast(BF16)
+            mean_ps = shared_ps[:, HALF // 2 : HALF].rearrange("p (j k) -> p j k", k=4)
             stats = {}
             w0_ps = {}
 
-            def turn_w0(g, pool=psum_one, tag="w0t"):
-                w0t_ps = pool.tile([P, PACK, P], BF16, tag=tag)
+            def turn_w0(g, w0t_ps):
                 for t in range(PACK):
-                    nc.tensor.transpose(w0t_ps[:, t, :], w0_raw[g // GROUP][:, g % GROUP, t, :], ident_bf[:])
+                    nc.tensor.transpose(w0t_ps[:, P * t : P * (t + 1)], w0_raw[g // GROUP][:, g % GROUP, t, :], ident_bf[:])
                 w0_ps[g] = w0t_ps
 
             def copy_w0(g):
-                nc.scalar.copy(out=w0T[:, PACK * g : PACK * (g + 1), :], in_=w0_ps[g][:])
+                nc.scalar.copy(
+                    out=w0T[:, PACK * g : PACK * (g + 1), :], in_=w0_ps[g].rearrange("p (t m) -> p t m", t=PACK)
+                )
 
             groups = [[0], [1]] + [[g, g + 1] for g in range(2, PASSES, 2)]
             group_of = {g: k for k, members in enumerate(groups) for g in members}
@@ -268,9 +271,10 @@ def tile_vfe_k_kernel(tc, voxel_feats, W0, gamma0, beta0, W1, gamma1, beta1, out
                 nc.tensor.matmul(out=sum_ps[:], lhsT=ones_bf[:], rhs=x_sb[:, m, :], start=(m == 0), stop=(m == POINTS - 1))
             mu_rows = once.tile([P, C], F32)
             nc.vector.tensor_scalar(out=mu_rows[:], in0=sum_ps[:], scalar1=1.0 / ROWS, scalar2=None, op0=ALU.mult)
-            turn_w0(0)
+            turn_w0(0, w0t_bank)
             copy_w0(0)
-            turn_w0(1, psum_y0, "y0")
+            w0t_other = psum_y0.tile([P, PACK * P], BF16, name="w0t_other", tag="y0")
+            turn_w0(1, w0t_other[:])
             col_ps = psum_y0.tile([P, 2], F32, tag="y0")
             for m in range(POINTS):
                 nc.tensor.matmul(out=col_ps[:], lhsT=x_sb[:, m, :], rhs=ones_bf[:, 0:2], start=(m == 0), stop=(m == POINTS - 1))
@@ -307,10 +311,12 @@ def tile_vfe_k_kernel(tc, voxel_feats, W0, gamma0, beta0, W1, gamma1, beta1, out
             moments(0)
             gb_words = gb_rows[:].bitcast(F32)
             gb_ps = psum_y0.tile([P, 3, P], F32, tag="y0")
+            gb1_ps = gb_ps[:, 2, :].bitcast(BF16)[:, 0:P]
             for u in range(2):
                 nc.tensor.transpose(gb_ps[:, u, :], gb_words[:, u : 2 * P : 2], ident_f32[:])
-            nc.tensor.transpose(gb_ps[:, 2, :], gb_words[:, 0:P], ident_f32[:])
-            turn_w0(2)
+            nc.tensor.transpose(gb1_ps, gb_rows[:, 0:P], ident_bf[:])
+            w0t_third = psum_one.tile([P, PACK * P], BF16, name="w0t_third", tag="y0_last")
+            turn_w0(2, w0t_third[:])
             copy_w0(2)
             turn_w1(1)
             gb_halves = gb_ps[:].rearrange("p u r -> p (u r)").bitcast(BF16).rearrange("p (u r e) -> p u r e", u=3, e=2)
@@ -318,15 +324,15 @@ def tile_vfe_k_kernel(tc, voxel_feats, W0, gamma0, beta0, W1, gamma1, beta1, out
                 variance(0, t)
             deviation(0)
             copy_w1(1)
-            turn_w0(3)
-            copy_w0(3)
             for u in range(2):
                 nc.vector.tensor_copy(
                     out=gb[:, 0 : 2 * CHUNKS].rearrange("p (r u e) -> p u r e", u=2, e=2)[:, u], in_=gb_halves[:, u, 0:32, :]
                 )
             for work in constants(0):
                 work()
-            nc.vector.tensor_copy(out=gb[:, 128:132].rearrange("p (r e) -> p r e", e=2), in_=gb_halves[:, 2, 32:34, :])
+            nc.vector.tensor_copy(out=gb[:, 128:132], in_=gb1_ps[:, 32:36])
+            turn_w0(3, w0t_bank)
+            copy_w0(3)
             moments(1)
             load_w1(4)
 
@@ -355,12 +361,9 @@ def tile_vfe_k_kernel(tc, voxel_feats, W0, gamma0, beta0, W1, gamma1, beta1, out
                 small = constants(ready) if ready is not None else []
                 for work in small[0:1]:
                     work()
-                if s == 0:
-                    multiply0(s, 3)
+                multiply0(s, 3, psum_one, "y0_last")
                 for g in moments_of:
                     moments(g)
-                if s > 0:
-                    multiply0(s, 3)
                 copy_w1(w1_tile)
                 normalise0(s, 3)
 
@@ -396,7 +399,7 @@ def tile_vfe_k_kernel(tc, voxel_feats, W0, gamma0, beta0, W1, gamma1, beta1, out
                     for work in small[4:5]:
                         work()
                 if s + 4 < PASSES:
-                    turn_w0(s + 4)
+                    turn_w0(s + 4, w0t_bank)
                     copy_w0(s + 4)
                 if w1_tile % GROUP == 1:
                     load_w1(w1_tile // GROUP + 4)
@@ -461,6 +464,9 @@ def tile_vfe_k_kernel(tc, voxel_feats, W0, gamma0, beta0, W1, gamma1, beta1, out
                 in_=a_grouped[k][:].rearrange("p i w -> p (i w)"),
             )
 
+        def vector_rows(s):
+            return {2 * PASSES - 2: 320, 2 * PASSES - 1: 128}.get(s, VECTOR_ROWS)
+
         half_pairs = PASSES // GROUP
         last_pair = 2 * half_pairs - 1
         ya_tiles = {}
@@ -473,7 +479,7 @@ def tile_vfe_k_kernel(tc, voxel_feats, W0, gamma0, beta0, W1, gamma1, beta1, out
                 turn_w1(w1_tile)
             multiply0(s, 3)
             normalise0(s, 0)
-            interleave0(s - 1, nc.scalar.copy, VECTOR_ROWS, HALF)
+            interleave0(s - 1, nc.scalar.copy, vector_rows(s - 1), HALF)
             for t in range(1, 3):
                 normalise0(s, t)
             if w1_tile < W1_TILES:
@@ -487,7 +493,7 @@ def tile_vfe_k_kernel(tc, voxel_feats, W0, gamma0, beta0, W1, gamma1, beta1, out
                 ya_tiles[0] = ya_ps
                 layer1_peak(0, ya_ps, range(PASSES - 8))
 
-            interleave0(s - 1, nc.vector.tensor_copy, 0, VECTOR_ROWS)
+            interleave0(s - 1, nc.vector.tensor_copy, 0, vector_rows(s - 1))
             k = s // 2 - 1
             if s % 2 == 0:
                 if k > half_pairs:
@@ -514,11 +520,11 @@ def tile_vfe_k_kernel(tc, voxel_feats, W0, gamma0, beta0, W1, gamma1, beta1, out
         ya = last.tile([P, 2, VOXELS], F32)
         y1_late = last.tile([P, 2, HALF], F32)
         end = PASSES - 1
-        interleave0(2 * PASSES - 1, nc.scalar.copy, VECTOR_ROWS, HALF)
+        interleave0(2 * PASSES - 1, nc.scalar.copy, vector_rows(2 * PASSES - 1), HALF)
         for h in range(2):
             nc.scalar.activation(out=signed[:, h, 0, :], in_=acc[h][0][:], func=ACT.Copy, scale=sgn1[:, h : h + 1])
         layer1(end - 1, 1, p_codes_of[end - 1][:], p_scales_of[end - 1][:])
-        interleave0(2 * PASSES - 1, nc.vector.tensor_copy, 0, VECTOR_ROWS)
+        interleave0(2 * PASSES - 1, nc.vector.tensor_copy, 0, vector_rows(2 * PASSES - 1))
         peak_all(last_pair - 1)
         quantise_p(end)
         best_two(2 * PASSES - 1)
@@ -563,35 +569,48 @@ def tile_vfe_k_kernel(tc, voxel_feats, W0, gamma0, beta0, W1, gamma1, beta1, out
         def statistics1(h, half):
             nc.vector.bn_stats(out=stats1[:, h, half, :], in_=signed[:, h, 0, :] if half == 0 else y1_late[:, h, :])
 
+        std1 = last.tile([P, 2], F32)
+        rstd1 = last.tile([P, 2], F32)
+        z1 = last.tile([P, 2, VOXELS], F32)
+        out_sb = last.tile([P, 2, P], F32)
+
+        def aggregate(h):
+            nc.vector.bn_aggr(out=mv1[:, h, :], in_=stats1[:, h, :, :].rearrange("p q s -> p (q s)"))
+            nc.scalar.activation(out=std1[:, h : h + 1], in_=mv1[:, h, 1:2], func=ACT.Sqrt, bias=eps[:, 0:1])
+
+        def centre(h):
+            nc.vector.tensor_scalar(
+                out=best[:, h, :], in0=best[:, h, :], scalar1=mv1[:, h, 0:1], scalar2=gamma1_abs[:, h : h + 1],
+                op0=ALU.subtract, op1=ALU.mult,
+            )
+
+        def finish(h):
+            nc.vector.reciprocal(out=rstd1[:, h : h + 1], in_=std1[:, h : h + 1])
+            nc.scalar.activation(
+                out=z1[:, h, :], in_=best[:, h, :], func=ACT.Relu, bias=beta1_t[:, h : h + 1], scale=rstd1[:, h : h + 1]
+            )
+
+        def store(h):
+            out_ps = psum_y0.tile([P, P], F32, tag="y0")
+            nc.tensor.transpose(out_ps[:], z1[:, h, :], ident_f32[:])
+            nc.vector.tensor_copy(out=out_sb[:, h, :], in_=out_ps[:])
+            nc.sync.dma_start(out=out[:, h * P : (h + 1) * P], in_=out_sb[:, h, :])
+
         add_peak(0, 0)
         add_peak(1, 0)
         add_peak(0, 1)
         add_peak(1, 1)
         statistics1(0, 1)
-        statistics1(1, 1)
         nc.vector.tensor_tensor(out=best[:], in0=best[:], in1=peak1[:], op=ALU.max)
         statistics1(0, 0)
         nc.vector.tensor_tensor(out=best[:], in0=best[:], in1=ya[:], op=ALU.add)
-        nc.vector.bn_aggr(out=mv1[:, 0, :], in_=stats1[:, 0, :, :].rearrange("p q s -> p (q s)"))
+        aggregate(0)
+        statistics1(1, 1)
+        centre(0)
         statistics1(1, 0)
-        nc.vector.bn_aggr(out=mv1[:, 1, :], in_=stats1[:, 1, :, :].rearrange("p q s -> p (q s)"))
-        std1 = last.tile([P, 2], F32)
-        rstd1 = last.tile([P, 2], F32)
-        nc.scalar.activation(out=std1[:], in_=mv1[:, :, 1], func=ACT.Sqrt, bias=eps[:, 0:1])
-        for h in range(2):
-            nc.vector.tensor_scalar(
-                out=best[:, h, :], in0=best[:, h, :], scalar1=mv1[:, h, 0:1], scalar2=gamma1_abs[:, h : h + 1],
-                op0=ALU.subtract, op1=ALU.mult,
-            )
-        nc.vector.reciprocal(out=rstd1[:], in_=std1[:])
-
-        z1 = last.tile([P, 2, VOXELS], F32)
-        out_ps = psum_y0.tile([P, 2, P], F32, tag="y0")
-        for h in range(2):
-            nc.scalar.activation(
-                out=z1[:, h, :], in_=best[:, h, :], func=ACT.Relu, bias=beta1_t[:, h : h + 1], scale=rstd1[:, h : h + 1]
-            )
-            nc.tensor.transpose(out_ps[:, h, :], z1[:, h, :], ident_f32[:])
-        out_sb = last.tile([P, P, 2], F32)
-        nc.vector.tensor_copy(out=out_sb[:], in_=out_ps[:].rearrange("p h c -> p c h"))
-        nc.sync.dma_start(out=out, in_=out_sb[:].rearrange("p c h -> p (c h)"))
+        finish(0)
+        aggregate(1)
+        centre(1)
+        finish(1)
+        store(0)
+        store(1)

@@ -20,6 +20,7 @@ C = 128
 C0 = 8192
 C1 = 256
 EPS = 1e-3
+TINY = 1e-30
 PACK = 4
 K_PASS = P * PACK
 PASSES = C0 // K_PASS
@@ -49,10 +50,9 @@ def tile_vfe_k_kernel(tc, voxel_feats, W0, gamma0, beta0, W1, gamma1, beta1, out
         sgn1 = keep.tile([P, 2], F32)
         gamma1_abs = keep.tile([P, 2], F32)
         eps = keep.tile([P, 1], F32)
-        w0T = keep.tile([P, CHUNKS, P], F32)
+        w0T = keep.tile([P, CHUNKS, P], BF16)
         scale0 = keep.tile([P, CHUNKS], F32)
         shift0 = keep.tile([P, CHUNKS], F32)
-        w0T_halves = w0T[:].rearrange("p j m -> p (j m)").bitcast(BF16)
         w1_codes = keep.tile([P, 2, PASSES, C1], U32, align_bytes=64)
         w1_scales = keep.tile([P, 2, PASSES, C1], U8, align_bytes=64)
         p_codes_first = keep.tile([P, PASSES, HALF], U32, align_bytes=64)
@@ -108,14 +108,11 @@ def tile_vfe_k_kernel(tc, voxel_feats, W0, gamma0, beta0, W1, gamma1, beta1, out
         grouped_of = {}
         best_of = {}
 
-        def w0T_bf(j):
-            return w0T_halves[:, 2 * P * j + 1 : 2 * P * (j + 1) : 2]
-
         def multiply0(s, t, pool=psum_y0, tag="y0"):
             half, g = divmod(s, PASSES)
             y0_ps = pool.tile([P, HALF], F32, tag=tag)
             nc.tensor.matmul(
-                out=y0_ps[:], lhsT=w0T_bf(PACK * g + t), rhs=xT[:, half * HALF : (half + 1) * HALF], start=True, stop=True
+                out=y0_ps[:], lhsT=w0T[:, PACK * g + t, :], rhs=xT[:, half * HALF : (half + 1) * HALF], start=True, stop=True
             )
             y0_tiles[s, t] = y0_ps
 
@@ -157,7 +154,6 @@ def tile_vfe_k_kernel(tc, voxel_feats, W0, gamma0, beta0, W1, gamma1, beta1, out
         with ExitStack() as first:
             once = first.enter_context(tc.tile_pool(name="once", bufs=1))
             stage = first.enter_context(tc.tile_pool(name="stage", bufs=2))
-            psum_two = first.enter_context(tc.psum_pool(name="psum_two", bufs=2))
             psum_one = first.enter_context(tc.psum_pool(name="psum_one", bufs=1))
 
             x_sb = once.tile([P, POINTS, C], BF16)
@@ -177,12 +173,12 @@ def tile_vfe_k_kernel(tc, voxel_feats, W0, gamma0, beta0, W1, gamma1, beta1, out
             gb_rows = once.tile([P, K_PASS], BF16)
             nc.vector.memset(gb_rows[:], 0.0)
             load_w0(0)
+            load_w0(1)
             load_w1(0)
             nc.sync.dma_start(out=gb_rows[0:16, :], in_=gamma0.rearrange("(r w) -> r w", w=K_PASS))
             nc.sync.dma_start(out=gb_rows[16:32, :], in_=beta0.rearrange("(r w) -> r w", w=K_PASS))
             nc.sync.dma_start(out=gb_rows[32:34, 0:P], in_=gamma1.rearrange("(r w) -> r w", w=P))
             nc.sync.dma_start(out=gb_rows[34:36, 0:P], in_=beta1.rearrange("(r w) -> r w", w=P))
-            load_w0(1)
             load_w1(1)
             load_w0(2)
             load_w1(2)
@@ -201,80 +197,93 @@ def tile_vfe_k_kernel(tc, voxel_feats, W0, gamma0, beta0, W1, gamma1, beta1, out
             nc.scalar.activation(out=warm[:], in_=ones_f32[:], func=ACT.Sqrt)
             make_identity(nc, ident_bf[:])
             make_identity(nc, ident_f32[:])
+            mask_above = once.tile([P, C], BF16)
+            nc.gpsimd.memset(mask_above[:], 0.0)
+            nc.gpsimd.affine_select(
+                out=mask_above[:], in_=mask_above[:], pattern=[[-1, C]], compare_op=ALU.is_ge, fill=2.0, base=0, channel_multiplier=1
+            )
+            mask_below = once.tile([P, C], BF16)
+            nc.gpsimd.memset(mask_below[:], -2.0)
+            nc.gpsimd.affine_select(
+                out=mask_below[:], in_=mask_below[:], pattern=[[-1, C]], compare_op=ALU.is_gt, fill=0.0, base=0, channel_multiplier=1
+            )
 
-            shared_ps = psum_one.tile([P, HALF], F32, name="shared")
-            w0t_bank = shared_ps[:, 0 : HALF // 2].bitcast(BF16)
-            mean_ps = shared_ps[:, HALF // 2 : HALF].rearrange("p (j k) -> p j k", k=4)
-            stats = {}
+            stat_ps = psum_one.tile([P, CHUNKS, 4], F32)
             w0_ps = {}
 
-            def turn_w0(g, w0t_ps):
+            def turn_w0(g, pool=psum_one, tag="w0t"):
+                w0t_ps = pool.tile([P, PACK, P], BF16, tag=tag)
                 for t in range(PACK):
-                    nc.tensor.transpose(w0t_ps[:, P * t : P * (t + 1)], w0_raw[g // GROUP][:, g % GROUP, t, :], ident_bf[:])
+                    nc.tensor.transpose(w0t_ps[:, t, :], w0_raw[g // GROUP][:, g % GROUP, t, :], ident_bf[:])
                 w0_ps[g] = w0t_ps
 
             def copy_w0(g):
-                nc.scalar.copy(
-                    out=w0T[:, PACK * g : PACK * (g + 1), :], in_=w0_ps[g].rearrange("p (t m) -> p t m", t=PACK)
-                )
+                nc.scalar.copy(out=w0T[:, PACK * g : PACK * (g + 1), :], in_=w0_ps[g][:])
 
             groups = [[0], [1]] + [[g, g + 1] for g in range(2, PASSES, 2)]
-            group_of = {g: k for k, members in enumerate(groups) for g in members}
+            products = {}
+            deviations = {}
+
+            def columns(k):
+                return slice(PACK * groups[k][0], PACK * (groups[k][-1] + 1))
+
+            formed_of = {}
+
+            def apply_form(g):
+                formed = psum_one.tile([P, PACK, P], F32, tag="wide")
+                nc.tensor.matmul(
+                    out=formed[:].rearrange("p t m -> p (t m)"), lhsT=form[:],
+                    rhs=w0T[:, PACK * g : PACK * (g + 1), :].rearrange("p t m -> p (t m)"), start=True, stop=True,
+                )
+                formed_of[g] = formed
+
+            def close_form(g):
+                formed = formed_of[g]
+                product = stage.tile([P, PACK, P], F32, bufs=3)
+                nc.vector.scalar_tensor_tensor(
+                    out=product[:].rearrange("p t m -> p (t m)"), in0=formed[:].rearrange("p t m -> p (t m)"), scalar=column_scale[:],
+                    in1=w0T[:, PACK * g : PACK * (g + 1), :].rearrange("p t m -> p (t m)"), op0=ALU.mult, op1=ALU.mult,
+                )
+                products[g] = product
 
             def moments(g):
-                k = group_of[g]
-                i = groups[k].index(g)
-                if i == 0:
-                    var_g = stage.tile([P, PACK * GROUP], F32)
-                    stats[k] = [var_g]
-                wcov_ps = psum_two.tile([P, PACK, C], F32, tag="wcov")
                 for t in range(PACK):
-                    nc.tensor.matmul(out=wcov_ps[:, t, :], lhsT=w0T[:, PACK * g + t, :], rhs=cov[:], start=True, stop=True)
+                    j = PACK * g + t
+                    nc.tensor.matmul(out=stat_ps[:, j, :], lhsT=w0T[:, j, :], rhs=mu_pieces[:], start=True, stop=True)
                 for t in range(PACK):
-                    nc.tensor.matmul(
-                        out=mean_ps[:, PACK * g + t, :], lhsT=w0T_bf(PACK * g + t), rhs=mu_pieces[:], start=True, stop=True
-                    )
-                w0_ps[g] = wcov_ps
-
-            def variance(g, t):
-                k = group_of[g]
-                i = groups[k].index(g)
-                prod = stage.tile([P, C], F32)
-                nc.vector.scalar_tensor_tensor(
-                    out=prod[:], in0=w0_ps[g][:, t, :], scalar=1.0, in1=w0_raw[g // GROUP][:, g % GROUP, t, :],
-                    op0=ALU.mult, op1=ALU.mult, accum_out=stats[k][0][:, PACK * i + t : PACK * i + t + 1],
-                )
+                    j = PACK * g + t
+                    nc.tensor.matmul(out=stat_ps[:, j, 3:4], lhsT=products[g][:, t, :], rhs=ones_f32[:], start=True, stop=True)
 
             def deviation(k):
                 n = PACK * len(groups[k])
                 std_g = stage.tile([P, PACK * GROUP], F32)
-                nc.scalar.activation(out=std_g[:, 0:n], in_=stats[k][0][:, 0:n], func=ACT.Sqrt, bias=eps[:, 0:1])
-                stats[k].append(std_g)
+                nc.scalar.activation(
+                    out=std_g[:, 0:n], in_=stat_ps[:, columns(k), 3], func=ACT.Sqrt, bias=eps[:, 0:1], scale=1.0 / ROWS
+                )
+                deviations[k] = std_g
 
             def constants(k):
                 n = PACK * len(groups[k])
-                cols = slice(PACK * groups[k][0], PACK * groups[k][0] + n)
-                std_g = stats[k][1]
+                cols = columns(k)
+                std_g = deviations[k]
                 mean_g = stage.tile([P, PACK * GROUP], F32)
                 rstd_g = stage.tile([P, PACK * GROUP], F32)
                 mscale_g = stage.tile([P, PACK * GROUP], F32)
                 return [
-                    lambda: nc.vector.tensor_reduce(out=mean_g[:, 0:n], in_=mean_ps[:, cols, :], axis=AX.X, op=ALU.add),
+                    lambda: nc.vector.tensor_reduce(out=mean_g[:, 0:n], in_=stat_ps[:, cols, 0:3], axis=AX.X, op=ALU.add),
                     lambda: nc.vector.reciprocal(out=rstd_g[:, 0:n], in_=std_g[:, 0:n]),
                     lambda: nc.vector.tensor_tensor(out=scale0[:, cols], in0=gamma0_t[:, cols], in1=rstd_g[:, 0:n], op=ALU.mult),
                     lambda: nc.vector.tensor_tensor(out=mscale_g[:, 0:n], in0=mean_g[:, 0:n], in1=scale0[:, cols], op=ALU.mult),
                     lambda: nc.vector.tensor_tensor(out=shift0[:, cols], in0=beta0_t[:, cols], in1=mscale_g[:, 0:n], op=ALU.subtract),
                 ]
 
-            sum_ps = psum_two.tile([P, C], F32, tag="wcov")
+            sum_ps = psum_one.tile([P, C], F32, tag="y0_last")
             for m in range(POINTS):
                 nc.tensor.matmul(out=sum_ps[:], lhsT=ones_bf[:], rhs=x_sb[:, m, :], start=(m == 0), stop=(m == POINTS - 1))
             mu_rows = once.tile([P, C], F32)
             nc.vector.tensor_scalar(out=mu_rows[:], in0=sum_ps[:], scalar1=1.0 / ROWS, scalar2=None, op0=ALU.mult)
-            turn_w0(0, w0t_bank)
+            turn_w0(0)
             copy_w0(0)
-            w0t_other = psum_y0.tile([P, PACK * P], BF16, name="w0t_other", tag="y0")
-            turn_w0(1, w0t_other[:])
             col_ps = psum_y0.tile([P, 2], F32, tag="y0")
             for m in range(POINTS):
                 nc.tensor.matmul(out=col_ps[:], lhsT=x_sb[:, m, :], rhs=ones_bf[:, 0:2], start=(m == 0), stop=(m == POINTS - 1))
@@ -282,8 +291,7 @@ def tile_vfe_k_kernel(tc, voxel_feats, W0, gamma0, beta0, W1, gamma1, beta1, out
             for m in range(POINTS):
                 nc.tensor.transpose(xt_ps[:, m, :], x_sb[:, m, :], ident_bf[:])
             nc.scalar.copy(out=xT[:], in_=xt_ps[:].rearrange("p m n -> p (m n)"))
-            copy_w0(1)
-            cov_ps = psum_two.tile([P, C], F32, tag="wcov")
+            cov_ps = psum_one.tile([P, C], F32, tag="wide")
             for q in range(2):
                 xc = once.tile([P, POINTS // 2, C], F32, name="xc%d" % q)
                 nc.vector.tensor_tensor(
@@ -294,6 +302,11 @@ def tile_vfe_k_kernel(tc, voxel_feats, W0, gamma0, beta0, W1, gamma1, beta1, out
                     nc.tensor.matmul(
                         out=cov_ps[:], lhsT=xc[:, m, :], rhs=xc[:, m, :], start=(q == 0 and m == 0), stop=(q == 1 and m == 3)
                     )
+            minus_mu = once.tile([P, 1], F32)
+            nc.vector.tensor_scalar(out=minus_mu[:], in0=col_ps[:, 0:1], scalar1=-1.0 / ROWS, scalar2=None, op0=ALU.mult)
+            squares = once.tile([P, ROWS], BF16)
+            spread = once.tile([P, 1], F32)
+            nc.scalar.activation(out=squares[:], in_=xT[:], func=ACT.Square, bias=minus_mu[:, 0:1], accum_out=spread[:])
             rest0 = once.tile([P, 1], F32)
             rest1 = once.tile([P, 1], F32)
             rest2 = once.tile([P, 1], F32)
@@ -303,104 +316,147 @@ def tile_vfe_k_kernel(tc, voxel_feats, W0, gamma0, beta0, W1, gamma1, beta1, out
             nc.vector.tensor_copy(out=mu_pieces[:, 1:2], in_=rest1[:])
             nc.vector.tensor_tensor(out=rest2[:], in0=rest1[:], in1=mu_pieces[:, 1:2], op=ALU.subtract)
             nc.vector.tensor_copy(out=mu_pieces[:, 2:3], in_=rest2[:])
-            cov = once.tile([P, C], F32)
-            nc.vector.tensor_scalar(out=cov[:], in0=cov_ps[:], scalar1=1.0 / ROWS, scalar2=None, op0=ALU.mult)
 
+            diagonal = once.tile([P, 1], BF16)
+            over_diagonal = once.tile([P, 1], F32)
+            column_scale = once.tile([P, 1], F32)
+            high = once.tile([P, C], BF16)
+            lack = once.tile([P, C], BF16)
+            above = once.tile([P, C], BF16)
+            below = once.tile([P, C], BF16)
+            upper = once.tile([P, C], BF16)
+            on = once.tile([P, C], BF16)
+            form = once.tile([P, C], BF16)
+            nc.vector.tensor_scalar(out=diagonal[:], in0=spread[:], scalar1=TINY, scalar2=None, op0=ALU.max)
+            nc.vector.tensor_copy(out=high[:], in_=cov_ps[:])
+            nc.vector.reciprocal(out=over_diagonal[:], in_=diagonal[:])
+            nc.vector.tensor_tensor(out=above[:], in0=high[:], in1=mask_above[:], op=ALU.mult)
+            nc.vector.scalar_tensor_tensor(
+                out=column_scale[:], in0=spread[:], scalar=TINY, in1=over_diagonal[:], op0=ALU.max, op1=ALU.mult
+            )
+            nc.vector.tensor_scalar(out=on[:], in0=ident_bf[:], scalar1=diagonal[:, 0:1], scalar2=None, op0=ALU.mult)
+            nc.vector.scalar_tensor_tensor(
+                out=lack[:], in0=high[:], scalar=column_scale[:, 0:1], in1=cov_ps[:], op0=ALU.mult, op1=ALU.subtract
+            )
+            nc.vector.tensor_tensor(out=upper[:], in0=above[:], in1=on[:], op=ALU.add)
+            nc.vector.tensor_tensor(out=below[:], in0=lack[:], in1=mask_below[:], op=ALU.mult)
+            nc.vector.tensor_tensor(out=form[:], in0=upper[:], in1=below[:], op=ALU.add)
+
+            turn_w0(1)
+            copy_w0(1)
             turn_w1(0)
             copy_w1(0)
-            moments(0)
+            turn_w0(2)
+            copy_w0(2)
+            apply_form(0)
+            close_form(0)
             gb_words = gb_rows[:].bitcast(F32)
             gb_ps = psum_y0.tile([P, 3, P], F32, tag="y0")
             gb1_ps = gb_ps[:, 2, :].bitcast(BF16)[:, 0:P]
             for u in range(2):
                 nc.tensor.transpose(gb_ps[:, u, :], gb_words[:, u : 2 * P : 2], ident_f32[:])
             nc.tensor.transpose(gb1_ps, gb_rows[:, 0:P], ident_bf[:])
-            w0t_third = psum_one.tile([P, PACK * P], BF16, name="w0t_third", tag="y0_last")
-            turn_w0(2, w0t_third[:])
-            copy_w0(2)
-            turn_w1(1)
             gb_halves = gb_ps[:].rearrange("p u r -> p (u r)").bitcast(BF16).rearrange("p (u r e) -> p u r e", u=3, e=2)
-            for t in range(PACK):
-                variance(0, t)
-            deviation(0)
-            copy_w1(1)
             for u in range(2):
                 nc.vector.tensor_copy(
                     out=gb[:, 0 : 2 * CHUNKS].rearrange("p (r u e) -> p u r e", u=2, e=2)[:, u], in_=gb_halves[:, u, 0:32, :]
                 )
+            nc.vector.tensor_copy(out=gb[:, 128:132], in_=gb1_ps[:, 32:36])
+            turn_w0(3)
+            copy_w0(3)
+            moments(0)
+            deviation(0)
             for work in constants(0):
                 work()
-            nc.vector.tensor_copy(out=gb[:, 128:132], in_=gb1_ps[:, 32:36])
-            turn_w0(3, w0t_bank)
-            copy_w0(3)
-            moments(1)
+            for t in range(3):
+                multiply0(0, t)
+            apply_form(1)
+            close_form(1)
+            turn_w0(4)
+            turn_w1(1)
+            apply_form(2)
+            close_form(2)
             load_w1(4)
 
-            for s in range(PASSES):
+            normalise0(0, 0)
+            copy_w0(4)
+            normalise0(0, 1)
+            multiply0(0, 3, psum_one, "y0_last")
+            moments(1)
+            normalise0(0, 2)
+            deviation(1)
+            small = constants(1)
+            small[0]()
+            apply_form(3)
+            moments(2)
+            normalise0(0, 3)
+            copy_w1(1)
+            nc.vector.tensor_scalar(out=sgn1[:], in0=gamma1_t, scalar1=0.0, scalar2=2.0, op0=ALU.is_ge, op1=ALU.mult)
+            small[1]()
+            nc.vector.tensor_scalar(out=sgn1[:], in0=sgn1[:], scalar1=1.0, scalar2=None, op0=ALU.subtract)
+            small[2]()
+            nc.vector.tensor_tensor(out=gamma1_abs[:], in0=gamma1_t, in1=sgn1[:], op=ALU.mult)
+            small[3]()
+            small[4]()
+            for t in range(3):
+                multiply0(1, t)
+            normalise0(1, 0)
+            interleave0(0, nc.vector.tensor_copy, 0, VECTOR_ROWS)
+            close_form(3)
+            turn_w1(2)
+            turn_w0(5)
+            moments(3)
+            apply_form(4)
+            quantise_w1(0)
+            close_form(4)
+            normalise0(1, 1)
+            copy_w1(2)
+            copy_w0(5)
+            for s in range(1, PASSES):
                 w1_tile = s + 2
-                moments_of = [2, 3] if s == 0 else [s + 3] if s + 3 < PASSES else []
-                variances_of = [2] if s == 0 else [s + 3] if s + 3 < PASSES else []
-                ready = 1 if s == 0 else s // 2 + 2 if s % 2 == 1 and s + 1 < PASSES else None
-                if s == 0:
-                    for t in range(PACK):
-                        variance(1, t)
-                for t in range(3):
-                    multiply0(s, t)
+                ready = s // 2 + 2 if s % 2 == 1 and s + 1 < PASSES else None
+                if s > 1:
+                    for t in range(3):
+                        multiply0(s, t)
                 turn_w1(w1_tile)
-                if s >= 1:
+                if s + 5 < PASSES:
+                    turn_w0(s + 5)
+                if s > 1:
                     interleave0(s - 1, nc.vector.tensor_copy, 0, VECTOR_ROWS)
-                if s == 1:
-                    for t in range(PACK):
-                        variance(3, t)
-                for t in range(3):
+                    normalise0(s, 0)
+                interleave0(s - 1, nc.scalar.copy, VECTOR_ROWS, HALF)
+                if ready is not None:
+                    deviation(ready)
+                for t in range(1 if s > 1 else 2, 3):
                     normalise0(s, t)
-                    if t == 0 and s >= 1:
-                        interleave0(s - 1, nc.scalar.copy, VECTOR_ROWS, HALF)
-                    if t == (1 if s == 1 else 0) and ready is not None:
-                        deviation(ready)
                 small = constants(ready) if ready is not None else []
                 for work in small[0:1]:
                     work()
                 multiply0(s, 3, psum_one, "y0_last")
-                for g in moments_of:
-                    moments(g)
+                if s + 3 < PASSES:
+                    moments(s + 3)
                 copy_w1(w1_tile)
                 normalise0(s, 3)
 
+                for work in small[1:2]:
+                    work()
                 if s % 2 == 0:
                     quantise_w1(w1_tile // GROUP - 1)
                 elif s >= 3:
                     best_four(s // 2 - 1, peak_first[:, s - 3 : s - 1, :])
-                for work in small[1:2]:
-                    work()
-                if s == 0:
-                    nc.vector.tensor_scalar(out=sgn1[:], in0=gamma1_t, scalar1=0.0, scalar2=2.0, op0=ALU.is_ge, op1=ALU.mult)
-                else:
-                    quantise_first(s - 1)
                 for work in small[2:3]:
                     work()
-                if s == 0:
-                    nc.vector.tensor_scalar(out=sgn1[:], in0=sgn1[:], scalar1=1.0, scalar2=None, op0=ALU.subtract)
-                else:
-                    best_two(s - 1)
+                quantise_first(s - 1)
                 for work in small[3:4]:
                     work()
-                if s == 0:
-                    nc.vector.tensor_tensor(out=gamma1_abs[:], in0=gamma1_t, in1=sgn1[:], op=ALU.mult)
-                    for work in small[4:5]:
-                        work()
-                for g in variances_of:
-                    for t in range(PACK):
-                        variance(g, t)
-                        if s > 0 and t == 0:
-                            for work in small[4:5]:
-                                work()
-                if not variances_of:
-                    for work in small[4:5]:
-                        work()
+                best_two(s - 1)
+                for work in small[4:5]:
+                    work()
                 if s + 4 < PASSES:
-                    turn_w0(s + 4, w0t_bank)
-                    copy_w0(s + 4)
+                    apply_form(s + 4)
+                    close_form(s + 4)
+                if s + 5 < PASSES:
+                    copy_w0(s + 5)
                 if w1_tile % GROUP == 1:
                     load_w1(w1_tile // GROUP + 4)
 
@@ -465,7 +521,7 @@ def tile_vfe_k_kernel(tc, voxel_feats, W0, gamma0, beta0, W1, gamma1, beta1, out
             )
 
         def vector_rows(s):
-            return {2 * PASSES - 2: 320, 2 * PASSES - 1: 128}.get(s, VECTOR_ROWS)
+            return {2 * PASSES - 2: 320, 2 * PASSES - 1: 256}.get(s, VECTOR_ROWS)
 
         half_pairs = PASSES // GROUP
         last_pair = 2 * half_pairs - 1

@@ -27,7 +27,8 @@ PASSES = C0 // K_PASS
 CHUNKS = C0 // P
 HALF = ROWS // 2
 GROUP = 2
-VECTOR_ROWS = 448
+VECTOR_ROWS = 480
+EARLY = 2
 W1_TILES = 2 * PASSES
 
 FLOPS = 2 * ROWS * C * C0 + 2 * ROWS * C0 * C1 + 2 * VOXELS * C0 * C1
@@ -51,6 +52,8 @@ def tile_vfe_k_kernel(tc, voxel_feats, W0, gamma0, beta0, W1, gamma1, beta1, out
         gamma1_abs = keep.tile([P, 2], F32)
         eps = keep.tile([P, 1], F32)
         w0T = keep.tile([P, CHUNKS, P], BF16)
+        w0T_wide = keep.tile([P, EARLY * PACK, P], F32)
+        w0T_halves = w0T_wide[:].rearrange("p j m -> p (j m)").bitcast(BF16)
         scale0 = keep.tile([P, CHUNKS], F32)
         shift0 = keep.tile([P, CHUNKS], F32)
         w1_codes = keep.tile([P, 2, PASSES, C1], U32, align_bytes=64)
@@ -108,11 +111,16 @@ def tile_vfe_k_kernel(tc, voxel_feats, W0, gamma0, beta0, W1, gamma1, beta1, out
         grouped_of = {}
         best_of = {}
 
+        def weights0(j):
+            if j >= EARLY * PACK:
+                return w0T[:, j, :]
+            return w0T_halves[:, 2 * P * j + 1 : 2 * P * (j + 1) : 2]
+
         def multiply0(s, t, pool=psum_y0, tag="y0"):
             half, g = divmod(s, PASSES)
             y0_ps = pool.tile([P, HALF], F32, tag=tag)
             nc.tensor.matmul(
-                out=y0_ps[:], lhsT=w0T[:, PACK * g + t, :], rhs=xT[:, half * HALF : (half + 1) * HALF], start=True, stop=True
+                out=y0_ps[:], lhsT=weights0(PACK * g + t), rhs=xT[:, half * HALF : (half + 1) * HALF], start=True, stop=True
             )
             y0_tiles[s, t] = y0_ps
 
@@ -217,8 +225,9 @@ def tile_vfe_k_kernel(tc, voxel_feats, W0, gamma0, beta0, W1, gamma1, beta1, out
                     nc.tensor.transpose(w0t_ps[:, t, :], w0_raw[g // GROUP][:, g % GROUP, t, :], ident_bf[:])
                 w0_ps[g] = w0t_ps
 
-            def copy_w0(g):
-                nc.scalar.copy(out=w0T[:, PACK * g : PACK * (g + 1), :], in_=w0_ps[g][:])
+            def copy_w0(g, engine_copy=nc.scalar.copy):
+                into = w0T if g >= EARLY else w0T_wide
+                engine_copy(out=into[:, PACK * g : PACK * (g + 1), :], in_=w0_ps[g][:])
 
             groups = [[0], [1]] + [[g, g + 1] for g in range(2, PASSES, 2)]
             products = {}
@@ -249,17 +258,35 @@ def tile_vfe_k_kernel(tc, voxel_feats, W0, gamma0, beta0, W1, gamma1, beta1, out
             def moments(g):
                 for t in range(PACK):
                     j = PACK * g + t
-                    nc.tensor.matmul(out=stat_ps[:, j, :], lhsT=w0T[:, j, :], rhs=mu_pieces[:], start=True, stop=True)
+                    nc.tensor.matmul(out=stat_ps[:, j, :], lhsT=weights0(j), rhs=mu_pieces[:], start=True, stop=True)
                 for t in range(PACK):
                     j = PACK * g + t
-                    nc.tensor.matmul(out=stat_ps[:, j, 3:4], lhsT=products[g][:, t, :], rhs=ones_f32[:], start=True, stop=True)
+                    if g >= EARLY:
+                        nc.tensor.matmul(out=stat_ps[:, j, 3:4], lhsT=products[g][:, t, :], rhs=ones_f32[:], start=True, stop=True)
+
+            early_var = once.tile([P, EARLY * PACK], F32)
+            early_ps = {}
+
+            def multiply_early(g):
+                wide_ps = psum_one.tile([P, PACK, C], F32, tag="wide")
+                for t in range(PACK):
+                    nc.tensor.matmul(out=wide_ps[:, t, :], lhsT=w0T_wide[:, PACK * g + t, :], rhs=cov[:], start=True, stop=True)
+                early_ps[g] = wide_ps
+
+            def variance_early(g):
+                for t in range(PACK):
+                    j = PACK * g + t
+                    weighted = stage.tile([P, C], F32)
+                    nc.vector.scalar_tensor_tensor(
+                        out=weighted[:], in0=early_ps[g][:, t, :], scalar=1.0, in1=w0_raw[g // GROUP][:, g % GROUP, t, :],
+                        op0=ALU.mult, op1=ALU.mult, accum_out=early_var[:, j : j + 1],
+                    )
 
             def deviation(k):
                 n = PACK * len(groups[k])
                 std_g = stage.tile([P, PACK * GROUP], F32)
-                nc.scalar.activation(
-                    out=std_g[:, 0:n], in_=stat_ps[:, columns(k), 3], func=ACT.Sqrt, bias=eps[:, 0:1], scale=1.0 / ROWS
-                )
+                variances = stat_ps[:, columns(k), 3] if groups[k][0] >= EARLY else early_var[:, columns(k)]
+                nc.scalar.activation(out=std_g[:, 0:n], in_=variances, func=ACT.Sqrt, bias=eps[:, 0:1], scale=1.0 / ROWS)
                 deviations[k] = std_g
 
             def constants(k):
@@ -284,13 +311,15 @@ def tile_vfe_k_kernel(tc, voxel_feats, W0, gamma0, beta0, W1, gamma1, beta1, out
             nc.vector.tensor_scalar(out=mu_rows[:], in0=sum_ps[:], scalar1=1.0 / ROWS, scalar2=None, op0=ALU.mult)
             turn_w0(0)
             copy_w0(0)
+            turn_w0(1, psum_y0, "y0")
             col_ps = psum_y0.tile([P, 2], F32, tag="y0")
             for m in range(POINTS):
                 nc.tensor.matmul(out=col_ps[:], lhsT=x_sb[:, m, :], rhs=ones_bf[:, 0:2], start=(m == 0), stop=(m == POINTS - 1))
-            xt_ps = psum_y0.tile([P, POINTS, VOXELS], BF16, tag="y0")
+            xt_ps = psum_y0.tile([P, ROWS], BF16, tag="y0")
             for m in range(POINTS):
-                nc.tensor.transpose(xt_ps[:, m, :], x_sb[:, m, :], ident_bf[:])
-            nc.scalar.copy(out=xT[:], in_=xt_ps[:].rearrange("p m n -> p (m n)"))
+                nc.tensor.transpose(xt_ps[:, VOXELS * m : VOXELS * (m + 1)], x_sb[:, m, :], ident_bf[:])
+            nc.scalar.copy(out=xT[:], in_=xt_ps[:])
+            copy_w0(1)
             cov_ps = psum_one.tile([P, C], F32, tag="wide")
             for q in range(2):
                 xc = once.tile([P, POINTS // 2, C], F32, name="xc%d" % q)
@@ -316,6 +345,12 @@ def tile_vfe_k_kernel(tc, voxel_feats, W0, gamma0, beta0, W1, gamma1, beta1, out
             nc.vector.tensor_copy(out=mu_pieces[:, 1:2], in_=rest1[:])
             nc.vector.tensor_tensor(out=rest2[:], in0=rest1[:], in1=mu_pieces[:, 1:2], op=ALU.subtract)
             nc.vector.tensor_copy(out=mu_pieces[:, 2:3], in_=rest2[:])
+            cov = once.tile([P, C], F32)
+            nc.vector.tensor_copy(out=cov[:], in_=cov_ps[:])
+            turn_w1(0)
+            copy_w1(0)
+            multiply_early(0)
+            moments(0)
 
             diagonal = once.tile([P, 1], BF16)
             over_diagonal = once.tile([P, 1], F32)
@@ -327,85 +362,83 @@ def tile_vfe_k_kernel(tc, voxel_feats, W0, gamma0, beta0, W1, gamma1, beta1, out
             upper = once.tile([P, C], BF16)
             on = once.tile([P, C], BF16)
             form = once.tile([P, C], BF16)
+            nc.vector.tensor_copy(out=high[:], in_=cov[:])
             nc.vector.tensor_scalar(out=diagonal[:], in0=spread[:], scalar1=TINY, scalar2=None, op0=ALU.max)
-            nc.vector.tensor_copy(out=high[:], in_=cov_ps[:])
-            nc.vector.reciprocal(out=over_diagonal[:], in_=diagonal[:])
             nc.vector.tensor_tensor(out=above[:], in0=high[:], in1=mask_above[:], op=ALU.mult)
+            nc.vector.reciprocal(out=over_diagonal[:], in_=diagonal[:])
+            nc.vector.tensor_scalar(out=on[:], in0=ident_bf[:], scalar1=diagonal[:, 0:1], scalar2=None, op0=ALU.mult)
             nc.vector.scalar_tensor_tensor(
                 out=column_scale[:], in0=spread[:], scalar=TINY, in1=over_diagonal[:], op0=ALU.max, op1=ALU.mult
             )
-            nc.vector.tensor_scalar(out=on[:], in0=ident_bf[:], scalar1=diagonal[:, 0:1], scalar2=None, op0=ALU.mult)
-            nc.vector.scalar_tensor_tensor(
-                out=lack[:], in0=high[:], scalar=column_scale[:, 0:1], in1=cov_ps[:], op0=ALU.mult, op1=ALU.subtract
-            )
             nc.vector.tensor_tensor(out=upper[:], in0=above[:], in1=on[:], op=ALU.add)
-            nc.vector.tensor_tensor(out=below[:], in0=lack[:], in1=mask_below[:], op=ALU.mult)
-            nc.vector.tensor_tensor(out=form[:], in0=upper[:], in1=below[:], op=ALU.add)
 
-            turn_w0(1)
-            copy_w0(1)
-            turn_w1(0)
-            copy_w1(0)
-            turn_w0(2)
-            copy_w0(2)
-            apply_form(0)
-            close_form(0)
             gb_words = gb_rows[:].bitcast(F32)
             gb_ps = psum_y0.tile([P, 3, P], F32, tag="y0")
             gb1_ps = gb_ps[:, 2, :].bitcast(BF16)[:, 0:P]
             for u in range(2):
                 nc.tensor.transpose(gb_ps[:, u, :], gb_words[:, u : 2 * P : 2], ident_f32[:])
             nc.tensor.transpose(gb1_ps, gb_rows[:, 0:P], ident_bf[:])
+            turn_w0(2)
+            variance_early(0)
+            deviation(0)
             gb_halves = gb_ps[:].rearrange("p u r -> p (u r)").bitcast(BF16).rearrange("p (u r e) -> p u r e", u=3, e=2)
             for u in range(2):
                 nc.vector.tensor_copy(
                     out=gb[:, 0 : 2 * CHUNKS].rearrange("p (r u e) -> p u r e", u=2, e=2)[:, u], in_=gb_halves[:, u, 0:32, :]
                 )
             nc.vector.tensor_copy(out=gb[:, 128:132], in_=gb1_ps[:, 32:36])
-            turn_w0(3)
-            copy_w0(3)
-            moments(0)
-            deviation(0)
-            for work in constants(0):
-                work()
+            small = constants(0)
+            small[0]()
+            small[1]()
+            nc.vector.scalar_tensor_tensor(
+                out=lack[:], in0=high[:], scalar=column_scale[:, 0:1], in1=cov[:], op0=ALU.mult, op1=ALU.subtract
+            )
+            small[2]()
+            copy_w0(2, nc.vector.tensor_copy)
+            small[3]()
+            nc.vector.tensor_tensor(out=below[:], in0=lack[:], in1=mask_below[:], op=ALU.mult)
+            small[4]()
+            multiply_early(1)
             for t in range(3):
                 multiply0(0, t)
-            apply_form(1)
-            close_form(1)
-            turn_w0(4)
+            turn_w0(3)
+            moments(1)
             turn_w1(1)
-            apply_form(2)
-            close_form(2)
             load_w1(4)
 
+            nc.vector.tensor_tensor(out=form[:], in0=upper[:], in1=below[:], op=ALU.add)
+            variance_early(1)
+            copy_w0(3, nc.vector.tensor_copy)
             normalise0(0, 0)
-            copy_w0(4)
-            normalise0(0, 1)
             multiply0(0, 3, psum_one, "y0_last")
-            moments(1)
-            normalise0(0, 2)
+            normalise0(0, 1)
             deviation(1)
             small = constants(1)
             small[0]()
-            apply_form(3)
-            moments(2)
+            apply_form(2)
+            normalise0(0, 2)
             normalise0(0, 3)
             copy_w1(1)
+            turn_w0(4)
             nc.vector.tensor_scalar(out=sgn1[:], in0=gamma1_t, scalar1=0.0, scalar2=2.0, op0=ALU.is_ge, op1=ALU.mult)
             small[1]()
             nc.vector.tensor_scalar(out=sgn1[:], in0=sgn1[:], scalar1=1.0, scalar2=None, op0=ALU.subtract)
             small[2]()
             nc.vector.tensor_tensor(out=gamma1_abs[:], in0=gamma1_t, in1=sgn1[:], op=ALU.mult)
             small[3]()
+            close_form(2)
             small[4]()
+            apply_form(3)
             for t in range(3):
                 multiply0(1, t)
-            normalise0(1, 0)
-            interleave0(0, nc.vector.tensor_copy, 0, VECTOR_ROWS)
             close_form(3)
+            copy_w0(4, nc.vector.tensor_copy)
+            moments(2)
             turn_w1(2)
             turn_w0(5)
             moments(3)
+            normalise0(1, 0)
+            interleave0(0, nc.vector.tensor_copy, 0, HALF)
             apply_form(4)
             quantise_w1(0)
             close_form(4)
@@ -422,9 +455,8 @@ def tile_vfe_k_kernel(tc, voxel_feats, W0, gamma0, beta0, W1, gamma1, beta1, out
                 if s + 5 < PASSES:
                     turn_w0(s + 5)
                 if s > 1:
-                    interleave0(s - 1, nc.vector.tensor_copy, 0, VECTOR_ROWS)
+                    interleave0(s - 1, nc.vector.tensor_copy, 0, HALF)
                     normalise0(s, 0)
-                interleave0(s - 1, nc.scalar.copy, VECTOR_ROWS, HALF)
                 if ready is not None:
                     deviation(ready)
                 for t in range(1 if s > 1 else 2, 3):
@@ -521,7 +553,7 @@ def tile_vfe_k_kernel(tc, voxel_feats, W0, gamma0, beta0, W1, gamma1, beta1, out
             )
 
         def vector_rows(s):
-            return {2 * PASSES - 2: 320, 2 * PASSES - 1: 256}.get(s, VECTOR_ROWS)
+            return {PASSES - 1: HALF, 2 * PASSES - 2: 320, 2 * PASSES - 1: 256}.get(s, VECTOR_ROWS)
 
         half_pairs = PASSES // GROUP
         last_pair = 2 * half_pairs - 1
@@ -535,7 +567,8 @@ def tile_vfe_k_kernel(tc, voxel_feats, W0, gamma0, beta0, W1, gamma1, beta1, out
                 turn_w1(w1_tile)
             multiply0(s, 3)
             normalise0(s, 0)
-            interleave0(s - 1, nc.scalar.copy, vector_rows(s - 1), HALF)
+            if vector_rows(s - 1) < HALF:
+                interleave0(s - 1, nc.scalar.copy, vector_rows(s - 1), HALF)
             for t in range(1, 3):
                 normalise0(s, t)
             if w1_tile < W1_TILES:

@@ -27,7 +27,8 @@ PASSES = C0 // K_PASS
 CHUNKS = C0 // P
 HALF = ROWS // 2
 GROUP = 2
-VECTOR_ROWS = 480
+FIRST_ROWS = 480
+VECTOR_ROWS = 464
 EARLY = 2
 W1_TILES = 2 * PASSES
 
@@ -406,20 +407,30 @@ def tile_vfe_k_kernel(tc, voxel_feats, W0, gamma0, beta0, W1, gamma1, beta1, out
             turn_w1(1)
             load_w1(4)
 
+            def start(s, t):
+                if t == PACK - 1:
+                    multiply0(s, t, psum_one, "y0_last")
+                else:
+                    multiply0(s, t)
+
             nc.vector.tensor_tensor(out=form[:], in0=upper[:], in1=below[:], op=ALU.add)
             variance_early(1)
             copy_w0(3, nc.vector.tensor_copy)
+            start(0, 3)
             normalise0(0, 0)
-            multiply0(0, 3, psum_one, "y0_last")
+            start(1, 0)
             normalise0(0, 1)
             deviation(1)
             small = constants(1)
             small[0]()
             apply_form(2)
+            start(1, 1)
             normalise0(0, 2)
-            normalise0(0, 3)
-            copy_w1(1)
             turn_w0(4)
+            start(1, 2)
+            normalise0(0, 3)
+            start(1, 3)
+            copy_w1(1)
             nc.vector.tensor_scalar(out=sgn1[:], in0=gamma1_t, scalar1=0.0, scalar2=2.0, op0=ALU.is_ge, op1=ALU.mult)
             small[1]()
             nc.vector.tensor_scalar(out=sgn1[:], in0=sgn1[:], scalar1=1.0, scalar2=None, op0=ALU.subtract)
@@ -429,52 +440,83 @@ def tile_vfe_k_kernel(tc, voxel_feats, W0, gamma0, beta0, W1, gamma1, beta1, out
             close_form(2)
             small[4]()
             apply_form(3)
-            for t in range(3):
-                multiply0(1, t)
-            close_form(3)
-            copy_w0(4, nc.vector.tensor_copy)
             moments(2)
             turn_w1(2)
-            turn_w0(5)
-            moments(3)
-            normalise0(1, 0)
             interleave0(0, nc.vector.tensor_copy, 0, HALF)
+            close_form(3)
+            copy_w0(4, nc.vector.tensor_copy)
+            moments(3)
+
+            normalise0(1, 0)
+            start(2, 0)
+            normalise0(1, 1)
+            start(2, 1)
             apply_form(4)
             quantise_w1(0)
+            normalise0(1, 2)
+            start(2, 2)
+            turn_w0(5)
+            normalise0(1, 3)
+            start(2, 3)
+            deviation(2)
+            small = constants(2)
+            small[0]()
+            quantise_first(0)
+            small[1]()
             close_form(4)
-            normalise0(1, 1)
+            small[2]()
             copy_w1(2)
-            copy_w0(5)
-            for s in range(1, PASSES):
+            best_two(0)
+            small[3]()
+            copy_w0(5, nc.vector.tensor_copy)
+            small[4]()
+            turn_w1(3)
+            moments(4)
+            apply_form(5)
+            turn_w0(6)
+            copy_w1(3)
+            close_form(5)
+            load_w1(5)
+
+            for s in range(2, PASSES):
                 w1_tile = s + 2
                 ready = s // 2 + 2 if s % 2 == 1 and s + 1 < PASSES else None
-                if s > 1:
-                    for t in range(3):
-                        multiply0(s, t)
                 turn_w1(w1_tile)
-                if s + 5 < PASSES:
-                    turn_w0(s + 5)
-                if s > 1:
-                    interleave0(s - 1, nc.vector.tensor_copy, 0, HALF)
-                    normalise0(s, 0)
+                interleave0(s - 1, nc.vector.tensor_copy, 0, FIRST_ROWS)
+                normalise0(s, 0)
+                if s == 2:
+                    copy_w0(6)
+                if FIRST_ROWS < HALF:
+                    interleave0(s - 1, nc.scalar.copy, FIRST_ROWS, HALF)
                 if ready is not None:
                     deviation(ready)
-                for t in range(1 if s > 1 else 2, 3):
-                    normalise0(s, t)
                 small = constants(ready) if ready is not None else []
                 for work in small[0:1]:
                     work()
-                multiply0(s, 3, psum_one, "y0_last")
+                if s + 1 < PASSES:
+                    start(s + 1, 0)
+                if s + 5 < PASSES:
+                    turn_w0(s + 5)
+                normalise0(s, 1)
+                if s + 1 < PASSES:
+                    start(s + 1, 1)
+                if s + 4 < PASSES:
+                    apply_form(s + 4)
+                normalise0(s, 2)
+                if s + 1 < PASSES:
+                    start(s + 1, 2)
                 if s + 3 < PASSES:
                     moments(s + 3)
                 copy_w1(w1_tile)
                 normalise0(s, 3)
+                if s + 1 < PASSES:
+                    start(s + 1, 3)
 
                 for work in small[1:2]:
                     work()
                 if s % 2 == 0:
                     quantise_w1(w1_tile // GROUP - 1)
-                elif s >= 3:
+                else:
                     best_four(s // 2 - 1, peak_first[:, s - 3 : s - 1, :])
                 for work in small[2:3]:
                     work()
@@ -485,7 +527,6 @@ def tile_vfe_k_kernel(tc, voxel_feats, W0, gamma0, beta0, W1, gamma1, beta1, out
                 for work in small[4:5]:
                     work()
                 if s + 4 < PASSES:
-                    apply_form(s + 4)
                     close_form(s + 4)
                 if s + 5 < PASSES:
                     copy_w0(s + 5)
@@ -553,7 +594,7 @@ def tile_vfe_k_kernel(tc, voxel_feats, W0, gamma0, beta0, W1, gamma1, beta1, out
             )
 
         def vector_rows(s):
-            return {PASSES - 1: HALF, 2 * PASSES - 2: 320, 2 * PASSES - 1: 256}.get(s, VECTOR_ROWS)
+            return {PASSES - 1: FIRST_ROWS, 2 * PASSES - 2: 320, 2 * PASSES - 1: 256}.get(s, VECTOR_ROWS)
 
         half_pairs = PASSES // GROUP
         last_pair = 2 * half_pairs - 1

from contextlib import ExitStack

import concourse.mybir as mybir
from concourse.masks import make_identity

BF16 = mybir.dt.bfloat16
F32 = mybir.dt.float32
U32 = mybir.dt.uint32
U8 = mybir.dt.uint8
FP8X4 = mybir.dt.float8_e4m3fn_x4
ALU = mybir.AluOpType
ACT = mybir.ActivationFunctionType
AX = mybir.AxisListType

P = 128
VOXELS = 128
POINTS = 8
ROWS = VOXELS * POINTS
C = 128
C0 = 8192
C1 = 256
EPS = 1e-3
TINY = 1e-30
PACK = 4
K_PASS = P * PACK
PASSES = C0 // K_PASS
CHUNKS = C0 // P
HALF = ROWS // 2
GROUP = 2
FIRST_ROWS = 480
VECTOR_ROWS = 464
EARLY = 2
W1_TILES = 2 * PASSES

FLOPS = 2 * ROWS * C * C0 + 2 * ROWS * C0 * C1 + 2 * VOXELS * C0 * C1


def tile_vfe_k_kernel(tc, voxel_feats, W0, gamma0, beta0, W1, gamma1, beta1, out):
    nc = tc.nc
    with ExitStack() as ctx:
        keep = ctx.enter_context(tc.tile_pool(name="keep", bufs=1))
        flow = ctx.enter_context(tc.tile_pool(name="flow", bufs=3))
        loads = ctx.enter_context(tc.tile_pool(name="loads", bufs=4))
        psum_y0 = ctx.enter_context(tc.psum_pool(name="psum_y0", bufs=3))
        psum_w1 = ctx.enter_context(tc.psum_pool(name="psum_w1", bufs=1))
        ctx.enter_context(tc.manual_schedule())

        xT = keep.tile([P, ROWS], BF16)
        ident_bf = keep.tile([P, P], BF16)
        ident_f32 = keep.tile([P, P], F32)
        gb = keep.tile([P, 132], F32)
        sgn1 = keep.tile([P, 2], F32)
        gamma1_abs = keep.tile([P, 2], F32)
        eps = keep.tile([P, 1], F32)
        w0T = keep.tile([P, CHUNKS, P], BF16)
        w0T_wide = keep.tile([P, EARLY * PACK, P], F32)
        w0T_halves = w0T_wide[:].rearrange("p j m -> p (j m)").bitcast(BF16)
        scale0 = keep.tile([P, CHUNKS], F32)
        shift0 = keep.tile([P, CHUNKS], F32)
        w1_codes = keep.tile([P, 2, PASSES, C1], U32, align_bytes=64)
        w1_scales = keep.tile([P, 2, PASSES, C1], U8, align_bytes=64)
        p_codes_first = keep.tile([P, PASSES, HALF], U32, align_bytes=64)
        p_scales_first = keep.tile([P, PASSES, HALF], U8, align_bytes=64)
        peak_first = keep.tile([P, PASSES, PACK * VOXELS], BF16)
        a_codes = keep.tile([P, PASSES, VOXELS], U32, align_bytes=64)
        a_scales = keep.tile([P, PASSES, VOXELS], U8, align_bytes=64)
        gamma0_t = gb[:, 0:CHUNKS]
        beta0_t = gb[:, CHUNKS : 2 * CHUNKS]
        gamma1_t = gb[:, 128:130]
        beta1_t = gb[:, 130:132]

        w1_view = W1.rearrange("(h n) k -> n h k", h=2)
        w1_raw = {}
        w1_grouped = {}

        def load_w1(q):
            raw = loads.tile([P, 2, GROUP * K_PASS], BF16)
            nc.sync.dma_start(out=raw[:], in_=w1_view[:, :, q * GROUP * K_PASS : (q + 1) * GROUP * K_PASS])
            w1_raw[q] = raw

        w1_ps = {}

        def turn_w1(i):
            q, r = divmod(i, GROUP)
            words = w1_raw[q][:].bitcast(F32)
            w1t_ps = psum_w1.tile([P, 2, 2, P], F32, tag="w1t")
            for h in range(2):
                for u in range(2):
                    nc.tensor.transpose(w1t_ps[:, h, u, :], words[:, h, 256 * r + u : 256 * (r + 1) : 2], ident_f32[:])
            w1_ps[i] = w1t_ps

        def copy_w1(i):
            q, r = divmod(i, GROUP)
            if r == 0:
                grouped = flow.tile([P, GROUP, PACK * C1], BF16, name="w1_g", align_bytes=64)
                w1_grouped[q] = grouped
            nc.scalar.copy(
                out=w1_grouped[q][:, r, :].bitcast(F32).rearrange("p (h n u) -> p h n u", h=2, u=2),
                in_=w1_ps[i][:].rearrange("p h u n -> p h n u"),
            )

        def quantise_w1(q):
            part, g = divmod(GROUP * q, PASSES)
            nc.vector.quantize_mx(
                out=w1_codes[:, part, g : g + GROUP, :].rearrange("p g n -> p (g n)").bitcast(FP8X4),
                scales=w1_scales[:, part, g : g + GROUP, :].rearrange("p g n -> p (g n)"),
                in_=w1_grouped[q][:].rearrange("p i w -> p (i w)"),
            )

        y0_tiles = {}
        planes_of = {}
        grouped_of = {}
        best_of = {}

        def weights0(j):
            if j >= EARLY * PACK:
                return w0T[:, j, :]
            return w0T_halves[:, 2 * P * j + 1 : 2 * P * (j + 1) : 2]

        def multiply0(s, t, pool=psum_y0, tag="y0"):
            half, g = divmod(s, PASSES)
            y0_ps = pool.tile([P, HALF], F32, tag=tag)
            nc.tensor.matmul(
                out=y0_ps[:], lhsT=weights0(PACK * g + t), rhs=xT[:, half * HALF : (half + 1) * HALF], start=True, stop=True
            )
            y0_tiles[s, t] = y0_ps

        def normalise0(s, t):
            j = PACK * (s % PASSES) + t
            if t == 0:
                planes = flow.tile([P, PACK, HALF], BF16)
                planes_of[s] = planes
            nc.scalar.activation(
                out=planes_of[s][:, t, :], in_=y0_tiles[s, t][:], func=ACT.Relu, bias=shift0[:, j : j + 1], scale=scale0[:, j : j + 1]
            )

        def interleave0(s, engine_copy, lo, hi):
            if s not in grouped_of:
                grouped = flow.tile([P, PACK * HALF], BF16, align_bytes=64)
                grouped_of[s] = grouped
            engine_copy(
                out=grouped_of[s][:, PACK * lo : PACK * hi].rearrange("p (c i t) -> p c t i", i=4, t=PACK),
                in_=planes_of[s][:, :, lo:hi].rearrange("p t (c i) -> p c t i", i=4),
            )

        def best_two(s):
            k, i = divmod(s, GROUP)
            if i == 0:
                best2 = flow.tile([P, GROUP, 2 * PACK * VOXELS], BF16, bufs=2)
                best_of[k] = best2
            nc.vector.tensor_tensor(
                out=best_of[k][:, i, :], in0=grouped_of[s][:, 0:1024], in1=grouped_of[s][:, 1024:2048], op=ALU.max
            )

        def best_four(k, out):
            nc.vector.tensor_tensor(out=out, in0=best_of[k][:, :, 0:512], in1=best_of[k][:, :, 512:1024], op=ALU.max)

        def quantise_first(g):
            nc.vector.quantize_mx(
                out=p_codes_first[:, g, :].bitcast(FP8X4), scales=p_scales_first[:, g, :], in_=grouped_of[g][:]
            )

        with ExitStack() as first:
            once = first.enter_context(tc.tile_pool(name="once", bufs=1))
            stage = first.enter_context(tc.tile_pool(name="stage", bufs=2))
            psum_one = first.enter_context(tc.psum_pool(name="psum_one", bufs=1))

            x_sb = once.tile([P, POINTS, C], BF16)
            nc.sync.dma_start(out=x_sb[:], in_=voxel_feats)
            w0_view = W0.rearrange("(g p t) c -> p g (t c)", p=P, t=PACK)
            w0_raw = []

            def load_w0(q):
                raw = once.tile([P, GROUP, PACK, C], BF16, name="w0_raw%d" % q)
                w0_raw.append(raw)
                nc.sync.dma_start(
                    out=raw[:].rearrange("p g t c -> p g (t c)"), in_=w0_view[:, GROUP * q : GROUP * (q + 1), :]
                )

            ones_bf = once.tile([P, P], BF16)
            nc.vector.memset(ones_bf[:], 1.0)
            gb_rows = once.tile([P, K_PASS], BF16)
            nc.vector.memset(gb_rows[:], 0.0)
            load_w0(0)
            load_w0(1)
            load_w1(0)
            nc.sync.dma_start(out=gb_rows[0:16, :], in_=gamma0.rearrange("(r w) -> r w", w=K_PASS))
            nc.sync.dma_start(out=gb_rows[16:32, :], in_=beta0.rearrange("(r w) -> r w", w=K_PASS))
            nc.sync.dma_start(out=gb_rows[32:34, 0:P], in_=gamma1.rearrange("(r w) -> r w", w=P))
            nc.sync.dma_start(out=gb_rows[34:36, 0:P], in_=beta1.rearrange("(r w) -> r w", w=P))
            load_w1(1)
            load_w0(2)
            load_w1(2)
            for q in range(3, 6):
                load_w0(q)
            load_w1(3)
            load_w0(6)
            load_w0(7)

            ones_f32 = once.tile([P, 1], F32)
            nc.vector.memset(ones_f32[:], 1.0)
            mu_pieces = once.tile([P, 4], BF16)
            nc.vector.memset(mu_pieces[:], 0.0)
            nc.vector.tensor_scalar(out=eps[:], in0=ones_f32[:], scalar1=EPS, scalar2=None, op0=ALU.mult)
            warm = once.tile([P, 1], F32)
            nc.scalar.activation(out=warm[:], in_=ones_f32[:], func=ACT.Sqrt)
            make_identity(nc, ident_bf[:])
            make_identity(nc, ident_f32[:])
            mask_above = once.tile([P, C], BF16)
            nc.gpsimd.memset(mask_above[:], 0.0)
            nc.gpsimd.affine_select(
                out=mask_above[:], in_=mask_above[:], pattern=[[-1, C]], compare_op=ALU.is_ge, fill=2.0, base=0, channel_multiplier=1
            )
            mask_below = once.tile([P, C], BF16)
            nc.gpsimd.memset(mask_below[:], -2.0)
            nc.gpsimd.affine_select(
                out=mask_below[:], in_=mask_below[:], pattern=[[-1, C]], compare_op=ALU.is_gt, fill=0.0, base=0, channel_multiplier=1
            )

            stat_ps = psum_one.tile([P, CHUNKS, 4], F32)
            w0_ps = {}

            def turn_w0(g, pool=psum_one, tag="w0t"):
                w0t_ps = pool.tile([P, PACK, P], BF16, tag=tag)
                for t in range(PACK):
                    nc.tensor.transpose(w0t_ps[:, t, :], w0_raw[g // GROUP][:, g % GROUP, t, :], ident_bf[:])
                w0_ps[g] = w0t_ps

            def copy_w0(g, engine_copy=nc.scalar.copy):
                into = w0T if g >= EARLY else w0T_wide
                engine_copy(out=into[:, PACK * g : PACK * (g + 1), :], in_=w0_ps[g][:])

            groups = [[0], [1]] + [[g, g + 1] for g in range(2, PASSES, 2)]
            products = {}
            deviations = {}

            def columns(k):
                return slice(PACK * groups[k][0], PACK * (groups[k][-1] + 1))

            formed_of = {}

            def apply_form(g):
                formed = psum_one.tile([P, PACK, P], F32, tag="wide")
                nc.tensor.matmul(
                    out=formed[:].rearrange("p t m -> p (t m)"), lhsT=form[:],
                    rhs=w0T[:, PACK * g : PACK * (g + 1), :].rearrange("p t m -> p (t m)"), start=True, stop=True,
                )
                formed_of[g] = formed

            def close_form(g):
                formed = formed_of[g]
                product = stage.tile([P, PACK, P], F32, bufs=3)
                nc.vector.scalar_tensor_tensor(
                    out=product[:].rearrange("p t m -> p (t m)"), in0=formed[:].rearrange("p t m -> p (t m)"), scalar=column_scale[:],
                    in1=w0T[:, PACK * g : PACK * (g + 1), :].rearrange("p t m -> p (t m)"), op0=ALU.mult, op1=ALU.mult,
                )
                products[g] = product

            def moments(g):
                for t in range(PACK):
                    j = PACK * g + t
                    nc.tensor.matmul(out=stat_ps[:, j, :], lhsT=weights0(j), rhs=mu_pieces[:], start=True, stop=True)
                for t in range(PACK):
                    j = PACK * g + t
                    if g >= EARLY:
                        nc.tensor.matmul(out=stat_ps[:, j, 3:4], lhsT=products[g][:, t, :], rhs=ones_f32[:], start=True, stop=True)

            early_var = once.tile([P, EARLY * PACK], F32)
            early_ps = {}

            def multiply_early(g):
                wide_ps = psum_one.tile([P, PACK, C], F32, tag="wide")
                for t in range(PACK):
                    nc.tensor.matmul(out=wide_ps[:, t, :], lhsT=w0T_wide[:, PACK * g + t, :], rhs=cov[:], start=True, stop=True)
                early_ps[g] = wide_ps

            def variance_early(g):
                for t in range(PACK):
                    j = PACK * g + t
                    weighted = stage.tile([P, C], F32)
                    nc.vector.scalar_tensor_tensor(
                        out=weighted[:], in0=early_ps[g][:, t, :], scalar=1.0, in1=w0_raw[g // GROUP][:, g % GROUP, t, :],
                        op0=ALU.mult, op1=ALU.mult, accum_out=early_var[:, j : j + 1],
                    )

            def deviation(k):
                n = PACK * len(groups[k])
                std_g = stage.tile([P, PACK * GROUP], F32)
                variances = stat_ps[:, columns(k), 3] if groups[k][0] >= EARLY else early_var[:, columns(k)]
                nc.scalar.activation(out=std_g[:, 0:n], in_=variances, func=ACT.Sqrt, bias=eps[:, 0:1], scale=1.0 / ROWS)
                deviations[k] = std_g

            def constants(k):
                n = PACK * len(groups[k])
                cols = columns(k)
                std_g = deviations[k]
                mean_g = stage.tile([P, PACK * GROUP], F32)
                rstd_g = stage.tile([P, PACK * GROUP], F32)
                mscale_g = stage.tile([P, PACK * GROUP], F32)
                return [
                    lambda: nc.vector.tensor_reduce(out=mean_g[:, 0:n], in_=stat_ps[:, cols, 0:3], axis=AX.X, op=ALU.add),
                    lambda: nc.vector.reciprocal(out=rstd_g[:, 0:n], in_=std_g[:, 0:n]),
                    lambda: nc.vector.tensor_tensor(out=scale0[:, cols], in0=gamma0_t[:, cols], in1=rstd_g[:, 0:n], op=ALU.mult),
                    lambda: nc.vector.tensor_tensor(out=mscale_g[:, 0:n], in0=mean_g[:, 0:n], in1=scale0[:, cols], op=ALU.mult),
                    lambda: nc.vector.tensor_tensor(out=shift0[:, cols], in0=beta0_t[:, cols], in1=mscale_g[:, 0:n], op=ALU.subtract),
                ]

            sum_ps = psum_one.tile([P, C], F32, tag="y0_last")
            for m in range(POINTS):
                nc.tensor.matmul(out=sum_ps[:], lhsT=ones_bf[:], rhs=x_sb[:, m, :], start=(m == 0), stop=(m == POINTS - 1))
            mu_rows = once.tile([P, C], F32)
            nc.vector.tensor_scalar(out=mu_rows[:], in0=sum_ps[:], scalar1=1.0 / ROWS, scalar2=None, op0=ALU.mult)
            turn_w0(0)
            copy_w0(0)
            turn_w0(1, psum_y0, "y0")
            col_ps = psum_y0.tile([P, 2], F32, tag="y0")
            for m in range(POINTS):
                nc.tensor.matmul(out=col_ps[:], lhsT=x_sb[:, m, :], rhs=ones_bf[:, 0:2], start=(m == 0), stop=(m == POINTS - 1))
            xt_ps = psum_y0.tile([P, ROWS], BF16, tag="y0")
            for m in range(POINTS):
                nc.tensor.transpose(xt_ps[:, VOXELS * m : VOXELS * (m + 1)], x_sb[:, m, :], ident_bf[:])
            nc.scalar.copy(out=xT[:], in_=xt_ps[:])
            copy_w0(1)
            cov_ps = psum_one.tile([P, C], F32, tag="wide")
            for q in range(2):
                xc = once.tile([P, POINTS // 2, C], F32, name="xc%d" % q)
                nc.vector.tensor_tensor(
                    out=xc[:], in0=x_sb[:, 4 * q : 4 * (q + 1), :],
                    in1=mu_rows[:].unsqueeze(1).to_broadcast([P, POINTS // 2, C]), op=ALU.subtract,
                )
                for m in range(POINTS // 2):
                    nc.tensor.matmul(
                        out=cov_ps[:], lhsT=xc[:, m, :], rhs=xc[:, m, :], start=(q == 0 and m == 0), stop=(q == 1 and m == 3)
                    )
            minus_mu = once.tile([P, 1], F32)
            nc.vector.tensor_scalar(out=minus_mu[:], in0=col_ps[:, 0:1], scalar1=-1.0 / ROWS, scalar2=None, op0=ALU.mult)
            squares = once.tile([P, ROWS], BF16)
            spread = once.tile([P, 1], F32)
            nc.scalar.activation(out=squares[:], in_=xT[:], func=ACT.Square, bias=minus_mu[:, 0:1], accum_out=spread[:])
            rest0 = once.tile([P, 1], F32)
            rest1 = once.tile([P, 1], F32)
            rest2 = once.tile([P, 1], F32)
            nc.vector.tensor_scalar(out=rest0[:], in0=col_ps[:, 0:1], scalar1=1.0 / ROWS, scalar2=None, op0=ALU.mult)
            nc.vector.tensor_copy(out=mu_pieces[:, 0:1], in_=rest0[:])
            nc.vector.tensor_tensor(out=rest1[:], in0=rest0[:], in1=mu_pieces[:, 0:1], op=ALU.subtract)
            nc.vector.tensor_copy(out=mu_pieces[:, 1:2], in_=rest1[:])
            nc.vector.tensor_tensor(out=rest2[:], in0=rest1[:], in1=mu_pieces[:, 1:2], op=ALU.subtract)
            nc.vector.tensor_copy(out=mu_pieces[:, 2:3], in_=rest2[:])
            cov = once.tile([P, C], F32)
            nc.vector.tensor_copy(out=cov[:], in_=cov_ps[:])
            turn_w1(0)
            copy_w1(0)
            multiply_early(0)
            moments(0)

            diagonal = once.tile([P, 1], BF16)
            over_diagonal = once.tile([P, 1], F32)
            column_scale = once.tile([P, 1], F32)
            high = once.tile([P, C], BF16)
            lack = once.tile([P, C], BF16)
            above = once.tile([P, C], BF16)
            below = once.tile([P, C], BF16)
            upper = once.tile([P, C], BF16)
            on = once.tile([P, C], BF16)
            form = once.tile([P, C], BF16)
            nc.vector.tensor_copy(out=high[:], in_=cov[:])
            nc.vector.tensor_scalar(out=diagonal[:], in0=spread[:], scalar1=TINY, scalar2=None, op0=ALU.max)
            nc.vector.tensor_tensor(out=above[:], in0=high[:], in1=mask_above[:], op=ALU.mult)
            nc.vector.reciprocal(out=over_diagonal[:], in_=diagonal[:])
            nc.vector.tensor_scalar(out=on[:], in0=ident_bf[:], scalar1=diagonal[:, 0:1], scalar2=None, op0=ALU.mult)
            nc.vector.scalar_tensor_tensor(
                out=column_scale[:], in0=spread[:], scalar=TINY, in1=over_diagonal[:], op0=ALU.max, op1=ALU.mult
            )
            nc.vector.tensor_tensor(out=upper[:], in0=above[:], in1=on[:], op=ALU.add)

            gb_words = gb_rows[:].bitcast(F32)
            gb_ps = psum_y0.tile([P, 3, P], F32, tag="y0")
            gb1_ps = gb_ps[:, 2, :].bitcast(BF16)[:, 0:P]
            for u in range(2):
                nc.tensor.transpose(gb_ps[:, u, :], gb_words[:, u : 2 * P : 2], ident_f32[:])
            nc.tensor.transpose(gb1_ps, gb_rows[:, 0:P], ident_bf[:])
            turn_w0(2)
            variance_early(0)
            deviation(0)
            gb_halves = gb_ps[:].rearrange("p u r -> p (u r)").bitcast(BF16).rearrange("p (u r e) -> p u r e", u=3, e=2)
            for u in range(2):
                nc.vector.tensor_copy(
                    out=gb[:, 0 : 2 * CHUNKS].rearrange("p (r u e) -> p u r e", u=2, e=2)[:, u], in_=gb_halves[:, u, 0:32, :]
                )
            nc.vector.tensor_copy(out=gb[:, 128:132], in_=gb1_ps[:, 32:36])
            small = constants(0)
            small[0]()
            small[1]()
            nc.vector.scalar_tensor_tensor(
                out=lack[:], in0=high[:], scalar=column_scale[:, 0:1], in1=cov[:], op0=ALU.mult, op1=ALU.subtract
            )
            small[2]()
            copy_w0(2, nc.vector.tensor_copy)
            small[3]()
            nc.vector.tensor_tensor(out=below[:], in0=lack[:], in1=mask_below[:], op=ALU.mult)
            small[4]()
            multiply_early(1)
            for t in range(3):
                multiply0(0, t)
            turn_w0(3)
            moments(1)
            turn_w1(1)
            load_w1(4)

            def start(s, t):
                if t == PACK - 1:
                    multiply0(s, t, psum_one, "y0_last")
                else:
                    multiply0(s, t)

            nc.vector.tensor_tensor(out=form[:], in0=upper[:], in1=below[:], op=ALU.add)
            variance_early(1)
            copy_w0(3, nc.vector.tensor_copy)
            start(0, 3)
            normalise0(0, 0)
            start(1, 0)
            normalise0(0, 1)
            deviation(1)
            small = constants(1)
            small[0]()
            apply_form(2)
            start(1, 1)
            normalise0(0, 2)
            turn_w0(4)
            start(1, 2)
            normalise0(0, 3)
            start(1, 3)
            copy_w1(1)
            nc.vector.tensor_scalar(out=sgn1[:], in0=gamma1_t, scalar1=0.0, scalar2=2.0, op0=ALU.is_ge, op1=ALU.mult)
            small[1]()
            nc.vector.tensor_scalar(out=sgn1[:], in0=sgn1[:], scalar1=1.0, scalar2=None, op0=ALU.subtract)
            small[2]()
            nc.vector.tensor_tensor(out=gamma1_abs[:], in0=gamma1_t, in1=sgn1[:], op=ALU.mult)
            small[3]()
            close_form(2)
            small[4]()
            apply_form(3)
            moments(2)
            turn_w1(2)
            interleave0(0, nc.vector.tensor_copy, 0, HALF)
            close_form(3)
            copy_w0(4, nc.vector.tensor_copy)
            moments(3)

            normalise0(1, 0)
            start(2, 0)
            normalise0(1, 1)
            start(2, 1)
            apply_form(4)
            quantise_w1(0)
            normalise0(1, 2)
            start(2, 2)
            turn_w0(5)
            normalise0(1, 3)
            start(2, 3)
            deviation(2)
            small = constants(2)
            small[0]()
            quantise_first(0)
            small[1]()
            close_form(4)
            small[2]()
            copy_w1(2)
            best_two(0)
            small[3]()
            copy_w0(5, nc.vector.tensor_copy)
            small[4]()
            turn_w1(3)
            moments(4)
            apply_form(5)
            turn_w0(6)
            copy_w1(3)
            close_form(5)
            load_w1(5)

            for s in range(2, PASSES):
                w1_tile = s + 2
                ready = s // 2 + 2 if s % 2 == 1 and s + 1 < PASSES else None
                turn_w1(w1_tile)
                interleave0(s - 1, nc.vector.tensor_copy, 0, FIRST_ROWS)
                normalise0(s, 0)
                if s == 2:
                    copy_w0(6)
                if FIRST_ROWS < HALF:
                    interleave0(s - 1, nc.scalar.copy, FIRST_ROWS, HALF)
                if ready is not None:
                    deviation(ready)
                small = constants(ready) if ready is not None else []
                for work in small[0:1]:
                    work()
                if s + 1 < PASSES:
                    start(s + 1, 0)
                if s + 5 < PASSES:
                    turn_w0(s + 5)
                normalise0(s, 1)
                if s + 1 < PASSES:
                    start(s + 1, 1)
                if s + 4 < PASSES:
                    apply_form(s + 4)
                normalise0(s, 2)
                if s + 1 < PASSES:
                    start(s + 1, 2)
                if s + 3 < PASSES:
                    moments(s + 3)
                copy_w1(w1_tile)
                normalise0(s, 3)
                if s + 1 < PASSES:
                    start(s + 1, 3)

                for work in small[1:2]:
                    work()
                if s % 2 == 0:
                    quantise_w1(w1_tile // GROUP - 1)
                else:
                    best_four(s // 2 - 1, peak_first[:, s - 3 : s - 1, :])
                for work in small[2:3]:
                    work()
                quantise_first(s - 1)
                for work in small[3:4]:
                    work()
                best_two(s - 1)
                for work in small[4:5]:
                    work()
                if s + 4 < PASSES:
                    close_form(s + 4)
                if s + 5 < PASSES:
                    copy_w0(s + 5)
                if w1_tile % GROUP == 1:
                    load_w1(w1_tile // GROUP + 4)

        last = ctx.enter_context(tc.tile_pool(name="last", bufs=1))
        late = ctx.enter_context(tc.tile_pool(name="late", bufs=3))
        psum_acc = ctx.enter_context(tc.psum_pool(name="psum_acc", bufs=1))
        acc = [[psum_acc.tile([P, HALF], F32, name="acc%d%d" % (h, half)) for half in range(2)] for h in range(2)]

        def layer1(g, half, codes, scales):
            for h in range(2):
                nc.tensor.matmul_mx(
                    out=acc[h][half][:],
                    lhsT=w1_codes[:, 0, g, h * P : (h + 1) * P].bitcast(FP8X4),
                    lhsT_scale=w1_scales[:, 0, g, h * P : (h + 1) * P],
                    rhs=codes.bitcast(FP8X4),
                    rhs_scale=scales,
                    start=(g == 0),
                    stop=(g == PASSES - 1),
                )

        def layer1_peak(h, ya_ps, passes):
            for g in passes:
                nc.tensor.matmul_mx(
                    out=ya_ps[:],
                    lhsT=w1_codes[:, 1, g, h * P : (h + 1) * P].bitcast(FP8X4),
                    lhsT_scale=w1_scales[:, 1, g, h * P : (h + 1) * P],
                    rhs=a_codes[:, g, :].bitcast(FP8X4),
                    rhs_scale=a_scales[:, g, :],
                    start=(g == 0),
                    stop=(g == PASSES - 1),
                )

        p_codes_of = {}
        p_scales_of = {}
        peak_of = {}
        a_grouped = {}

        def quantise_p(g):
            p_codes = late.tile([P, HALF], U32, align_bytes=64)
            p_scales = late.tile([P, HALF], U8, align_bytes=64)
            p_codes_of[g] = p_codes
            p_scales_of[g] = p_scales
            nc.vector.quantize_mx(out=p_codes[:].bitcast(FP8X4), scales=p_scales[:], in_=grouped_of[PASSES + g][:])

        def peak_four(k):
            peak = late.tile([P, GROUP, PACK * VOXELS], BF16, bufs=2)
            peak_of[k] = peak
            best_four(k, peak[:])

        def peak_all(k):
            g = GROUP * k - PASSES
            a_pair = late.tile([P, GROUP, PACK * VOXELS], BF16, bufs=2, align_bytes=64)
            a_grouped[k] = a_pair
            nc.vector.tensor_tensor(out=a_pair[:], in0=peak_of[k][:], in1=peak_first[:, g : g + GROUP, :], op=ALU.max)

        def quantise_a(k):
            g = GROUP * k - PASSES
            nc.vector.quantize_mx(
                out=a_codes[:, g : g + GROUP, :].rearrange("p g n -> p (g n)").bitcast(FP8X4),
                scales=a_scales[:, g : g + GROUP, :].rearrange("p g n -> p (g n)"),
                in_=a_grouped[k][:].rearrange("p i w -> p (i w)"),
            )

        def vector_rows(s):
            return {PASSES - 1: FIRST_ROWS, 2 * PASSES - 2: 320, 2 * PASSES - 1: 256}.get(s, VECTOR_ROWS)

        half_pairs = PASSES // GROUP
        last_pair = 2 * half_pairs - 1
        ya_tiles = {}
        for s in range(PASSES, 2 * PASSES):
            g = s - PASSES
            w1_tile = s + 2
            for t in range(3):
                multiply0(s, t)
            if w1_tile < W1_TILES:
                turn_w1(w1_tile)
            multiply0(s, 3)
            normalise0(s, 0)
            if vector_rows(s - 1) < HALF:
                interleave0(s - 1, nc.scalar.copy, vector_rows(s - 1), HALF)
            for t in range(1, 3):
                normalise0(s, t)
            if w1_tile < W1_TILES:
                copy_w1(w1_tile)
            normalise0(s, 3)
            layer1(g, 0, p_codes_first[:, g, :], p_scales_first[:, g, :])
            if g >= 2:
                layer1(g - 2, 1, p_codes_of[g - 2][:], p_scales_of[g - 2][:])
            if w1_tile == W1_TILES:
                ya_ps = psum_w1.tile([P, VOXELS], F32, tag="w1t")
                ya_tiles[0] = ya_ps
                layer1_peak(0, ya_ps, range(PASSES - 8))

            interleave0(s - 1, nc.vector.tensor_copy, 0, vector_rows(s - 1))
            k = s // 2 - 1
            if s % 2 == 0:
                if k > half_pairs:
                    peak_all(k - 1)
                if w1_tile <= W1_TILES:
                    quantise_w1(w1_tile // GROUP - 1)
            elif k < half_pairs:
                best_four(k, peak_first[:, GROUP * k : GROUP * (k + 1), :])
            else:
                peak_four(k)
            if g == 0:
                quantise_first(s - 1)
            else:
                quantise_p(g - 1)
            if s % 2 == 1 and k > half_pairs:
                quantise_a(k - 1)
            best_two(s - 1)
            if w1_tile % GROUP == 1 and w1_tile // GROUP + 4 < W1_TILES // GROUP:
                load_w1(w1_tile // GROUP + 4)

        signed = last.tile([P, 2, 2, HALF], F32)
        peak1 = last.tile([P, 2, VOXELS], F32)
        half4 = last.tile([P, 2, 256], F32)
        ya = last.tile([P, 2, VOXELS], F32)
        y1_late = last.tile([P, 2, HALF], F32)
        end = PASSES - 1
        interleave0(2 * PASSES - 1, nc.scalar.copy, vector_rows(2 * PASSES - 1), HALF)
        for h in range(2):
            nc.scalar.activation(out=signed[:, h, 0, :], in_=acc[h][0][:], func=ACT.Copy, scale=sgn1[:, h : h + 1])
        layer1(end - 1, 1, p_codes_of[end - 1][:], p_scales_of[end - 1][:])
        interleave0(2 * PASSES - 1, nc.vector.tensor_copy, 0, vector_rows(2 * PASSES - 1))
        peak_all(last_pair - 1)
        quantise_p(end)
        best_two(2 * PASSES - 1)
        quantise_a(last_pair - 1)
        peak_four(last_pair)
        nc.vector.tensor_tensor(out=half4[:], in0=signed[:, :, 0, 0:256], in1=signed[:, :, 0, 256:512], op=ALU.max)
        peak_all(last_pair)
        nc.vector.tensor_tensor(out=peak1[:], in0=half4[:, :, 0:128], in1=half4[:, :, 128:256], op=ALU.max)
        quantise_a(last_pair)
        ya_ps1 = psum_y0.tile([P, VOXELS], F32, tag="y0")
        ya_tiles[1] = ya_ps1
        layer1_peak(0, ya_tiles[0], range(PASSES - 8, PASSES - 4))
        layer1_peak(1, ya_ps1, range(PASSES - 4))
        layer1(end, 1, p_codes_of[end][:], p_scales_of[end][:])
        for h in range(2):
            nc.scalar.activation(out=signed[:, h, 1, :], in_=acc[h][1][:], func=ACT.Copy, scale=sgn1[:, h : h + 1])
        for h in range(2):
            layer1_peak(h, ya_tiles[h], range(PASSES - 4, PASSES - 2))
        for h in range(2):
            layer1_peak(h, ya_tiles[h], range(PASSES - 2, PASSES))
        best = last.tile([P, 2, VOXELS], F32)
        nc.vector.tensor_tensor(out=half4[:], in0=signed[:, :, 1, 0:256], in1=signed[:, :, 1, 256:512], op=ALU.max)
        nc.vector.tensor_tensor(out=best[:], in0=half4[:, :, 0:128], in1=half4[:, :, 128:256], op=ALU.max)

        stats1 = last.tile([P, 2, 2, 6], F32)
        mv1 = last.tile([P, 2, 2], F32)
        for h in range(2):
            nc.scalar.activation(out=ya[:, h, :], in_=ya_tiles[h][:], func=ACT.Copy, scale=sgn1[:, h : h + 1])

        def add_peak(h, half):
            points = "p (m n) -> p m n"
            shared = ya[:, h, :].unsqueeze(1).to_broadcast([P, POINTS // 2, VOXELS])
            if half == 0:
                first4 = signed[:, h, 0, :].rearrange(points, n=VOXELS)
                nc.gpsimd.tensor_tensor(out=first4, in0=first4, in1=shared, op=ALU.add)
            else:
                nc.vector.scalar_tensor_tensor(
                    out=y1_late[:, h, :].rearrange(points, n=VOXELS), in0=acc[h][1][:].rearrange(points, n=VOXELS), scalar=sgn1[:, h : h + 1], in1=shared,
                    op0=ALU.mult, op1=ALU.add,
                )

        def statistics1(h, half):
            nc.vector.bn_stats(out=stats1[:, h, half, :], in_=signed[:, h, 0, :] if half == 0 else y1_late[:, h, :])

        std1 = last.tile([P, 2], F32)
        rstd1 = last.tile([P, 2], F32)
        z1 = last.tile([P, 2, VOXELS], F32)
        out_sb = last.tile([P, 2, P], F32)

        def aggregate(h):
            nc.vector.bn_aggr(out=mv1[:, h, :], in_=stats1[:, h, :, :].rearrange("p q s -> p (q s)"))
            nc.scalar.activation(out=std1[:, h : h + 1], in_=mv1[:, h, 1:2], func=ACT.Sqrt, bias=eps[:, 0:1])

        def centre(h):
            nc.vector.tensor_scalar(
                out=best[:, h, :], in0=best[:, h, :], scalar1=mv1[:, h, 0:1], scalar2=gamma1_abs[:, h : h + 1],
                op0=ALU.subtract, op1=ALU.mult,
            )

        def finish(h):
            nc.vector.reciprocal(out=rstd1[:, h : h + 1], in_=std1[:, h : h + 1])
            nc.scalar.activation(
                out=z1[:, h, :], in_=best[:, h, :], func=ACT.Relu, bias=beta1_t[:, h : h + 1], scale=rstd1[:, h : h + 1]
            )

        def store(h):
            out_ps = psum_y0.tile([P, P], F32, tag="y0")
            nc.tensor.transpose(out_ps[:], z1[:, h, :], ident_f32[:])
            nc.vector.tensor_copy(out=out_sb[:, h, :], in_=out_ps[:])
            nc.sync.dma_start(out=out[:, h * P : (h + 1) * P], in_=out_sb[:, h, :])

        add_peak(0, 0)
        add_peak(1, 0)
        add_peak(0, 1)
        add_peak(1, 1)
        statistics1(0, 1)
        nc.vector.tensor_tensor(out=best[:], in0=best[:], in1=peak1[:], op=ALU.max)
        statistics1(0, 0)
        nc.vector.tensor_tensor(out=best[:], in0=best[:], in1=ya[:], op=ALU.add)
        aggregate(0)
        statistics1(1, 1)
        centre(0)
        statistics1(1, 0)
        finish(0)
        aggregate(1)
        centre(1)
        finish(1)
        store(0)
        store(1)
